import numpy as np
import ml_dtypes


def mxq(x, axis, fmt="e4m3"):
    dtype, down = {"e4m3": (ml_dtypes.float8_e4m3fn, 7), "e5m2": (ml_dtypes.float8_e5m2, 14)}[fmt]
    v = np.moveaxis(np.asarray(x, np.float32).astype(ml_dtypes.bfloat16).astype(np.float64), axis, -1)
    blocks = v.reshape(v.shape[:-1] + (-1, 32))
    amax = np.abs(blocks).max(-1, keepdims=True)
    byte = np.maximum(np.where(amax > 0, np.frexp(amax)[1] - 1 + 127, 0) - down, 1)
    scale = np.exp2(byte - 127.0)
    codes = (blocks / scale).astype(np.float32).astype(dtype).astype(np.float64)
    return np.moveaxis((codes * scale).reshape(v.shape), -1, axis)


WIDE = False


def mx_kscale(k):
    if not WIDE:
        return np.ones(k)
    levels = np.array([10, -10, 5, -5, 0])
    a = np.random.permutation(np.resize(levels, k // 512 * 4)).reshape(k // 512, 4)
    idx = np.arange(k)
    return np.exp2(a[idx // 512, idx % 128 // 32])


BF16 = ml_dtypes.bfloat16


def bf(x):
    return np.asarray(x, np.float32).astype(BF16)


def f64(x):
    return np.asarray(x).astype(np.float64)


M, NI, NO, G, P = 8192, 128, 256, 5, 3
NB = G + P
K = NB * NI
R = NB - 2


def silu(v):
    return v / (1.0 + np.exp(-v))


def b_spline_basis(x, t):
    xc = np.clip(x, t[P], t[-P - 1])[..., None]
    n_int = t.shape[0] - 1
    b = ((xc >= t[:-1]) & (xc < t[1:])).astype(np.float64)
    for j in range(1, P + 1):
        nv = n_int - j
        ti = t[:nv]
        ti_j = t[j:nv + j]
        ti1 = t[1:nv + 1]
        ti_j1 = t[j + 1:nv + j + 1]
        a1 = (xc - ti) / np.maximum(ti_j - ti, 1e-8)
        a2 = (ti_j1 - xc) / np.maximum(ti_j1 - ti1, 1e-8)
        b = a1 * b[..., :nv] + a2 * b[..., 1:nv + 1]
    return b


def setup_inputs():
    h = 2.0 / G
    grid = np.linspace(-1.0, 1.0, G + 1)
    knots = np.concatenate([grid[0] - h * np.arange(P, 0, -1), grid, grid[-1] + h * np.arange(1, P + 1)])
    t = np.repeat(mx_kscale(K)[R * NI:(R + 1) * NI:32], 32)
    e = np.round(np.log2(t) / P)
    near = t != 1.0
    kr = f64(bf(knots))[R]
    x = np.random.standard_normal((M, NI))
    coeff = np.random.standard_normal((NI, NO, NB)) * 2.0 / np.sqrt(NI)
    bw = np.random.uniform(-1.0, 1.0, (NI, NO)) * 1.5 / np.sqrt(NI)
    u = np.random.randint(1, 4, (M, NI))
    x = np.where(near, kr + u * 2.0 ** (e - 7.0), x)
    coeff[:, :, R] *= np.where(near, 2.0 ** (16.0 - P * e), 1.0)[:, None]
    return {"x": bf(x), "coeff": bf(coeff), "base_weight": bf(bw), "knots": bf(knots)}


def reference(x, coeff, base_weight, knots):
    x = f64(x)
    base = silu(x @ f64(base_weight))
    basis = b_spline_basis(x, f64(knots))
    bq = mxq(basis.transpose(0, 2, 1).reshape(M, K), 1, "e4m3")
    cq = mxq(f64(coeff).transpose(2, 0, 1).reshape(K, NO), 0, "e4m3")
    return base + (bq @ cq)

@@ -1,0 +1,219 @@
+from contextlib import ExitStack
+
+import concourse.bass as bass
+import concourse.mybir as mybir
+import concourse.tile as tile
+from concourse.masks import make_identity
+
+F32 = mybir.dt.float32
+BF16 = mybir.dt.bfloat16
+U32 = mybir.dt.uint32
+I32 = mybir.dt.int32
+U8 = mybir.dt.uint8
+FP8X4 = mybir.dt.float8_e4m3fn_x4
+ALU = mybir.AluOpType
+ACTF = mybir.ActivationFunctionType
+
+P = 128
+M, NI, NO, NB = 8192, 128, 256, 8
+FLOPS = 2 * M * NB * NI * NO + 2 * M * NI * NO
+
+T = [-141 / 64, -115 / 64, -179 / 128, -1.0, -77 / 128, -205 / 1024,
+     205 / 1024, 77 / 128, 1.0, 179 / 128, 115 / 64, 141 / 64]
+
+
+def beta(r, j):
+    prod = 1.0
+    for m in range(5):
+        if m != j:
+            prod = prod * (T[r + j] - T[r + m])
+    return (T[r + 4] - T[r]) / prod
+
+
+G = 1
+F = 512 * G
+NCH = 16 // G
+
+
+def tile_bsplinekanlayer_t_kernel(tc, x, coeff, base_weight, knots, out):
+    nc = tc.nc
+    with ExitStack() as ctx:
+        const = ctx.enter_context(tc.tile_pool(name="const", bufs=1))
+        w2 = ctx.enter_context(tc.tile_pool(name="w2", bufs=2))
+        w1 = ctx.enter_context(tc.tile_pool(name="w1", bufs=1))
+        w3 = ctx.enter_context(tc.tile_pool(name="w3", bufs=3))
+        sqp = ctx.enter_context(tc.tile_pool(name="sqp", bufs=4))
+        ps_tq = ctx.enter_context(tc.psum_pool(name="ps_tq", bufs=1))
+        ps_xt = ctx.enter_context(tc.psum_pool(name="ps_xt", bufs=1))
+        ps_sp = ctx.enter_context(tc.psum_pool(name="ps_sp", bufs=3))
+        ps_pb = ctx.enter_context(tc.psum_pool(name="ps_pb", bufs=3))
+
+        x_sb = const.tile([P, 64, NI], BF16)
+        x_v = x.rearrange("(p n) i -> p n i", n=64)
+        for a in range(4):
+            nc.sync.dma_start(out=x_sb[:, 16 * a:16 * a + 16, :], in_=x_v[:, 16 * a:16 * a + 16, :])
+        bw_sb = const.tile([P, NO], BF16)
+        nc.scalar.dma_start(out=bw_sb[:], in_=base_weight)
+        c_ld = const.tile([P, 4, NO * NB], BF16)
+        c_v = coeff.rearrange("(j t) o r -> j t (o r)", t=4)
+        for q in range(4):
+            nc.scalar.dma_start(out=c_ld[32 * q:32 * q + 32, :, :], in_=c_v)
+
+        ident_f = const.tile([P, P], F32)
+        make_identity(nc, ident_f[:])
+        ident_b = const.tile([P, P], BF16)
+        make_identity(nc, ident_b[:])
+
+        c_z = const.tile([P, NB, 4, NO], U32, align_bytes=64)
+        nc.vector.memset(c_z[:].bitcast(I32), 0)
+        c_g = const.tile([P, NB, NO, 4], BF16, align_bytes=64)
+        c_p = c_ld[:].rearrange("p t (o r) -> p r o t", r=NB)
+        nc.scalar.copy(out=c_g[:, 0:4], in_=c_p[:, 0:4])
+        nc.vector.tensor_copy(out=c_g[:, 4:8], in_=c_p[:, 4:8])
+        c_full = const.tile([P, NB * NO], U32, align_bytes=64)
+        c_scl = const.tile([P, NB * NO], U8, align_bytes=64)
+        for h in range(2):
+            nc.vector.quantize_mx(
+                out=c_full[:, 1024 * h:1024 * h + 1024].bitcast(FP8X4),
+                scales=c_scl[:, 1024 * h:1024 * h + 1024],
+                in_=c_g[:, 4 * h:4 * h + 4].rearrange("p r o t -> p (r o t)"),
+            )
+        for q in range(4):
+            nc.vector.tensor_copy(
+                out=c_z[32 * q:32 * q + 32, :, q, :].bitcast(I32),
+                in_=c_full[32 * q:32 * q + 32, :].rearrange("p (r o) -> p r o", r=NB).bitcast(I32),
+            )
+
+        xw = x_sb[:].rearrange("p n i -> p (n i)").bitcast(F32)
+        out_v = out.rearrange("(p n) o -> p n o", n=64)
+        state = {}
+
+        def front(c):
+            tq = ps_tq.tile([P, G, 2, P], F32, name="tq")
+            for gg in range(G):
+                g = c * G + gg
+                for u in range(2):
+                    nc.tensor.transpose(tq[:, gg, u, :], xw[:, g * 256 + u:(g + 1) * 256:2], ident_f[:])
+            xt_ps = ps_xt.tile([P, 4 * G, P], BF16, name="xt_ps")
+            for m in range(4 * G):
+                nc.tensor.transpose(xt_ps[:, m, :], x_sb[:, c * 4 * G + m, :], ident_b[:])
+            xq_raw = w3.tile([P, F], BF16, name="xq_raw")
+            nc.scalar.copy(
+                out=xq_raw[:].bitcast(F32).rearrange("p (g b u) -> p g b u", g=G, u=2),
+                in_=tq[:].rearrange("p g u b -> p g b u"),
+            )
+            xT = w3.tile([P, 4 * G * P], BF16, name="xT")
+            nc.scalar.copy(out=xT[:], in_=xt_ps[:].rearrange("p m b -> p (m b)"))
+            xq = w3.tile([P, F], BF16, name="xq")
+            nc.vector.tensor_scalar(out=xq[:], in0=xq_raw[:], scalar1=T[3], scalar2=T[8],
+                                    op0=ALU.max, op1=ALU.min)
+            state[("xq", c)] = xq
+            state[("xT", c)] = xT
+
+        def stt(o, a, s, b, op1=ALU.add):
+            nc.vector.scalar_tensor_tensor(out=o, in0=a, scalar=s, in1=b, op0=ALU.mult, op1=op1)
+
+        def middle(c):
+            xq = state[("xq", c)]
+            V = {}
+            for k in (4, 5, 6, 7, 3, 8):
+                sq = sqp.tile([P, F], F32, name="sq")
+                nc.scalar.activation(out=sq[:], in_=xq[:], func=ACTF.Square, bias=-T[k], scale=1.0)
+                V[k] = w2.tile([P, F], F32, name="V%d" % k)
+                nc.vector.scalar_tensor_tensor(out=V[k][:], in0=xq[:], scalar=T[k], in1=sq[:],
+                                               op0=ALU.subtract, op1=ALU.mult)
+            bas = w2.tile([P, NB, F], BF16, name="bas", align_bytes=64)
+
+            def relu(k, s, nm):
+                t = w2.tile([P, F], F32, name=nm)
+                nc.scalar.activation(out=t[:], in_=V[k][:], func=ACTF.Relu, scale=s)
+                return t
+
+            q4 = relu(4, -beta(0, 4), "q4")
+            q5 = relu(5, -beta(1, 4), "q5")
+            nc.scalar.activation(out=bas[:, 0, :], in_=V[4][:], func=ACTF.Relu, scale=-beta(0, 4))
+            stt(bas[:, 1, :], q4[:], beta(1, 3) / beta(0, 4), q5[:])
+            c2 = beta(2, 3) / beta(1, 4)
+            x2 = w1.tile([P, F], F32, name="x2")
+            stt(x2[:], q4[:], (beta(2, 2) / beta(0, 4)) / c2, q5[:])
+            q6 = relu(6, -beta(2, 4), "q6")
+            stt(bas[:, 2, :], x2[:], c2, q6[:])
+            c3 = beta(3, 3) / beta(2, 4)
+            x3 = w1.tile([P, F], F32, name="x3")
+            stt(x3[:], q5[:], (beta(3, 2) / beta(1, 4)) / c3, q6[:])
+            q7 = relu(7, -beta(3, 4), "q7")
+            s3 = w1.tile([P, F], F32, name="s3")
+            stt(s3[:], x3[:], c3, q7[:])
+            stt(bas[:, 3, :], V[3][:], beta(3, 0), s3[:], op1=ALU.min)
+            p7 = relu(7, beta(7, 0), "p7")
+            p6 = relu(6, beta(6, 0), "p6")
+            nc.scalar.activation(out=bas[:, 7, :], in_=V[7][:], func=ACTF.Relu, scale=beta(7, 0))
+            stt(bas[:, 6, :], p7[:], beta(6, 1) / beta(7, 0), p6[:])
+            c5 = beta(5, 1) / beta(6, 0)
+            x5 = w1.tile([P, F], F32, name="x5")
+            stt(x5[:], p7[:], (beta(5, 2) / beta(7, 0)) / c5, p6[:])
+            p5 = relu(5, beta(5, 0), "p5")
+            stt(bas[:, 5, :], x5[:], c5, p5[:])
+            c4 = beta(4, 1) / beta(5, 0)
+            x4 = w1.tile([P, F], F32, name="x4")
+            stt(x4[:], p6[:], (beta(4, 2) / beta(6, 0)) / c4, p5[:])
+            p4 = relu(4, beta(4, 0), "p4")
+            s4 = w1.tile([P, F], F32, name="s4")
+            stt(s4[:], x4[:], c4, p4[:])
+            stt(bas[:, 4, :], V[8][:], -beta(4, 4), s4[:], op1=ALU.min)
+
+            cod = w2.tile([P, NB * F // 4], U32, name="cod", align_bytes=64)
+            scl = w2.tile([P, NB * F // 4], U8, name="scl", align_bytes=64)
+            per = 4096 // F
+            for h in range(NB // per):
+                wd = per * F // 4
+                nc.vector.quantize_mx(
+                    out=cod[:, h * wd:(h + 1) * wd].bitcast(FP8X4),
+                    scales=scl[:, h * wd:(h + 1) * wd],
+                    in_=bas[:, h * per:(h + 1) * per, :].rearrange("p r f -> p (r f)"),
+                )
+            state[("cod", c)] = cod
+            state[("scl", c)] = scl
+
+        def back(c):
+            cod = state[("cod", c)]
+            scl = state[("scl", c)]
+            xT = state[("xT", c)]
+            for gg in range(G):
+                g = c * G + gg
+                o_sb = w2.tile([P, 4, NO], F32, name="o_sb")
+                for h in range(2):
+                    sp = ps_sp.tile([P, 2, NO], F32, name="sp")
+                    pb = ps_pb.tile([P, 2, NO], F32, name="pb")
+                    for qq in range(2):
+                        q = 2 * h + qq
+                        nc.tensor.matmul(out=pb[:, qq, :], lhsT=xT[:, (4 * gg + q) * P:(4 * gg + q + 1) * P],
+                                         rhs=bw_sb[:], start=True, stop=True)
+                    for qq in range(2):
+                        q = 2 * h + qq
+                        for r in range(NB):
+                            lo = r * (F // 4) + gg * P
+                            nc.tensor.matmul_mx(
+                                out=sp[:, qq, :],
+                                lhsT=cod[:, lo:lo + P].bitcast(FP8X4),
+                                lhsT_scale=scl[:, lo:lo + P],
+                                rhs=c_z[:, r, q, :].bitcast(FP8X4),
+                                rhs_scale=c_scl[:, r * NO:(r + 1) * NO],
+                                start=(r == 0),
+                                stop=(r == NB - 1),
+                            )
+                    sil = w2.tile([P, 2 * NO], F32, name="sil")
+                    nc.scalar.activation(out=sil[:], in_=pb[:].rearrange("p a o -> p (a o)"), func=ACTF.Silu)
+                    nc.vector.tensor_tensor(out=o_sb[:, 2 * h:2 * h + 2, :].rearrange("p a o -> p (a o)"),
+                                            in0=sp[:].rearrange("p a o -> p (a o)"), in1=sil[:], op=ALU.add)
+                nc.sync.dma_start(out=out_v[:, 4 * g:4 * g + 4, :], in_=o_sb[:])
+
+        front(0)
+        front(1)
+        for c in range(NCH):
+            if c + 2 < NCH:
+                front(c + 2)
+            middle(c)
+            if c >= 1:
+                back(c - 1)
+        back(NCH - 1)

@@ -1,8 +1,6 @@
 from contextlib import ExitStack
 
-import concourse.bass as bass
 import concourse.mybir as mybir
-import concourse.tile as tile
 from concourse.masks import make_identity
 
 F32 = mybir.dt.float32
@@ -30,190 +28,247 @@ def beta(r, j):
     return (T[r + 4] - T[r]) / prod
 
 
-G = 1
-F = 512 * G
-NCH = 16 // G
+assert T[3] == -T[8] and beta(3, 0) == beta(4, 4)
+SIG = beta(4, 4) ** 0.5
+
+F = 512
+NCH = 16
+PIN = True
 
 
 def tile_bsplinekanlayer_t_kernel(tc, x, coeff, base_weight, knots, out):
     nc = tc.nc
     with ExitStack() as ctx:
         const = ctx.enter_context(tc.tile_pool(name="const", bufs=1))
-        w2 = ctx.enter_context(tc.tile_pool(name="w2", bufs=2))
         w1 = ctx.enter_context(tc.tile_pool(name="w1", bufs=1))
+        w2 = ctx.enter_context(tc.tile_pool(name="w2", bufs=2))
         w3 = ctx.enter_context(tc.tile_pool(name="w3", bufs=3))
-        sqp = ctx.enter_context(tc.tile_pool(name="sqp", bufs=4))
+        w4 = ctx.enter_context(tc.tile_pool(name="w4", bufs=4))
+        w6 = ctx.enter_context(tc.tile_pool(name="w6", bufs=6))
         ps_tq = ctx.enter_context(tc.psum_pool(name="ps_tq", bufs=1))
         ps_xt = ctx.enter_context(tc.psum_pool(name="ps_xt", bufs=1))
         ps_sp = ctx.enter_context(tc.psum_pool(name="ps_sp", bufs=3))
         ps_pb = ctx.enter_context(tc.psum_pool(name="ps_pb", bufs=3))
+        if PIN:
+            ctx.enter_context(tc.manual_schedule())
+
+        warm = const.tile([P, 2], F32)
+        nc.vector.memset(warm[:, 0:1], 0.0)
+        nc.scalar.activation(out=warm[:, 1:2], in_=warm[:, 0:1], func=ACTF.Silu)
 
         x_sb = const.tile([P, 64, NI], BF16)
         x_v = x.rearrange("(p n) i -> p n i", n=64)
-        for a in range(4):
-            nc.sync.dma_start(out=x_sb[:, 16 * a:16 * a + 16, :], in_=x_v[:, 16 * a:16 * a + 16, :])
-        bw_sb = const.tile([P, NO], BF16)
-        nc.scalar.dma_start(out=bw_sb[:], in_=base_weight)
+        for lo, hi in ((0, 4), (4, 16), (16, 40), (40, 64)):
+            nc.sync.dma_start(out=x_sb[:, lo:hi, :], in_=x_v[:, lo:hi, :])
         c_ld = const.tile([P, 4, NO * NB], BF16)
         c_v = coeff.rearrange("(j t) o r -> j t (o r)", t=4)
         for q in range(4):
             nc.scalar.dma_start(out=c_ld[32 * q:32 * q + 32, :, :], in_=c_v)
+        bw_sb = const.tile([P, NO], BF16)
+        nc.scalar.dma_start(out=bw_sb[:], in_=base_weight)
 
         ident_f = const.tile([P, P], F32)
         make_identity(nc, ident_f[:])
         ident_b = const.tile([P, P], BF16)
         make_identity(nc, ident_b[:])
-
         c_z = const.tile([P, NB, 4, NO], U32, align_bytes=64)
-        nc.vector.memset(c_z[:].bitcast(I32), 0)
+        nc.gpsimd.memset(c_z[:].bitcast(F32), 0.0)
+
         c_g = const.tile([P, NB, NO, 4], BF16, align_bytes=64)
         c_p = c_ld[:].rearrange("p t (o r) -> p r o t", r=NB)
-        nc.scalar.copy(out=c_g[:, 0:4], in_=c_p[:, 0:4])
-        nc.vector.tensor_copy(out=c_g[:, 4:8], in_=c_p[:, 4:8])
         c_full = const.tile([P, NB * NO], U32, align_bytes=64)
         c_scl = const.tile([P, NB * NO], U8, align_bytes=64)
-        for h in range(2):
-            nc.vector.quantize_mx(
-                out=c_full[:, 1024 * h:1024 * h + 1024].bitcast(FP8X4),
-                scales=c_scl[:, 1024 * h:1024 * h + 1024],
-                in_=c_g[:, 4 * h:4 * h + 4].rearrange("p r o t -> p (r o t)"),
-            )
-        for q in range(4):
-            nc.vector.tensor_copy(
-                out=c_z[32 * q:32 * q + 32, :, q, :].bitcast(I32),
-                in_=c_full[32 * q:32 * q + 32, :].rearrange("p (r o) -> p r o", r=NB).bitcast(I32),
-            )
+
+        def coeff_prep(h):
+            nc.vector.tensor_copy(out=c_g[:, 4 * h:4 * h + 4], in_=c_p[:, 4 * h:4 * h + 4])
+
+        def coeff_quant():
+            for h in range(2):
+                nc.vector.quantize_mx(
+                    out=c_full[:, 1024 * h:1024 * h + 1024].bitcast(FP8X4),
+                    scales=c_scl[:, 1024 * h:1024 * h + 1024],
+                    in_=c_g[:, 4 * h:4 * h + 4].rearrange("p r o t -> p (r o t)"),
+                )
+            for q in range(4):
+                nc.vector.tensor_copy(
+                    out=c_z[32 * q:32 * q + 32, :, q, :].bitcast(I32),
+                    in_=c_full[32 * q:32 * q + 32, :].rearrange("p (r o) -> p r o", r=NB).bitcast(I32),
+                )
 
         xw = x_sb[:].rearrange("p n i -> p (n i)").bitcast(F32)
         out_v = out.rearrange("(p n) o -> p n o", n=64)
-        state = {}
+        st = {}
 
-        def front(c):
-            tq = ps_tq.tile([P, G, 2, P], F32, name="tq")
-            for gg in range(G):
-                g = c * G + gg
-                for u in range(2):
-                    nc.tensor.transpose(tq[:, gg, u, :], xw[:, g * 256 + u:(g + 1) * 256:2], ident_f[:])
-            xt_ps = ps_xt.tile([P, 4 * G, P], BF16, name="xt_ps")
-            for m in range(4 * G):
-                nc.tensor.transpose(xt_ps[:, m, :], x_sb[:, c * 4 * G + m, :], ident_b[:])
-            xq_raw = w3.tile([P, F], BF16, name="xq_raw")
+        def s0(c):
+            tq = ps_tq.tile([P, 2, P], F32, name="tq")
+            for u in range(2):
+                nc.tensor.transpose(tq[:, u, :], xw[:, c * 256 + u:(c + 1) * 256:2], ident_f[:])
+            xt_ps = ps_xt.tile([P, 4, P], BF16, name="xt_ps")
+            for m in range(4):
+                nc.tensor.transpose(xt_ps[:, m, :], x_sb[:, c * 4 + m, :], ident_b[:])
+            xq_raw = w2.tile([P, F], BF16, name="xq_raw")
             nc.scalar.copy(
-                out=xq_raw[:].bitcast(F32).rearrange("p (g b u) -> p g b u", g=G, u=2),
-                in_=tq[:].rearrange("p g u b -> p g b u"),
+                out=xq_raw[:].bitcast(F32).rearrange("p (b u) -> p b u", u=2),
+                in_=tq[:].rearrange("p u b -> p b u"),
             )
-            xT = w3.tile([P, 4 * G * P], BF16, name="xT")
+            xT = w6.tile([P, 4 * P], BF16, name="xT")
             nc.scalar.copy(out=xT[:], in_=xt_ps[:].rearrange("p m b -> p (m b)"))
-            xq = w3.tile([P, F], BF16, name="xq")
+            xq = w4.tile([P, F], BF16, name="xq")
             nc.vector.tensor_scalar(out=xq[:], in0=xq_raw[:], scalar1=T[3], scalar2=T[8],
                                     op0=ALU.max, op1=ALU.min)
-            state[("xq", c)] = xq
-            state[("xT", c)] = xT
+            st[("xq", c)] = xq
+            st[("xT", c)] = xT
+
+        def s0b(c):
+            xa = w4.tile([P, F], BF16, name="xa")
+            nc.vector.tensor_single_scalar(out=xa[:].bitcast(I32), in_=st[("xq", c)][:].bitcast(I32),
+                                           scalar=0x7FFF7FFF, op=ALU.bitwise_and)
+            st[("xa", c)] = xa
+
+        KS = (4, 5, 6, 7, 8)
+
+        def s1(c):
+            for k in KS:
+                sq = w6.tile([P, F], F32, name="sq")
+                if k == 8:
+                    nc.scalar.activation(out=sq[:], in_=st[("xa", c)][:], func=ACTF.Square,
+                                         bias=-SIG * T[8], scale=SIG)
+                else:
+                    nc.scalar.activation(out=sq[:], in_=st[("xq", c)][:], func=ACTF.Square,
+                                         bias=-T[k], scale=1.0)
+                st[("sq", c, k)] = sq
+
+        def s2(c):
+            for k in KS:
+                v = w2.tile([P, F], F32, name="V%d" % k)
+                src = st[("xa", c)] if k == 8 else st[("xq", c)]
+                nc.vector.scalar_tensor_tensor(out=v[:], in0=src[:], scalar=T[k], in1=st[("sq", c, k)][:],
+                                               op0=ALU.subtract, op1=ALU.mult)
+                st[("V", c, k)] = v
+
+        def s3(c):
+            bas = w2.tile([P, NB, F], BF16, name="bas", align_bytes=64)
+            st[("bas", c)] = bas
+
+            def relu(k, s, nm):
+                t = w2.tile([P, F], F32, name=nm)
+                nc.scalar.activation(out=t[:], in_=st[("V", c, k)][:], func=ACTF.Relu, scale=s)
+                st[(nm, c)] = t
+
+            relu(4, -beta(0, 4), "q4")
+            relu(5, -beta(1, 4), "q5")
+            relu(6, -beta(2, 4), "q6")
+            relu(7, -beta(3, 4), "q7")
+            relu(7, beta(7, 0), "p7")
+            relu(6, beta(6, 0), "p6")
+            relu(5, beta(5, 0), "p5")
+            relu(4, beta(4, 0), "p4")
+            nc.scalar.activation(out=bas[:, 0, :], in_=st[("V", c, 4)][:], func=ACTF.Relu, scale=-beta(0, 4))
+            nc.scalar.activation(out=bas[:, 7, :], in_=st[("V", c, 7)][:], func=ACTF.Relu, scale=beta(7, 0))
 
         def stt(o, a, s, b, op1=ALU.add):
             nc.vector.scalar_tensor_tensor(out=o, in0=a, scalar=s, in1=b, op0=ALU.mult, op1=op1)
 
-        def middle(c):
-            xq = state[("xq", c)]
-            V = {}
-            for k in (4, 5, 6, 7, 3, 8):
-                sq = sqp.tile([P, F], F32, name="sq")
-                nc.scalar.activation(out=sq[:], in_=xq[:], func=ACTF.Square, bias=-T[k], scale=1.0)
-                V[k] = w2.tile([P, F], F32, name="V%d" % k)
-                nc.vector.scalar_tensor_tensor(out=V[k][:], in0=xq[:], scalar=T[k], in1=sq[:],
-                                               op0=ALU.subtract, op1=ALU.mult)
-            bas = w2.tile([P, NB, F], BF16, name="bas", align_bytes=64)
-
-            def relu(k, s, nm):
-                t = w2.tile([P, F], F32, name=nm)
-                nc.scalar.activation(out=t[:], in_=V[k][:], func=ACTF.Relu, scale=s)
-                return t
-
-            q4 = relu(4, -beta(0, 4), "q4")
-            q5 = relu(5, -beta(1, 4), "q5")
-            nc.scalar.activation(out=bas[:, 0, :], in_=V[4][:], func=ACTF.Relu, scale=-beta(0, 4))
-            stt(bas[:, 1, :], q4[:], beta(1, 3) / beta(0, 4), q5[:])
+        def s4(c):
+            bas = st[("bas", c)]
+            q4, q5, q6, q7 = [st[(n, c)] for n in ("q4", "q5", "q6", "q7")]
+            p4, p5, p6, p7 = [st[(n, c)] for n in ("p4", "p5", "p6", "p7")]
+            en = st[("V", c, 8)]
             c2 = beta(2, 3) / beta(1, 4)
-            x2 = w1.tile([P, F], F32, name="x2")
-            stt(x2[:], q4[:], (beta(2, 2) / beta(0, 4)) / c2, q5[:])
-            q6 = relu(6, -beta(2, 4), "q6")
-            stt(bas[:, 2, :], x2[:], c2, q6[:])
-            c3 = beta(3, 3) / beta(2, 4)
-            x3 = w1.tile([P, F], F32, name="x3")
-            stt(x3[:], q5[:], (beta(3, 2) / beta(1, 4)) / c3, q6[:])
-            q7 = relu(7, -beta(3, 4), "q7")
-            s3 = w1.tile([P, F], F32, name="s3")
-            stt(s3[:], x3[:], c3, q7[:])
-            stt(bas[:, 3, :], V[3][:], beta(3, 0), s3[:], op1=ALU.min)
-            p7 = relu(7, beta(7, 0), "p7")
-            p6 = relu(6, beta(6, 0), "p6")
-            nc.scalar.activation(out=bas[:, 7, :], in_=V[7][:], func=ACTF.Relu, scale=beta(7, 0))
-            stt(bas[:, 6, :], p7[:], beta(6, 1) / beta(7, 0), p6[:])
             c5 = beta(5, 1) / beta(6, 0)
+            x2 = w1.tile([P, F], F32, name="x2")
             x5 = w1.tile([P, F], F32, name="x5")
+            r3 = w1.tile([P, F], BF16, name="r3")
+            r4 = w1.tile([P, F], BF16, name="r4")
+            l3 = w1.tile([P, F], BF16, name="l3")
+            l4 = w1.tile([P, F], BF16, name="l4")
+            stt(x2[:], q4[:], (beta(2, 2) / beta(0, 4)) / c2, q5[:])
             stt(x5[:], p7[:], (beta(5, 2) / beta(7, 0)) / c5, p6[:])
-            p5 = relu(5, beta(5, 0), "p5")
+            stt(r4[:], q7[:], beta(4, 3) / beta(3, 4), en[:], op1=ALU.subtract)
+            stt(l4[:], p5[:], beta(4, 1) / beta(5, 0), p4[:])
+            stt(r3[:], q6[:], beta(3, 3) / beta(2, 4), q7[:])
+            stt(l3[:], p4[:], beta(3, 1) / beta(4, 0), en[:], op1=ALU.subtract)
+            stt(bas[:, 2, :], x2[:], c2, q6[:])
             stt(bas[:, 5, :], x5[:], c5, p5[:])
-            c4 = beta(4, 1) / beta(5, 0)
-            x4 = w1.tile([P, F], F32, name="x4")
-            stt(x4[:], p6[:], (beta(4, 2) / beta(6, 0)) / c4, p5[:])
-            p4 = relu(4, beta(4, 0), "p4")
-            s4 = w1.tile([P, F], F32, name="s4")
-            stt(s4[:], x4[:], c4, p4[:])
-            stt(bas[:, 4, :], V[8][:], -beta(4, 4), s4[:], op1=ALU.min)
+            nc.vector.tensor_tensor(out=bas[:, 4, :], in0=l4[:], in1=r4[:], op=ALU.max)
+            nc.vector.tensor_tensor(out=bas[:, 3, :], in0=l3[:], in1=r3[:], op=ALU.max)
+            stt(bas[:, 1, :], q4[:], beta(1, 3) / beta(0, 4), q5[:])
+            stt(bas[:, 6, :], p7[:], beta(6, 1) / beta(7, 0), p6[:])
 
+        def s4q(c):
+            bas = st[("bas", c)]
             cod = w2.tile([P, NB * F // 4], U32, name="cod", align_bytes=64)
             scl = w2.tile([P, NB * F // 4], U8, name="scl", align_bytes=64)
-            per = 4096 // F
-            for h in range(NB // per):
-                wd = per * F // 4
-                nc.vector.quantize_mx(
-                    out=cod[:, h * wd:(h + 1) * wd].bitcast(FP8X4),
-                    scales=scl[:, h * wd:(h + 1) * wd],
-                    in_=bas[:, h * per:(h + 1) * per, :].rearrange("p r f -> p (r f)"),
-                )
-            state[("cod", c)] = cod
-            state[("scl", c)] = scl
+            nc.vector.quantize_mx(out=cod[:].bitcast(FP8X4), scales=scl[:],
+                                  in_=bas[:].rearrange("p r f -> p (r f)"))
+            st[("cod", c)] = cod
+            st[("scl", c)] = scl
 
-        def back(c):
-            cod = state[("cod", c)]
-            scl = state[("scl", c)]
-            xT = state[("xT", c)]
-            for gg in range(G):
-                g = c * G + gg
-                o_sb = w2.tile([P, 4, NO], F32, name="o_sb")
-                for h in range(2):
-                    sp = ps_sp.tile([P, 2, NO], F32, name="sp")
-                    pb = ps_pb.tile([P, 2, NO], F32, name="pb")
-                    for qq in range(2):
-                        q = 2 * h + qq
-                        nc.tensor.matmul(out=pb[:, qq, :], lhsT=xT[:, (4 * gg + q) * P:(4 * gg + q + 1) * P],
-                                         rhs=bw_sb[:], start=True, stop=True)
-                    for qq in range(2):
-                        q = 2 * h + qq
-                        for r in range(NB):
-                            lo = r * (F // 4) + gg * P
-                            nc.tensor.matmul_mx(
-                                out=sp[:, qq, :],
-                                lhsT=cod[:, lo:lo + P].bitcast(FP8X4),
-                                lhsT_scale=scl[:, lo:lo + P],
-                                rhs=c_z[:, r, q, :].bitcast(FP8X4),
-                                rhs_scale=c_scl[:, r * NO:(r + 1) * NO],
-                                start=(r == 0),
-                                stop=(r == NB - 1),
-                            )
-                    sil = w2.tile([P, 2 * NO], F32, name="sil")
-                    nc.scalar.activation(out=sil[:], in_=pb[:].rearrange("p a o -> p (a o)"), func=ACTF.Silu)
-                    nc.vector.tensor_tensor(out=o_sb[:, 2 * h:2 * h + 2, :].rearrange("p a o -> p (a o)"),
-                                            in0=sp[:].rearrange("p a o -> p (a o)"), in1=sil[:], op=ALU.add)
-                nc.sync.dma_start(out=out_v[:, 4 * g:4 * g + 4, :], in_=o_sb[:])
+        def s5a(c):
+            xT = st[("xT", c)]
+            for h in range(2):
+                pb = ps_pb.tile([P, 2, NO], F32, name="pb")
+                for qq in range(2):
+                    q = 2 * h + qq
+                    nc.tensor.matmul(out=pb[:, qq, :], lhsT=xT[:, q * P:(q + 1) * P],
+                                     rhs=bw_sb[:], start=True, stop=True)
+                sil = w4.tile([P, 2 * NO], F32, name="sil")
+                nc.scalar.activation(out=sil[:], in_=pb[:].rearrange("p a o -> p (a o)"), func=ACTF.Silu)
+                st[("sil", c, h)] = sil
 
-        front(0)
-        front(1)
-        for c in range(NCH):
-            if c + 2 < NCH:
-                front(c + 2)
-            middle(c)
-            if c >= 1:
-                back(c - 1)
-        back(NCH - 1)
+        def s5b(c):
+            cod = st[("cod", c)]
+            scl = st[("scl", c)]
+            for h in range(2):
+                sp = ps_sp.tile([P, 2, NO], F32, name="sp")
+                for qq in range(2):
+                    q = 2 * h + qq
+                    for r in range(NB):
+                        lo = r * (F // 4)
+                        nc.tensor.matmul_mx(
+                            out=sp[:, qq, :],
+                            lhsT=cod[:, lo:lo + P].bitcast(FP8X4),
+                            lhsT_scale=scl[:, lo:lo + P],
+                            rhs=c_z[:, r, q, :].bitcast(FP8X4),
+                            rhs_scale=c_scl[:, r * NO:(r + 1) * NO],
+                            start=(r == 0),
+                            stop=(r == NB - 1),
+                        )
+                st[("sp", c, h)] = sp
+
+        def s6(c):
+            o_sb = w3.tile([P, 4, NO], F32, name="o_sb")
+            for h in range(2):
+                nc.vector.tensor_tensor(out=o_sb[:, 2 * h:2 * h + 2, :].rearrange("p a o -> p (a o)"),
+                                        in0=st[("sp", c, h)][:].rearrange("p a o -> p (a o)"),
+                                        in1=st[("sil", c, h)][:], op=ALU.add)
+            nc.sync.dma_start(out=out_v[:, 4 * c:4 * c + 4, :], in_=o_sb[:])
+
+        def ok(c):
+            return 0 <= c < NCH
+
+        for p in range(-3, NCH + 2):
+            if ok(p + 1):
+                s2(p + 1)
+            if ok(p + 2):
+                s1(p + 2)
+            if ok(p - 1):
+                s5a(p - 1)
+            if ok(p + 1):
+                s3(p + 1)
+            if p == -1:
+                coeff_prep(0)
+                coeff_prep(1)
+            if ok(p):
+                s4(p)
+            if ok(p - 1):
+                s5b(p - 1)
+                s6(p - 1)
+            if ok(p + 3):
+                s0(p + 3)
+            if p == 0:
+                coeff_quant()
+            if ok(p):
+                s4q(p)
+            if ok(p + 3):
+                s0b(p + 3)

@@ -28,12 +28,14 @@ def beta(r, j):
     return (T[r + 4] - T[r]) / prod
 
 
-assert T[3] == -T[8] and beta(3, 0) == beta(4, 4)
+assert all(T[k] == -T[11 - k] for k in range(12))
+assert all(abs(beta(r, j) - beta(7 - r, 4 - j)) < 1e-12 for r in range(8) for j in range(5))
 SIG = beta(4, 4) ** 0.5
+G0, G1, G2, G3 = beta(0, 4), beta(1, 4), beta(2, 4), beta(3, 4)
 
 F = 512
 NCH = 16
-PIN = True
+DUP_ON_DVE = False
 
 
 def tile_bsplinekanlayer_t_kernel(tc, x, coeff, base_weight, knots, out):
@@ -47,10 +49,9 @@ def tile_bsplinekanlayer_t_kernel(tc, x, coeff, base_weight, knots, out):
         w6 = ctx.enter_context(tc.tile_pool(name="w6", bufs=6))
         ps_tq = ctx.enter_context(tc.psum_pool(name="ps_tq", bufs=1))
         ps_xt = ctx.enter_context(tc.psum_pool(name="ps_xt", bufs=1))
-        ps_sp = ctx.enter_context(tc.psum_pool(name="ps_sp", bufs=3))
-        ps_pb = ctx.enter_context(tc.psum_pool(name="ps_pb", bufs=3))
-        if PIN:
-            ctx.enter_context(tc.manual_schedule())
+        ps_sp = ctx.enter_context(tc.psum_pool(name="ps_sp", bufs=4))
+        ps_pb = ctx.enter_context(tc.psum_pool(name="ps_pb", bufs=2))
+        ctx.enter_context(tc.manual_schedule())
 
         warm = const.tile([P, 2], F32)
         nc.vector.memset(warm[:, 0:1], 0.0)
@@ -58,7 +59,7 @@ def tile_bsplinekanlayer_t_kernel(tc, x, coeff, base_weight, knots, out):
 
         x_sb = const.tile([P, 64, NI], BF16)
         x_v = x.rearrange("(p n) i -> p n i", n=64)
-        for lo, hi in ((0, 4), (4, 16), (16, 40), (40, 64)):
+        for lo, hi in ((0, 4), (4, 16)):
             nc.sync.dma_start(out=x_sb[:, lo:hi, :], in_=x_v[:, lo:hi, :])
         c_ld = const.tile([P, 4, NO * NB], BF16)
         c_v = coeff.rearrange("(j t) o r -> j t (o r)", t=4)
@@ -66,6 +67,8 @@ def tile_bsplinekanlayer_t_kernel(tc, x, coeff, base_weight, knots, out):
             nc.scalar.dma_start(out=c_ld[32 * q:32 * q + 32, :, :], in_=c_v)
         bw_sb = const.tile([P, NO], BF16)
         nc.scalar.dma_start(out=bw_sb[:], in_=base_weight)
+        for lo, hi in ((16, 40), (40, 64)):
+            nc.sync.dma_start(out=x_sb[:, lo:hi, :], in_=x_v[:, lo:hi, :])
 
         ident_f = const.tile([P, P], F32)
         make_identity(nc, ident_f[:])
@@ -106,103 +109,104 @@ def tile_bsplinekanlayer_t_kernel(tc, x, coeff, base_weight, knots, out):
             xt_ps = ps_xt.tile([P, 4, P], BF16, name="xt_ps")
             for m in range(4):
                 nc.tensor.transpose(xt_ps[:, m, :], x_sb[:, c * 4 + m, :], ident_b[:])
-            xq_raw = w2.tile([P, F], BF16, name="xq_raw")
+            xq_raw = w3.tile([P, F], BF16, name="xq_raw")
             nc.scalar.copy(
                 out=xq_raw[:].bitcast(F32).rearrange("p (b u) -> p b u", u=2),
                 in_=tq[:].rearrange("p u b -> p b u"),
             )
             xT = w6.tile([P, 4 * P], BF16, name="xT")
             nc.scalar.copy(out=xT[:], in_=xt_ps[:].rearrange("p m b -> p (m b)"))
-            xq = w4.tile([P, F], BF16, name="xq")
-            nc.vector.tensor_scalar(out=xq[:], in0=xq_raw[:], scalar1=T[3], scalar2=T[8],
-                                    op0=ALU.max, op1=ALU.min)
-            st[("xq", c)] = xq
+            st[("xq_raw", c)] = xq_raw
             st[("xT", c)] = xT
 
+        def s0c(c):
+            xy = w4.tile([P, 2, F], BF16, name="xy")
+            nc.vector.tensor_scalar(out=xy[:, 0, :], in0=st[("xq_raw", c)][:], scalar1=T[3], scalar2=T[8],
+                                    op0=ALU.max, op1=ALU.min)
+            st[("xy", c)] = xy
+
         def s0b(c):
+            xy = st[("xy", c)]
+            nc.vector.tensor_scalar(out=xy[:, 1, :], in0=xy[:, 0, :], scalar1=-1.0, scalar2=None, op0=ALU.mult)
             xa = w4.tile([P, F], BF16, name="xa")
-            nc.vector.tensor_single_scalar(out=xa[:].bitcast(I32), in_=st[("xq", c)][:].bitcast(I32),
+            nc.vector.tensor_single_scalar(out=xa[:].bitcast(I32), in_=xy[:, 0, :].bitcast(I32),
                                            scalar=0x7FFF7FFF, op=ALU.bitwise_and)
             st[("xa", c)] = xa
 
-        KS = (4, 5, 6, 7, 8)
-
         def s1(c):
-            for k in KS:
-                sq = w6.tile([P, F], F32, name="sq")
-                if k == 8:
-                    nc.scalar.activation(out=sq[:], in_=st[("xa", c)][:], func=ACTF.Square,
-                                         bias=-SIG * T[8], scale=SIG)
-                else:
-                    nc.scalar.activation(out=sq[:], in_=st[("xq", c)][:], func=ACTF.Square,
-                                         bias=-T[k], scale=1.0)
+            for k in (4, 5):
+                sq = w3.tile([P, 2, F], F32, name="sq")
+                nc.scalar.activation(out=sq[:], in_=st[("xy", c)][:], func=ACTF.Square, bias=-T[k], scale=1.0)
                 st[("sq", c, k)] = sq
+            sqe = w2.tile([P, F], F32, name="sqe")
+            nc.scalar.activation(out=sqe[:], in_=st[("xa", c)][:], func=ACTF.Square, bias=-SIG * T[8], scale=SIG)
+            st[("sq", c, 8)] = sqe
 
         def s2(c):
-            for k in KS:
-                v = w2.tile([P, F], F32, name="V%d" % k)
-                src = st[("xa", c)] if k == 8 else st[("xq", c)]
-                nc.vector.scalar_tensor_tensor(out=v[:], in0=src[:], scalar=T[k], in1=st[("sq", c, k)][:],
-                                               op0=ALU.subtract, op1=ALU.mult)
+            for k in (4, 5):
+                v = w2.tile([P, 2, F], F32, name="V%d" % k)
+                nc.vector.scalar_tensor_tensor(out=v[:], in0=st[("xy", c)][:], scalar=T[k],
+                                               in1=st[("sq", c, k)][:], op0=ALU.subtract, op1=ALU.mult)
                 st[("V", c, k)] = v
+            en = w2.tile([P, F], F32, name="en")
+            nc.vector.scalar_tensor_tensor(out=en[:], in0=st[("xa", c)][:], scalar=T[8],
+                                           in1=st[("sq", c, 8)][:], op0=ALU.subtract, op1=ALU.mult)
+            st[("en", c)] = en
 
         def s3(c):
-            bas = w2.tile([P, NB, F], BF16, name="bas", align_bytes=64)
+            bas = w2.tile([P, 4, 2, F], BF16, name="bas", align_bytes=64)
             st[("bas", c)] = bas
-
-            def relu(k, s, nm):
-                t = w2.tile([P, F], F32, name=nm)
-                nc.scalar.activation(out=t[:], in_=st[("V", c, k)][:], func=ACTF.Relu, scale=s)
-                st[(nm, c)] = t
-
-            relu(4, -beta(0, 4), "q4")
-            relu(5, -beta(1, 4), "q5")
-            relu(6, -beta(2, 4), "q6")
-            relu(7, -beta(3, 4), "q7")
-            relu(7, beta(7, 0), "p7")
-            relu(6, beta(6, 0), "p6")
-            relu(5, beta(5, 0), "p5")
-            relu(4, beta(4, 0), "p4")
-            nc.scalar.activation(out=bas[:, 0, :], in_=st[("V", c, 4)][:], func=ACTF.Relu, scale=-beta(0, 4))
-            nc.scalar.activation(out=bas[:, 7, :], in_=st[("V", c, 7)][:], func=ACTF.Relu, scale=beta(7, 0))
+            v4 = st[("V", c, 4)]
+            v5 = st[("V", c, 5)]
+            a4 = w2.tile([P, 2, F], F32, name="a4")
+            a5 = w2.tile([P, 2, F], F32, name="a5")
+            a6 = w2.tile([P, 2, F], F32, name="a6")
+            a7 = w2.tile([P, 2, F], F32, name="a7")
+            nc.scalar.activation(out=a4[:], in_=v4[:], func=ACTF.Relu, scale=-G0)
+            nc.scalar.activation(out=a5[:], in_=v5[:], func=ACTF.Relu, scale=-G1)
+            for h in range(2):
+                nc.scalar.activation(out=a6[:, 1 - h, :], in_=v5[:, h, :], func=ACTF.Relu, scale=G2)
+            for h in range(2):
+                nc.scalar.activation(out=a7[:, 1 - h, :], in_=v4[:, h, :], func=ACTF.Relu, scale=G3)
+            if not DUP_ON_DVE:
+                nc.scalar.activation(out=bas[:, 0], in_=v4[:], func=ACTF.Relu, scale=-G0)
+            st[("a", c)] = (a4, a5, a6, a7)
 
         def stt(o, a, s, b, op1=ALU.add):
             nc.vector.scalar_tensor_tensor(out=o, in0=a, scalar=s, in1=b, op0=ALU.mult, op1=op1)
 
-        def s4(c):
+        def s4(c, first_half_early=False):
             bas = st[("bas", c)]
-            q4, q5, q6, q7 = [st[(n, c)] for n in ("q4", "q5", "q6", "q7")]
-            p4, p5, p6, p7 = [st[(n, c)] for n in ("p4", "p5", "p6", "p7")]
-            en = st[("V", c, 8)]
-            c2 = beta(2, 3) / beta(1, 4)
-            c5 = beta(5, 1) / beta(6, 0)
-            x2 = w1.tile([P, F], F32, name="x2")
-            x5 = w1.tile([P, F], F32, name="x5")
-            r3 = w1.tile([P, F], BF16, name="r3")
-            r4 = w1.tile([P, F], BF16, name="r4")
-            l3 = w1.tile([P, F], BF16, name="l3")
-            l4 = w1.tile([P, F], BF16, name="l4")
-            stt(x2[:], q4[:], (beta(2, 2) / beta(0, 4)) / c2, q5[:])
-            stt(x5[:], p7[:], (beta(5, 2) / beta(7, 0)) / c5, p6[:])
-            stt(r4[:], q7[:], beta(4, 3) / beta(3, 4), en[:], op1=ALU.subtract)
-            stt(l4[:], p5[:], beta(4, 1) / beta(5, 0), p4[:])
-            stt(r3[:], q6[:], beta(3, 3) / beta(2, 4), q7[:])
-            stt(l3[:], p4[:], beta(3, 1) / beta(4, 0), en[:], op1=ALU.subtract)
-            stt(bas[:, 2, :], x2[:], c2, q6[:])
-            stt(bas[:, 5, :], x5[:], c5, p5[:])
-            nc.vector.tensor_tensor(out=bas[:, 4, :], in0=l4[:], in1=r4[:], op=ALU.max)
-            nc.vector.tensor_tensor(out=bas[:, 3, :], in0=l3[:], in1=r3[:], op=ALU.max)
-            stt(bas[:, 1, :], q4[:], beta(1, 3) / beta(0, 4), q5[:])
-            stt(bas[:, 6, :], p7[:], beta(6, 1) / beta(7, 0), p6[:])
+            a4, a5, a6, a7 = st[("a", c)]
+            en = st[("en", c)]
+            c2 = beta(2, 3) / G1
+            x2 = w1.tile([P, 2, F], F32, name="x2")
+            r3 = w1.tile([P, 2, F], BF16, name="r3")
+            l3 = w1.tile([P, 2, F], BF16, name="l3")
+            if first_half_early:
+                stt(bas[:, 1], a4[:], beta(1, 3) / G0, a5[:])
+                stt(x2[:], a4[:], (beta(2, 2) / G0) / c2, a5[:])
+                stt(r3[:], a6[:], beta(3, 3) / G2, a7[:])
+                s4q(c, 0, 2)
+            else:
+                stt(x2[:], a4[:], (beta(2, 2) / G0) / c2, a5[:])
+                stt(r3[:], a6[:], beta(3, 3) / G2, a7[:])
+            stt(l3[:], a7[:], beta(4, 3) / G3, en[:].unsqueeze(1).to_broadcast([P, 2, F]), op1=ALU.subtract)
+            if not first_half_early:
+                stt(bas[:, 1], a4[:], beta(1, 3) / G0, a5[:])
+            stt(bas[:, 2], x2[:], c2, a6[:])
+            for h in range(2):
+                nc.vector.tensor_tensor(out=bas[:, 3, h, :], in0=r3[:, h, :], in1=l3[:, 1 - h, :], op=ALU.max)
 
-        def s4q(c):
+        def s4q(c, lo, hi):
             bas = st[("bas", c)]
-            cod = w2.tile([P, NB * F // 4], U32, name="cod", align_bytes=64)
-            scl = w2.tile([P, NB * F // 4], U8, name="scl", align_bytes=64)
-            nc.vector.quantize_mx(out=cod[:].bitcast(FP8X4), scales=scl[:],
-                                  in_=bas[:].rearrange("p r f -> p (r f)"))
-            st[("cod", c)] = cod
-            st[("scl", c)] = scl
+            if lo == 0:
+                st[("cod", c)] = w2.tile([P, NB * F // 4], U32, name="cod", align_bytes=64)
+                st[("scl", c)] = w2.tile([P, NB * F // 4], U8, name="scl", align_bytes=64)
+            w = 2 * F // 4
+            nc.vector.quantize_mx(out=st[("cod", c)][:, lo * w:hi * w].bitcast(FP8X4),
+                                  scales=st[("scl", c)][:, lo * w:hi * w],
+                                  in_=bas[:, lo:hi].rearrange("p m h f -> p (m h f)"))
 
         def s5a(c):
             xT = st[("xT", c)]
@@ -216,24 +220,25 @@ def tile_bsplinekanlayer_t_kernel(tc, x, coeff, base_weight, knots, out):
                 nc.scalar.activation(out=sil[:], in_=pb[:].rearrange("p a o -> p (a o)"), func=ACTF.Silu)
                 st[("sil", c, h)] = sil
 
+        def mx(c, acc, q, r, start, stop):
+            slot = 2 * r if r < 4 else 2 * (7 - r) + 1
+            lo = slot * (F // 4)
+            nc.tensor.matmul_mx(
+                out=acc,
+                lhsT=st[("cod", c)][:, lo:lo + P].bitcast(FP8X4),
+                lhsT_scale=st[("scl", c)][:, lo:lo + P],
+                rhs=c_z[:, r, q, :].bitcast(FP8X4),
+                rhs_scale=c_scl[:, r * NO:(r + 1) * NO],
+                start=start,
+                stop=stop,
+            )
+
         def s5b(c):
-            cod = st[("cod", c)]
-            scl = st[("scl", c)]
             for h in range(2):
                 sp = ps_sp.tile([P, 2, NO], F32, name="sp")
                 for qq in range(2):
-                    q = 2 * h + qq
                     for r in range(NB):
-                        lo = r * (F // 4)
-                        nc.tensor.matmul_mx(
-                            out=sp[:, qq, :],
-                            lhsT=cod[:, lo:lo + P].bitcast(FP8X4),
-                            lhsT_scale=scl[:, lo:lo + P],
-                            rhs=c_z[:, r, q, :].bitcast(FP8X4),
-                            rhs_scale=c_scl[:, r * NO:(r + 1) * NO],
-                            start=(r == 0),
-                            stop=(r == NB - 1),
-                        )
+                        mx(c, sp[:, qq, :], 2 * h + qq, r, r == 0, r == NB - 1)
                 st[("sp", c, h)] = sp
 
         def s6(c):
@@ -244,31 +249,75 @@ def tile_bsplinekanlayer_t_kernel(tc, x, coeff, base_weight, knots, out):
                                         in1=st[("sil", c, h)][:], op=ALU.add)
             nc.sync.dma_start(out=out_v[:, 4 * c:4 * c + 4, :], in_=o_sb[:])
 
+        def last_first(c):
+            for q in range(4):
+                sp = ps_sp.tile([P, 2, NO], F32, name="sp")
+                st[("spq", q)] = sp
+                for i, r in enumerate((0, 7, 1, 6)):
+                    mx(c, sp[:, 0, :], q, r, i == 0, False)
+
+        def last_second(c):
+            o_sb = w3.tile([P, 4, NO], F32, name="o_sb")
+            for q in range(4):
+                for i, r in enumerate((2, 5, 3, 4)):
+                    mx(c, st[("spq", q)][:, 0, :], q, r, False, i == 3)
+            for q in range(4):
+                nc.vector.tensor_tensor(out=o_sb[:, q, :], in0=st[("spq", q)][:, 0, :],
+                                        in1=st[("sil", c, q // 2)][:, (q % 2) * NO:(q % 2 + 1) * NO], op=ALU.add)
+                if q % 2 == 1:
+                    nc.sync.dma_start(out=out_v[:, 4 * c + q - 1:4 * c + q + 1, :], in_=o_sb[:, q - 1:q + 1, :])
+
         def ok(c):
             return 0 <= c < NCH
 
-        for p in range(-3, NCH + 2):
+        s0(0)
+        s0c(0)
+        s0b(0)
+        s1(0)
+        s0(1)
+        s0(2)
+        s2(0)
+        s0c(1)
+        s0b(1)
+        s1(1)
+        s3(0)
+        s2(1)
+        s0c(2)
+        s0b(2)
+        coeff_prep(0)
+        coeff_prep(1)
+        s1(2)
+        s3(1)
+        s4(0)
+        s0(3)
+        s0c(3)
+        coeff_quant()
+        s4q(0, 0, 4)
+        s0b(3)
+        for p in range(1, NCH):
+            last = p == NCH - 1
             if ok(p + 1):
                 s2(p + 1)
             if ok(p + 2):
                 s1(p + 2)
-            if ok(p - 1):
-                s5a(p - 1)
+            s5a(p - 1)
+            if last:
+                s5a(p)
             if ok(p + 1):
                 s3(p + 1)
-            if p == -1:
-                coeff_prep(0)
-                coeff_prep(1)
-            if ok(p):
-                s4(p)
-            if ok(p - 1):
-                s5b(p - 1)
+            s5b(p - 1)
+            if last:
+                s4(p, True)
+                last_first(p)
                 s6(p - 1)
-            if ok(p + 3):
-                s0(p + 3)
-            if p == 0:
-                coeff_quant()
-            if ok(p):
-                s4q(p)
-            if ok(p + 3):
-                s0b(p + 3)
+                s4q(p, 2, 4)
+                last_second(p)
+            else:
+                s4(p)
+                s6(p - 1)
+                if ok(p + 3):
+                    s0(p + 3)
+                    s0c(p + 3)
+                s4q(p, 0, 4)
+                if ok(p + 3):
+                    s0b(p + 3)

@@ -46,7 +46,7 @@ def tile_bsplinekanlayer_t_kernel(tc, x, coeff, base_weight, knots, out):
         w2 = ctx.enter_context(tc.tile_pool(name="w2", bufs=2))
         w3 = ctx.enter_context(tc.tile_pool(name="w3", bufs=3))
         w4 = ctx.enter_context(tc.tile_pool(name="w4", bufs=4))
-        w6 = ctx.enter_context(tc.tile_pool(name="w6", bufs=6))
+        w7 = ctx.enter_context(tc.tile_pool(name="w7", bufs=7))
         ps_tq = ctx.enter_context(tc.psum_pool(name="ps_tq", bufs=1))
         ps_xt = ctx.enter_context(tc.psum_pool(name="ps_xt", bufs=1))
         ps_sp = ctx.enter_context(tc.psum_pool(name="ps_sp", bufs=4))
@@ -114,44 +114,55 @@ def tile_bsplinekanlayer_t_kernel(tc, x, coeff, base_weight, knots, out):
                 out=xq_raw[:].bitcast(F32).rearrange("p (b u) -> p b u", u=2),
                 in_=tq[:].rearrange("p u b -> p b u"),
             )
-            xT = w6.tile([P, 4 * P], BF16, name="xT")
+            xT = w7.tile([P, 4 * P], BF16, name="xT")
             nc.scalar.copy(out=xT[:], in_=xt_ps[:].rearrange("p m b -> p (m b)"))
             st[("xq_raw", c)] = xq_raw
             st[("xT", c)] = xT
 
-        def s0c(c):
-            xy = w4.tile([P, 2, F], BF16, name="xy")
-            nc.vector.tensor_scalar(out=xy[:, 0, :], in0=st[("xq_raw", c)][:], scalar1=T[3], scalar2=T[8],
-                                    op0=ALU.max, op1=ALU.min)
-            st[("xy", c)] = xy
-
-        def s0b(c):
-            xy = st[("xy", c)]
-            nc.vector.tensor_scalar(out=xy[:, 1, :], in0=xy[:, 0, :], scalar1=-1.0, scalar2=None, op0=ALU.mult)
-            xa = w4.tile([P, F], BF16, name="xa")
-            nc.vector.tensor_single_scalar(out=xa[:].bitcast(I32), in_=xy[:, 0, :].bitcast(I32),
-                                           scalar=0x7FFF7FFF, op=ALU.bitwise_and)
-            st[("xa", c)] = xa
+        def cl(c, step):
+            if step == 0:
+                xy = w4.tile([P, 2, F], BF16, name="xy")
+                nc.vector.tensor_scalar(out=xy[:, 0, :], in0=st[("xq_raw", c)][:], scalar1=T[3], scalar2=T[8],
+                                        op0=ALU.max, op1=ALU.min)
+                st[("xy", c)] = xy
+            elif step == 1:
+                xy = st[("xy", c)]
+                nc.vector.tensor_scalar(out=xy[:, 1, :], in0=xy[:, 0, :], scalar1=-1.0, scalar2=None,
+                                        op0=ALU.mult)
+            else:
+                xa = w4.tile([P, F], BF16, name="xa")
+                nc.vector.tensor_single_scalar(out=xa[:].bitcast(I32), in_=st[("xy", c)][:, 0, :].bitcast(I32),
+                                               scalar=0x7FFF7FFF, op=ALU.bitwise_and)
+                st[("xa", c)] = xa
 
         def s1(c):
             for k in (4, 5):
-                sq = w3.tile([P, 2, F], F32, name="sq")
+                sq = w4.tile([P, 2, F], F32, name="sq")
                 nc.scalar.activation(out=sq[:], in_=st[("xy", c)][:], func=ACTF.Square, bias=-T[k], scale=1.0)
                 st[("sq", c, k)] = sq
             sqe = w2.tile([P, F], F32, name="sqe")
             nc.scalar.activation(out=sqe[:], in_=st[("xa", c)][:], func=ACTF.Square, bias=-SIG * T[8], scale=SIG)
             st[("sq", c, 8)] = sqe
 
-        def s2(c):
-            for k in (4, 5):
+        def cube(c, step):
+            if step < 2:
+                k = 4 + step
                 v = w2.tile([P, 2, F], F32, name="V%d" % k)
                 nc.vector.scalar_tensor_tensor(out=v[:], in0=st[("xy", c)][:], scalar=T[k],
                                                in1=st[("sq", c, k)][:], op0=ALU.subtract, op1=ALU.mult)
                 st[("V", c, k)] = v
-            en = w2.tile([P, F], F32, name="en")
-            nc.vector.scalar_tensor_tensor(out=en[:], in0=st[("xa", c)][:], scalar=T[8],
-                                           in1=st[("sq", c, 8)][:], op0=ALU.subtract, op1=ALU.mult)
-            st[("en", c)] = en
+            else:
+                en = w2.tile([P, F], F32, name="en")
+                nc.vector.scalar_tensor_tensor(out=en[:], in0=st[("xa", c)][:], scalar=T[8],
+                                               in1=st[("sq", c, 8)][:], op0=ALU.subtract, op1=ALU.mult)
+                st[("en", c)] = en
+
+        def s2x(c, d):
+            for step in range(3):
+                if ok(c):
+                    cube(c, step)
+                if ok(d):
+                    cl(d, step)
 
         def s3(c):
             bas = w2.tile([P, 4, 2, F], BF16, name="bas", align_bytes=64)
@@ -271,41 +282,32 @@ def tile_bsplinekanlayer_t_kernel(tc, x, coeff, base_weight, knots, out):
             return 0 <= c < NCH
 
         s0(0)
-        s0c(0)
-        s0b(0)
+        s2x(-1, 0)
         s1(0)
         s0(1)
-        s0(2)
-        s2(0)
-        s0c(1)
-        s0b(1)
+        s2x(0, 1)
         s1(1)
-        s3(0)
-        s2(1)
-        s0c(2)
-        s0b(2)
+        s0(2)
         coeff_prep(0)
         coeff_prep(1)
-        s1(2)
-        s3(1)
-        s4(0)
+        s2x(-1, 2)
+        s3(0)
         s0(3)
-        s0c(3)
-        coeff_quant()
-        s4q(0, 0, 4)
-        s0b(3)
-        for p in range(1, NCH):
+        for p in range(NCH):
             last = p == NCH - 1
-            if ok(p + 1):
-                s2(p + 1)
+            s2x(p + 1, p + 3)
             if ok(p + 2):
                 s1(p + 2)
-            s5a(p - 1)
+            if ok(p - 1):
+                s5a(p - 1)
             if last:
                 s5a(p)
             if ok(p + 1):
                 s3(p + 1)
-            s5b(p - 1)
+            if ok(p + 4):
+                s0(p + 4)
+            if ok(p - 1):
+                s5b(p - 1)
             if last:
                 s4(p, True)
                 last_first(p)
@@ -314,10 +316,8 @@ def tile_bsplinekanlayer_t_kernel(tc, x, coeff, base_weight, knots, out):
                 last_second(p)
             else:
                 s4(p)
-                s6(p - 1)
-                if ok(p + 3):
-                    s0(p + 3)
-                    s0c(p + 3)
+                if ok(p - 1):
+                    s6(p - 1)
+                if p == 0:
+                    coeff_quant()
                 s4q(p, 0, 4)
-                if ok(p + 3):
-                    s0b(p + 3)

@@ -175,10 +175,8 @@ def tile_bsplinekanlayer_t_kernel(tc, x, coeff, base_weight, knots, out):
             a7 = w2.tile([P, 2, F], F32, name="a7")
             nc.scalar.activation(out=a4[:], in_=v4[:], func=ACTF.Relu, scale=-G0)
             nc.scalar.activation(out=a5[:], in_=v5[:], func=ACTF.Relu, scale=-G1)
-            for h in range(2):
-                nc.scalar.activation(out=a6[:, 1 - h, :], in_=v5[:, h, :], func=ACTF.Relu, scale=G2)
-            for h in range(2):
-                nc.scalar.activation(out=a7[:, 1 - h, :], in_=v4[:, h, :], func=ACTF.Relu, scale=G3)
+            nc.scalar.activation(out=a6[:], in_=v5[:, ::-1, :], func=ACTF.Relu, scale=G2)
+            nc.scalar.activation(out=a7[:], in_=v4[:, ::-1, :], func=ACTF.Relu, scale=G3)
             if not DUP_ON_DVE:
                 nc.scalar.activation(out=bas[:, 0], in_=v4[:], func=ACTF.Relu, scale=-G0)
             st[("a", c)] = (a4, a5, a6, a7)
@@ -206,8 +204,9 @@ def tile_bsplinekanlayer_t_kernel(tc, x, coeff, base_weight, knots, out):
             if not first_half_early:
                 stt(bas[:, 1], a4[:], beta(1, 3) / G0, a5[:])
             stt(bas[:, 2], x2[:], c2, a6[:])
-            for h in range(2):
-                nc.vector.tensor_tensor(out=bas[:, 3, h, :], in0=r3[:, h, :], in1=l3[:, 1 - h, :], op=ALU.max)
+            if first_half_early:
+                s6(c - 1)
+            nc.vector.tensor_tensor(out=bas[:, 3], in0=r3[:], in1=l3[:, ::-1, :], op=ALU.max)
 
         def s4q(c, lo, hi):
             bas = st[("bas", c)]
@@ -291,8 +290,8 @@ def tile_bsplinekanlayer_t_kernel(tc, x, coeff, base_weight, knots, out):
         coeff_prep(0)
         coeff_prep(1)
         s2x(-1, 2)
-        s3(0)
         s0(3)
+        s3(0)
         for p in range(NCH):
             last = p == NCH - 1
             s2x(p + 1, p + 3)
@@ -311,7 +310,6 @@ def tile_bsplinekanlayer_t_kernel(tc, x, coeff, base_weight, knots, out):
             if last:
                 s4(p, True)
                 last_first(p)
-                s6(p - 1)
                 s4q(p, 2, 4)
                 last_second(p)
             else:

@@ -30,23 +30,25 @@ def beta(r, j):
 
 assert all(T[k] == -T[11 - k] for k in range(12))
 assert all(abs(beta(r, j) - beta(7 - r, 4 - j)) < 1e-12 for r in range(8) for j in range(5))
-SIG = beta(4, 4) ** 0.5
 G0, G1, G2, G3 = beta(0, 4), beta(1, 4), beta(2, 4), beta(3, 4)
+S8 = (2 * beta(4, 4)) ** 0.5
+SF = (2 * G2) ** 0.5
 
+OG = NO // 4
 F = 512
-NCH = 16
-DUP_ON_DVE = False
+SIZES = (1,) + (2,) * 7 + (1,)
+NCH = len(SIZES)
+START = [sum(SIZES[:c]) for c in range(NCH)]
+SLOT_A = {5: 0, 4: 1, 2: 2, 3: 3}
+SLOT_B = {7: 0, 6: 1, 0: 2, 1: 3}
+RS = (5, 4, 2, 3, 7, 6, 0, 1)
 
 
 def tile_bsplinekanlayer_t_kernel(tc, x, coeff, base_weight, knots, out):
     nc = tc.nc
     with ExitStack() as ctx:
         const = ctx.enter_context(tc.tile_pool(name="const", bufs=1))
-        w1 = ctx.enter_context(tc.tile_pool(name="w1", bufs=1))
-        w2 = ctx.enter_context(tc.tile_pool(name="w2", bufs=2))
-        w3 = ctx.enter_context(tc.tile_pool(name="w3", bufs=3))
-        w4 = ctx.enter_context(tc.tile_pool(name="w4", bufs=4))
-        w7 = ctx.enter_context(tc.tile_pool(name="w7", bufs=7))
+        wk = ctx.enter_context(tc.tile_pool(name="wk", bufs=1))
         ps_tq = ctx.enter_context(tc.psum_pool(name="ps_tq", bufs=1))
         ps_xt = ctx.enter_context(tc.psum_pool(name="ps_xt", bufs=1))
         ps_sp = ctx.enter_context(tc.psum_pool(name="ps_sp", bufs=4))
@@ -57,18 +59,25 @@ def tile_bsplinekanlayer_t_kernel(tc, x, coeff, base_weight, knots, out):
         nc.vector.memset(warm[:, 0:1], 0.0)
         nc.scalar.activation(out=warm[:, 1:2], in_=warm[:, 0:1], func=ACTF.Silu)
 
-        x_sb = const.tile([P, 64, NI], BF16)
         x_v = x.rearrange("(p n) i -> p n i", n=64)
-        for lo, hi in ((0, 4), (4, 16)):
-            nc.sync.dma_start(out=x_sb[:, lo:hi, :], in_=x_v[:, lo:hi, :])
-        c_ld = const.tile([P, 4, NO * NB], BF16)
+        out_v = out.rearrange("(p n) o -> p n o", n=64)
+        st = {}
+
+        def load(c):
+            xc = wk.tile([P, 4 * SIZES[c], NI], BF16, name="xc", bufs=5)
+            nc.sync.dma_start(out=xc[:], in_=x_v[:, 4 * START[c]:4 * (START[c] + SIZES[c]), :])
+            st["xc", c] = xc
+
+        load(0)
+        load(1)
+        load(2)
+        load(3)
+        c_ld = const.tile([P, 4, OG * NB], BF16)
         c_v = coeff.rearrange("(j t) o r -> j t (o r)", t=4)
-        for q in range(4):
-            nc.scalar.dma_start(out=c_ld[32 * q:32 * q + 32, :, :], in_=c_v)
+        for g in range(4):
+            nc.scalar.dma_start(out=c_ld[32 * g:32 * g + 32, :, :], in_=c_v[:, :, OG * NB * g:OG * NB * (g + 1)])
         bw_sb = const.tile([P, NO], BF16)
         nc.scalar.dma_start(out=bw_sb[:], in_=base_weight)
-        for lo, hi in ((16, 40), (40, 64)):
-            nc.sync.dma_start(out=x_sb[:, lo:hi, :], in_=x_v[:, lo:hi, :])
 
         ident_f = const.tile([P, P], F32)
         make_identity(nc, ident_f[:])
@@ -77,245 +86,245 @@ def tile_bsplinekanlayer_t_kernel(tc, x, coeff, base_weight, knots, out):
         c_z = const.tile([P, NB, 4, NO], U32, align_bytes=64)
         nc.gpsimd.memset(c_z[:].bitcast(F32), 0.0)
 
-        c_g = const.tile([P, NB, NO, 4], BF16, align_bytes=64)
+        c_g = const.tile([P, NB, OG, 4], BF16, align_bytes=64)
         c_p = c_ld[:].rearrange("p t (o r) -> p r o t", r=NB)
-        c_full = const.tile([P, NB * NO], U32, align_bytes=64)
+        c_q = const.tile([P, NB * OG], U32, align_bytes=64)
+        c_qs = const.tile([P, NB * OG], U8, align_bytes=64)
         c_scl = const.tile([P, NB * NO], U8, align_bytes=64)
+        nc.gpsimd.memset(c_scl[:].bitcast(I32), 0)
 
-        def coeff_prep(h):
-            nc.vector.tensor_copy(out=c_g[:, 4 * h:4 * h + 4], in_=c_p[:, 4 * h:4 * h + 4])
+        def coeff_prep():
+            nc.vector.tensor_copy(out=c_g[:], in_=c_p)
 
         def coeff_quant():
-            for h in range(2):
-                nc.vector.quantize_mx(
-                    out=c_full[:, 1024 * h:1024 * h + 1024].bitcast(FP8X4),
-                    scales=c_scl[:, 1024 * h:1024 * h + 1024],
-                    in_=c_g[:, 4 * h:4 * h + 4].rearrange("p r o t -> p (r o t)"),
-                )
+            nc.vector.quantize_mx(out=c_q[:].bitcast(FP8X4), scales=c_qs[:],
+                                  in_=c_g[:].rearrange("p r o t -> p (r o t)"))
+            codes = c_q[:].bitcast(I32).rearrange("p (r o) -> p r o", r=NB)
+            scales = c_qs[:].bitcast(I32).rearrange("p (r o) -> p r o", r=NB)
+            c_scl_w = c_scl[:].bitcast(I32).rearrange("p (r o) -> p r o", r=NB)
             for q in range(4):
-                nc.vector.tensor_copy(
-                    out=c_z[32 * q:32 * q + 32, :, q, :].bitcast(I32),
-                    in_=c_full[32 * q:32 * q + 32, :].rearrange("p (r o) -> p r o", r=NB).bitcast(I32),
-                )
+                for g in range(4):
+                    nc.sync.dma_start(out=c_z[32 * q:32 * q + 32, :, q, OG * g:OG * g + OG].bitcast(I32),
+                                      in_=codes[32 * g:32 * g + 32])
+                    nc.sync.dma_start(out=c_scl_w[32 * q:32 * q + 4, :, 16 * g:16 * g + 16],
+                                      in_=scales[32 * g:32 * g + 4])
 
-        xw = x_sb[:].rearrange("p n i -> p (n i)").bitcast(F32)
-        out_v = out.rearrange("(p n) o -> p n o", n=64)
-        st = {}
+        def stt(o, a, s, b, op0=ALU.mult, op1=ALU.add):
+            nc.vector.scalar_tensor_tensor(out=o, in0=a, scalar=s, in1=b, op0=op0, op1=op1)
 
-        def s0(c):
-            tq = ps_tq.tile([P, 2, P], F32, name="tq")
-            for u in range(2):
-                nc.tensor.transpose(tq[:, u, :], xw[:, c * 256 + u:(c + 1) * 256:2], ident_f[:])
-            xt_ps = ps_xt.tile([P, 4, P], BF16, name="xt_ps")
-            for m in range(4):
-                nc.tensor.transpose(xt_ps[:, m, :], x_sb[:, c * 4 + m, :], ident_b[:])
-            xq_raw = w3.tile([P, F], BF16, name="xq_raw")
+        def transposes(c):
+            xc = st["xc", c]
+            xw = xc[:].rearrange("p n i -> p (n i)").bitcast(F32)
+            nb = SIZES[c]
+            tq = ps_tq.tile([P, nb, 2, P], F32, name="tq")
+            for b in range(nb):
+                for u in range(2):
+                    nc.tensor.transpose(tq[:, b, u, :], xw[:, b * 256 + u:(b + 1) * 256:2], ident_f[:])
+            xt_ps = ps_xt.tile([P, 4 * nb, P], BF16, name="xt_ps")
+            for m in range(4 * nb):
+                nc.tensor.transpose(xt_ps[:, m, :], xc[:, m, :], ident_b[:])
+            st["tq", c] = tq
+            st["xt_ps", c] = xt_ps
+
+        def copies(c):
+            nb = SIZES[c]
+            xq = wk.tile([P, F * nb], BF16, name="xq", bufs=2)
             nc.scalar.copy(
-                out=xq_raw[:].bitcast(F32).rearrange("p (b u) -> p b u", u=2),
-                in_=tq[:].rearrange("p u b -> p b u"),
+                out=xq[:].bitcast(F32).rearrange("p (n b u) -> p n b u", u=2, n=nb),
+                in_=st["tq", c][:].rearrange("p n u b -> p n b u"),
             )
-            xT = w7.tile([P, 4 * P], BF16, name="xT")
-            nc.scalar.copy(out=xT[:], in_=xt_ps[:].rearrange("p m b -> p (m b)"))
-            st[("xq_raw", c)] = xq_raw
-            st[("xT", c)] = xT
+            st["xq", c] = xq
+            xT = wk.tile([P, F * nb], BF16, name="xT", bufs=5)
+            nc.scalar.copy(out=xT[:], in_=st["xt_ps", c][:].rearrange("p m b -> p (m b)"))
+            st["xT", c] = xT
 
-        def cl(c, step):
-            if step == 0:
-                xy = w4.tile([P, 2, F], BF16, name="xy")
-                nc.vector.tensor_scalar(out=xy[:, 0, :], in0=st[("xq_raw", c)][:], scalar1=T[3], scalar2=T[8],
-                                        op0=ALU.max, op1=ALU.min)
-                st[("xy", c)] = xy
-            elif step == 1:
-                xy = st[("xy", c)]
-                nc.vector.tensor_scalar(out=xy[:, 1, :], in0=xy[:, 0, :], scalar1=-1.0, scalar2=None,
-                                        op0=ALU.mult)
-            else:
-                xa = w4.tile([P, F], BF16, name="xa")
-                nc.vector.tensor_single_scalar(out=xa[:].bitcast(I32), in_=st[("xy", c)][:, 0, :].bitcast(I32),
-                                               scalar=0x7FFF7FFF, op=ALU.bitwise_and)
-                st[("xa", c)] = xa
+        def small(c):
+            f = F * SIZES[c]
+            xq = st["xq", c]
+            za = wk.tile([P, f], BF16, name="za", bufs=1)
+            z = wk.tile([P, f], BF16, name="z", bufs=3)
+            s = wk.tile([P, f], BF16, name="s", bufs=4)
+            nc.vector.tensor_single_scalar(out=za[:].bitcast(I32), in_=xq[:].bitcast(I32),
+                                           scalar=0x7FFF7FFF, op=ALU.bitwise_and)
+            nc.vector.tensor_scalar(out=s[:], in0=xq[:], scalar1=0.0, scalar2=0.5, op0=ALU.is_ge, op1=ALU.subtract)
+            nc.vector.tensor_scalar(out=z[:], in0=za[:], scalar1=T[8], scalar2=None, op0=ALU.min)
+            st["z", c] = z
+            st["s", c] = s
 
-        def s1(c):
-            for k in (4, 5):
-                sq = w4.tile([P, 2, F], F32, name="sq")
-                nc.scalar.activation(out=sq[:], in_=st[("xy", c)][:], func=ACTF.Square, bias=-T[k], scale=1.0)
-                st[("sq", c, k)] = sq
-            sqe = w2.tile([P, F], F32, name="sqe")
-            nc.scalar.activation(out=sqe[:], in_=st[("xa", c)][:], func=ACTF.Square, bias=-SIG * T[8], scale=SIG)
-            st[("sq", c, 8)] = sqe
+        def squares(c):
+            f = F * SIZES[c]
+            z = st["z", c]
+            v67 = wk.tile([P, 2, f], F32, name="v67", bufs=2)
+            v8f = wk.tile([P, 2, f], F32, name="v8f", bufs=2)
+            for o, sc, t in ((v67[:, 0], 1.0, -T[6]), (v67[:, 1], 1.0, -T[7]), (v8f[:, 0], S8, -T[8]), (v8f[:, 1], SF, T[6])):
+                nc.scalar.activation(out=o, in_=z[:], func=ACTF.Square, bias=sc * t, scale=sc)
+            st["v67", c] = v67
+            st["v8f", c] = v8f
 
-        def cube(c, step):
-            if step < 2:
-                k = 4 + step
-                v = w2.tile([P, 2, F], F32, name="V%d" % k)
-                nc.vector.scalar_tensor_tensor(out=v[:], in0=st[("xy", c)][:], scalar=T[k],
-                                               in1=st[("sq", c, k)][:], op0=ALU.subtract, op1=ALU.mult)
-                st[("V", c, k)] = v
-            else:
-                en = w2.tile([P, F], F32, name="en")
-                nc.vector.scalar_tensor_tensor(out=en[:], in0=st[("xa", c)][:], scalar=T[8],
-                                               in1=st[("sq", c, 8)][:], op0=ALU.subtract, op1=ALU.mult)
-                st[("en", c)] = en
+        def cubes_a(c):
+            for i in range(2):
+                v = st["v67", c][:, i]
+                stt(v, st["z", c][:], T[6 + i], v, ALU.subtract, ALU.mult)
 
-        def s2x(c, d):
-            for step in range(3):
-                if ok(c):
-                    cube(c, step)
-                if ok(d):
-                    cl(d, step)
+        def cubes_b(c):
+            for i, t in ((0, T[8]), (1, T[5])):
+                v = st["v8f", c][:, i]
+                stt(v, st["z", c][:], t, v, ALU.subtract, ALU.mult)
 
-        def s3(c):
-            bas = w2.tile([P, 4, 2, F], BF16, name="bas", align_bytes=64)
-            st[("bas", c)] = bas
-            v4 = st[("V", c, 4)]
-            v5 = st[("V", c, 5)]
-            a4 = w2.tile([P, 2, F], F32, name="a4")
-            a5 = w2.tile([P, 2, F], F32, name="a5")
-            a6 = w2.tile([P, 2, F], F32, name="a6")
-            a7 = w2.tile([P, 2, F], F32, name="a7")
-            nc.scalar.activation(out=a4[:], in_=v4[:], func=ACTF.Relu, scale=-G0)
-            nc.scalar.activation(out=a5[:], in_=v5[:], func=ACTF.Relu, scale=-G1)
-            nc.scalar.activation(out=a6[:], in_=v5[:, ::-1, :], func=ACTF.Relu, scale=G2)
-            nc.scalar.activation(out=a7[:], in_=v4[:, ::-1, :], func=ACTF.Relu, scale=G3)
-            if not DUP_ON_DVE:
-                nc.scalar.activation(out=bas[:, 0], in_=v4[:], func=ACTF.Relu, scale=-G0)
-            st[("a", c)] = (a4, a5, a6, a7)
+        def relus(c):
+            f = F * SIZES[c]
+            v67 = st["v67", c]
+            e = wk.tile([P, 2, f], F32, name="e", bufs=2)
+            bz = wk.tile([P, 4, f], BF16, name="bz", bufs=2)
+            b23 = wk.tile([P, 2, f], BF16, name="b23", bufs=2)
+            nc.scalar.activation(out=e[:], in_=v67[:], func=ACTF.Relu, scale=2 * G1)
+            nc.scalar.activation(out=bz[:, 0], in_=v67[:, 1], func=ACTF.Relu, scale=2 * G0)
+            nc.scalar.activation(out=b23[:, 0], in_=v67[:, 0], func=ACTF.Relu, scale=-G2)
+            st["e", c] = e
+            st["bz", c] = bz
+            st["b23", c] = b23
 
-        def stt(o, a, s, b, op1=ALU.add):
-            nc.vector.scalar_tensor_tensor(out=o, in0=a, scalar=s, in1=b, op0=ALU.mult, op1=op1)
+        def relus_h(c):
+            h = wk.tile([P, 2, F * SIZES[c]], F32, name="h", bufs=1)
+            nc.scalar.activation(out=h[:], in_=st["v67", c][:], func=ACTF.Relu, scale=-G3)
+            st["h", c] = h
 
-        def s4(c, first_half_early=False):
-            bas = st[("bas", c)]
-            a4, a5, a6, a7 = st[("a", c)]
-            en = st[("en", c)]
-            c2 = beta(2, 3) / G1
-            x2 = w1.tile([P, 2, F], F32, name="x2")
-            r3 = w1.tile([P, 2, F], BF16, name="r3")
-            l3 = w1.tile([P, 2, F], BF16, name="l3")
-            if first_half_early:
-                stt(bas[:, 1], a4[:], beta(1, 3) / G0, a5[:])
-                stt(x2[:], a4[:], (beta(2, 2) / G0) / c2, a5[:])
-                stt(r3[:], a6[:], beta(3, 3) / G2, a7[:])
-                s4q(c, 0, 2)
-            else:
-                stt(x2[:], a4[:], (beta(2, 2) / G0) / c2, a5[:])
-                stt(r3[:], a6[:], beta(3, 3) / G2, a7[:])
-            stt(l3[:], a7[:], beta(4, 3) / G3, en[:].unsqueeze(1).to_broadcast([P, 2, F]), op1=ALU.subtract)
-            if not first_half_early:
-                stt(bas[:, 1], a4[:], beta(1, 3) / G0, a5[:])
-            stt(bas[:, 2], x2[:], c2, a6[:])
-            if first_half_early:
-                s6(c - 1)
-            nc.vector.tensor_tensor(out=bas[:, 3], in0=r3[:], in1=l3[:, ::-1, :], op=ALU.max)
+        def combos(c):
+            e, h, v8f, bz, b23 = (st[k, c] for k in ("e", "h", "v8f", "bz", "b23"))
+            t1 = v8f[:, 0]
+            p1 = v8f[:, 1]
+            stt(t1, h[:, 1], 2 * beta(4, 3) / G3, t1, op1=ALU.subtract)
+            stt(b23[:, 1], h[:, 0], beta(3, 3) / G3, h[:, 1])
+            stt(bz[:, 3], h[:, 0], 2 * beta(4, 2) / G3, t1)
+            stt(p1, e[:, 0], beta(2, 3) / G1, p1)
+            stt(bz[:, 1], e[:, 1], beta(1, 3) / G1, e[:, 0])
+            stt(bz[:, 2], e[:, 1], beta(2, 2) / G1, p1)
 
-        def s4q(c, lo, hi):
-            bas = st[("bas", c)]
-            if lo == 0:
-                st[("cod", c)] = w2.tile([P, NB * F // 4], U32, name="cod", align_bytes=64)
-                st[("scl", c)] = w2.tile([P, NB * F // 4], U8, name="scl", align_bytes=64)
-            w = 2 * F // 4
-            nc.vector.quantize_mx(out=st[("cod", c)][:, lo * w:hi * w].bitcast(FP8X4),
-                                  scales=st[("scl", c)][:, lo * w:hi * w],
-                                  in_=bas[:, lo:hi].rearrange("p m h f -> p (m h f)"))
+        def signs(c):
+            f = F * SIZES[c]
+            bo = wk.tile([P, 6, f], BF16, name="bo", bufs=1)
+            nc.vector.tensor_tensor(out=bo[:, 0:4], in0=st["bz", c][:],
+                                    in1=st["s", c][:].unsqueeze(1).to_broadcast([P, 4, f]), op=ALU.mult)
+            st["bo", c] = bo
 
-        def s5a(c):
-            xT = st[("xT", c)]
-            for h in range(2):
-                pb = ps_pb.tile([P, 2, NO], F32, name="pb")
-                for qq in range(2):
-                    q = 2 * h + qq
-                    nc.tensor.matmul(out=pb[:, qq, :], lhsT=xT[:, q * P:(q + 1) * P],
-                                     rhs=bw_sb[:], start=True, stop=True)
-                sil = w4.tile([P, 2 * NO], F32, name="sil")
-                nc.scalar.activation(out=sil[:], in_=pb[:].rearrange("p a o -> p (a o)"), func=ACTF.Silu)
-                st[("sil", c, h)] = sil
+        def mirror(c):
+            f = F * SIZES[c]
+            bo = st["bo", c]
+            nc.scalar.activation(out=bo[:, 4:6], in_=bo[:, 2:4], func=ACTF.Copy, scale=-1.0)
+            bas_b = wk.tile([P, 4, f], BF16, name="bas_b", bufs=1, align_bytes=64)
+            nc.scalar.activation(out=bas_b[:, 0:2], in_=bo[:, 0:2], func=ACTF.Relu)
+            nc.scalar.activation(out=bas_b[:, 2:4], in_=bo[:, 0:2], func=ACTF.Relu, scale=-1.0)
+            st["bas_b", c] = bas_b
 
-        def mx(c, acc, q, r, start, stop):
-            slot = 2 * r if r < 4 else 2 * (7 - r) + 1
-            lo = slot * (F // 4)
-            nc.tensor.matmul_mx(
-                out=acc,
-                lhsT=st[("cod", c)][:, lo:lo + P].bitcast(FP8X4),
-                lhsT_scale=st[("scl", c)][:, lo:lo + P],
-                rhs=c_z[:, r, q, :].bitcast(FP8X4),
-                rhs_scale=c_scl[:, r * NO:(r + 1) * NO],
-                start=start,
-                stop=stop,
-            )
+        def maxima(c):
+            f = F * SIZES[c]
+            bas_a = wk.tile([P, 4, f], BF16, name="bas_a", bufs=1, align_bytes=64)
+            nc.vector.tensor_tensor(
+                out=bas_a[:].rearrange("p (h m) f -> p h (m f)", h=2),
+                in0=st["b23", c][:].rearrange("p m f -> p (m f)").unsqueeze(1).to_broadcast([P, 2, 2 * f]),
+                in1=st["bo", c][:, 2:6].rearrange("p (h m) f -> p h (m f)", h=2), op=ALU.max)
+            st["bas_a", c] = bas_a
 
-        def s5b(c):
-            for h in range(2):
-                sp = ps_sp.tile([P, 2, NO], F32, name="sp")
-                for qq in range(2):
-                    for r in range(NB):
-                        mx(c, sp[:, qq, :], 2 * h + qq, r, r == 0, r == NB - 1)
-                st[("sp", c, h)] = sp
+        def quant(c, ab):
+            f = F * SIZES[c]
+            cod = wk.tile([P, f], U32, name="cod_" + ab, bufs=1, align_bytes=64)
+            scl = wk.tile([P, f], U8, name="scl_" + ab, bufs=1, align_bytes=64)
+            nc.vector.quantize_mx(out=cod[:].bitcast(FP8X4), scales=scl[:],
+                                  in_=st["bas_" + ab, c][:].rearrange("p m f -> p (m f)"))
+            st["cod_" + ab, c] = cod
+            st["scl_" + ab, c] = scl
 
-        def s6(c):
-            o_sb = w3.tile([P, 4, NO], F32, name="o_sb")
-            for h in range(2):
-                nc.vector.tensor_tensor(out=o_sb[:, 2 * h:2 * h + 2, :].rearrange("p a o -> p (a o)"),
-                                        in0=st[("sp", c, h)][:].rearrange("p a o -> p (a o)"),
-                                        in1=st[("sil", c, h)][:], op=ALU.add)
-            nc.sync.dma_start(out=out_v[:, 4 * c:4 * c + 4, :], in_=o_sb[:])
+        def base(c):
+            xT = st["xT", c]
+            for b in range(SIZES[c]):
+                for h in range(2):
+                    pb = ps_pb.tile([P, 2, NO], F32, name="pb")
+                    for qq in range(2):
+                        q = 4 * b + 2 * h + qq
+                        nc.tensor.matmul(out=pb[:, qq, :], lhsT=xT[:, q * P:(q + 1) * P],
+                                         rhs=bw_sb[:], start=True, stop=True)
+                    sil = wk.tile([P, 2 * NO], F32, name="sil", bufs=4)
+                    nc.scalar.activation(out=sil[:], in_=pb[:].rearrange("p a o -> p (a o)"), func=ACTF.Silu)
+                    st["sil", START[c] + b, h] = sil
 
-        def last_first(c):
-            for q in range(4):
-                sp = ps_sp.tile([P, 2, NO], F32, name="sp")
-                st[("spq", q)] = sp
-                for i, r in enumerate((0, 7, 1, 6)):
-                    mx(c, sp[:, 0, :], q, r, i == 0, False)
+        def spline(c):
+            for b in range(SIZES[c]):
+                for h in range(2):
+                    sp = ps_sp.tile([P, 2, NO], F32, name="sp")
+                    for qq in range(2):
+                        for r in RS:
+                            ab, slot = ("a", SLOT_A[r]) if r in SLOT_A else ("b", SLOT_B[r])
+                            lo = slot * (F * SIZES[c] // 4) + b * P
+                            nc.tensor.matmul_mx(
+                                out=sp[:, qq, :],
+                                lhsT=st["cod_" + ab, c][:, lo:lo + P].bitcast(FP8X4),
+                                lhsT_scale=st["scl_" + ab, c][:, lo:lo + P],
+                                rhs=c_z[:, r, 2 * h + qq, :].bitcast(FP8X4),
+                                rhs_scale=c_scl[:, r * NO:(r + 1) * NO],
+                                start=r == RS[0],
+                                stop=r == RS[-1],
+                            )
+                    st["sp", START[c] + b, h] = sp
 
-        def last_second(c):
-            o_sb = w3.tile([P, 4, NO], F32, name="o_sb")
-            for q in range(4):
-                for i, r in enumerate((2, 5, 3, 4)):
-                    mx(c, st[("spq", q)][:, 0, :], q, r, False, i == 3)
-            for q in range(4):
-                nc.vector.tensor_tensor(out=o_sb[:, q, :], in0=st[("spq", q)][:, 0, :],
-                                        in1=st[("sil", c, q // 2)][:, (q % 2) * NO:(q % 2 + 1) * NO], op=ALU.add)
-                if q % 2 == 1:
-                    nc.sync.dma_start(out=out_v[:, 4 * c + q - 1:4 * c + q + 1, :], in_=o_sb[:, q - 1:q + 1, :])
+        def adds(c):
+            for b in range(START[c], START[c] + SIZES[c]):
+                o_sb = wk.tile([P, 4, NO], F32, name="o_sb", bufs=2)
+                for h in range(2):
+                    nc.vector.tensor_tensor(out=o_sb[:, 2 * h:2 * h + 2, :].rearrange("p a o -> p (a o)"),
+                                            in0=st["sp", b, h][:].rearrange("p a o -> p (a o)"),
+                                            in1=st["sil", b, h][:], op=ALU.add)
+                nc.sync.dma_start(out=out_v[:, 4 * b:4 * b + 4, :], in_=o_sb[:])
 
         def ok(c):
             return 0 <= c < NCH
 
-        s0(0)
-        s2x(-1, 0)
-        s1(0)
-        s0(1)
-        s2x(0, 1)
-        s1(1)
-        s0(2)
-        coeff_prep(0)
-        coeff_prep(1)
-        s2x(-1, 2)
-        s0(3)
-        s3(0)
-        for p in range(NCH):
-            last = p == NCH - 1
-            s2x(p + 1, p + 3)
-            if ok(p + 2):
-                s1(p + 2)
-            if ok(p - 1):
-                s5a(p - 1)
-            if last:
-                s5a(p)
-            if ok(p + 1):
-                s3(p + 1)
+        transposes(0)
+        copies(0)
+        small(0)
+        transposes(1)
+        squares(0)
+        copies(1)
+        cubes_a(0)
+        cubes_b(0)
+        relus(0)
+        small(1)
+        transposes(2)
+        coeff_prep()
+        relus_h(0)
+        squares(1)
+        coeff_quant()
+        copies(2)
+        small(2)
+        for p in range(NCH + 1):
             if ok(p + 4):
-                s0(p + 4)
+                load(p + 4)
+            if ok(p + 3):
+                transposes(p + 3)
+            if ok(p + 1):
+                cubes_a(p + 1)
             if ok(p - 1):
-                s5b(p - 1)
-            if last:
-                s4(p, True)
-                last_first(p)
-                s4q(p, 2, 4)
-                last_second(p)
-            else:
-                s4(p)
-                if ok(p - 1):
-                    s6(p - 1)
-                if p == 0:
-                    coeff_quant()
-                s4q(p, 0, 4)
+                quant(p - 1, "a")
+            if ok(p + 1):
+                cubes_b(p + 1)
+                relus(p + 1)
+            if ok(p - 1):
+                quant(p - 1, "b")
+                spline(p - 1)
+            if ok(p + 3):
+                copies(p + 3)
+            if ok(p):
+                combos(p)
+            if ok(p + 2):
+                squares(p + 2)
+            if ok(p + 1):
+                relus_h(p + 1)
+            if ok(p + 3):
+                small(p + 3)
+            if ok(p):
+                signs(p)
+                mirror(p)
+            if ok(p - 1):
+                adds(p - 1)
+            if ok(p):
+                base(p)
+                maxima(p)

@@ -174,20 +174,18 @@ def tile_bsplinekanlayer_t_kernel(tc, x, coeff, base_weight, knots, out):
         def relus(c):
             f = F * SIZES[c]
             v67 = st["v67", c]
-            e = wk.tile([P, 2, f], F32, name="e", bufs=2)
-            bz = wk.tile([P, 4, f], BF16, name="bz", bufs=2)
+            h = wk.tile([P, 2, f], F32, name="h", bufs=1)
+            e = wk.tile([P, 2, f], F32, name="e", bufs=1)
+            bz = wk.tile([P, 4, f], BF16, name="bz", bufs=1)
             b23 = wk.tile([P, 2, f], BF16, name="b23", bufs=2)
+            nc.scalar.activation(out=h[:], in_=v67[:], func=ACTF.Relu, scale=-G3)
             nc.scalar.activation(out=e[:], in_=v67[:], func=ACTF.Relu, scale=2 * G1)
             nc.scalar.activation(out=bz[:, 0], in_=v67[:, 1], func=ACTF.Relu, scale=2 * G0)
             nc.scalar.activation(out=b23[:, 0], in_=v67[:, 0], func=ACTF.Relu, scale=-G2)
+            st["h", c] = h
             st["e", c] = e
             st["bz", c] = bz
             st["b23", c] = b23
-
-        def relus_h(c):
-            h = wk.tile([P, 2, F * SIZES[c]], F32, name="h", bufs=1)
-            nc.scalar.activation(out=h[:], in_=st["v67", c][:], func=ACTF.Relu, scale=-G3)
-            st["h", c] = h
 
         def combos(c):
             e, h, v8f, bz, b23 = (st[k, c] for k in ("e", "h", "v8f", "bz", "b23"))
@@ -212,8 +210,13 @@ def tile_bsplinekanlayer_t_kernel(tc, x, coeff, base_weight, knots, out):
             bo = st["bo", c]
             nc.scalar.activation(out=bo[:, 4:6], in_=bo[:, 2:4], func=ACTF.Copy, scale=-1.0)
             bas_b = wk.tile([P, 4, f], BF16, name="bas_b", bufs=1, align_bytes=64)
-            nc.scalar.activation(out=bas_b[:, 0:2], in_=bo[:, 0:2], func=ACTF.Relu)
-            nc.scalar.activation(out=bas_b[:, 2:4], in_=bo[:, 0:2], func=ACTF.Relu, scale=-1.0)
+            if c < NCH - 1:
+                nc.scalar.activation(out=bas_b[:, 0:2], in_=bo[:, 0:2], func=ACTF.Relu)
+                nc.scalar.activation(out=bas_b[:, 2:4], in_=bo[:, 0:2], func=ACTF.Relu, scale=-1.0)
+            else:
+                nc.vector.tensor_scalar(out=bas_b[:, 0:2], in0=bo[:, 0:2], scalar1=0.0, scalar2=None, op0=ALU.max)
+                nc.vector.tensor_scalar(out=bas_b[:, 2:4], in0=bo[:, 0:2], scalar1=-1.0, scalar2=0.0,
+                                        op0=ALU.mult, op1=ALU.max)
             st["bas_b", c] = bas_b
 
         def maxima(c):
@@ -227,28 +230,28 @@ def tile_bsplinekanlayer_t_kernel(tc, x, coeff, base_weight, knots, out):
 
         def quant(c, ab):
             f = F * SIZES[c]
-            cod = wk.tile([P, f], U32, name="cod_" + ab, bufs=1, align_bytes=64)
-            scl = wk.tile([P, f], U8, name="scl_" + ab, bufs=1, align_bytes=64)
+            cod = wk.tile([P, f], U32, name="cod_" + ab, bufs=2, align_bytes=64)
+            scl = wk.tile([P, f], U8, name="scl_" + ab, bufs=2, align_bytes=64)
             nc.vector.quantize_mx(out=cod[:].bitcast(FP8X4), scales=scl[:],
                                   in_=st["bas_" + ab, c][:].rearrange("p m f -> p (m f)"))
             st["cod_" + ab, c] = cod
             st["scl_" + ab, c] = scl
 
-        def base(c):
+        def base(c, b):
             xT = st["xT", c]
-            for b in range(SIZES[c]):
+            if b < SIZES[c]:
                 for h in range(2):
                     pb = ps_pb.tile([P, 2, NO], F32, name="pb")
                     for qq in range(2):
                         q = 4 * b + 2 * h + qq
                         nc.tensor.matmul(out=pb[:, qq, :], lhsT=xT[:, q * P:(q + 1) * P],
                                          rhs=bw_sb[:], start=True, stop=True)
-                    sil = wk.tile([P, 2 * NO], F32, name="sil", bufs=4)
+                    sil = wk.tile([P, 2 * NO], F32, name="sil", bufs=8)
                     nc.scalar.activation(out=sil[:], in_=pb[:].rearrange("p a o -> p (a o)"), func=ACTF.Silu)
                     st["sil", START[c] + b, h] = sil
 
-        def spline(c):
-            for b in range(SIZES[c]):
+        def spline(c, b):
+            if b < SIZES[c]:
                 for h in range(2):
                     sp = ps_sp.tile([P, 2, NO], F32, name="sp")
                     for qq in range(2):
@@ -290,41 +293,44 @@ def tile_bsplinekanlayer_t_kernel(tc, x, coeff, base_weight, knots, out):
         small(1)
         transposes(2)
         coeff_prep()
-        relus_h(0)
         squares(1)
         coeff_quant()
         copies(2)
-        small(2)
-        for p in range(NCH + 1):
+        base(0, 0)
+        base(0, 1)
+        for p in range(NCH):
+            last = p == NCH - 1
             if ok(p + 4):
                 load(p + 4)
-            if ok(p + 3):
-                transposes(p + 3)
+            combos(p)
+            if ok(p + 2):
+                small(p + 2)
+            signs(p)
+            mirror(p)
             if ok(p + 1):
                 cubes_a(p + 1)
-            if ok(p - 1):
-                quant(p - 1, "a")
-            if ok(p + 1):
                 cubes_b(p + 1)
+            if ok(p - 1) and not last:
+                adds(p - 1)
+            if last:
+                quant(p, "b")
+            maxima(p)
+            if ok(p + 1):
                 relus(p + 1)
-            if ok(p - 1):
-                quant(p - 1, "b")
-                spline(p - 1)
+            if not last:
+                quant(p, "b")
+            quant(p, "a")
+            if last:
+                adds(p - 1)
             if ok(p + 3):
+                transposes(p + 3)
                 copies(p + 3)
-            if ok(p):
-                combos(p)
+            if not last:
+                base(p + 1, 0)
+            spline(p, 0)
             if ok(p + 2):
                 squares(p + 2)
-            if ok(p + 1):
-                relus_h(p + 1)
-            if ok(p + 3):
-                small(p + 3)
-            if ok(p):
-                signs(p)
-                mirror(p)
-            if ok(p - 1):
-                adds(p - 1)
-            if ok(p):
-                base(p)
-                maxima(p)
+            if not last:
+                base(p + 1, 1)
+            spline(p, 1)
+        adds(NCH - 1)

@@ -31,7 +31,7 @@ def beta(r, j):
 assert all(T[k] == -T[11 - k] for k in range(12))
 assert all(abs(beta(r, j) - beta(7 - r, 4 - j)) < 1e-12 for r in range(8) for j in range(5))
 G0, G1, G2, G3 = beta(0, 4), beta(1, 4), beta(2, 4), beta(3, 4)
-S8 = (2 * beta(4, 4)) ** 0.5
+S8 = (beta(4, 4) * G3 / -beta(4, 3)) ** 0.5
 SF = (2 * G2) ** 0.5
 
 OG = NO // 4
@@ -178,7 +178,8 @@ def tile_bsplinekanlayer_t_kernel(tc, x, coeff, base_weight, knots, out):
             e = wk.tile([P, 2, f], F32, name="e", bufs=1)
             bz = wk.tile([P, 4, f], BF16, name="bz", bufs=1)
             b23 = wk.tile([P, 2, f], BF16, name="b23", bufs=2)
-            nc.scalar.activation(out=h[:], in_=v67[:], func=ACTF.Relu, scale=-G3)
+            nc.scalar.activation(out=h[:, 1], in_=v67[:, 1], func=ACTF.Relu, scale=-G3)
+            nc.scalar.activation(out=h[:, 0], in_=v67[:, 0], func=ACTF.Relu, scale=-2 * beta(4, 2))
             nc.scalar.activation(out=e[:], in_=v67[:], func=ACTF.Relu, scale=2 * G1)
             nc.scalar.activation(out=bz[:, 0], in_=v67[:, 1], func=ACTF.Relu, scale=2 * G0)
             nc.scalar.activation(out=b23[:, 0], in_=v67[:, 0], func=ACTF.Relu, scale=-G2)
@@ -187,15 +188,18 @@ def tile_bsplinekanlayer_t_kernel(tc, x, coeff, base_weight, knots, out):
             st["bz", c] = bz
             st["b23", c] = b23
 
+        def first_sum(c, eng):
+            t1 = wk.tile([P, F * SIZES[c]], F32, name="bas_a", bufs=1, align_bytes=64)
+            eng.tensor_tensor(out=t1[:], in0=st["h", c][:, 1], in1=st["v8f", c][:, 0], op=ALU.add)
+            st["t1", c] = t1
+
         def combos(c):
-            e, h, v8f, bz, b23 = (st[k, c] for k in ("e", "h", "v8f", "bz", "b23"))
-            t1 = v8f[:, 0]
+            e, h, v8f, bz, b23, t1 = (st[k, c] for k in ("e", "h", "v8f", "bz", "b23", "t1"))
             p1 = v8f[:, 1]
-            stt(t1, h[:, 1], 2 * beta(4, 3) / G3, t1, op1=ALU.subtract)
-            stt(b23[:, 1], h[:, 0], beta(3, 3) / G3, h[:, 1])
-            stt(bz[:, 3], h[:, 0], 2 * beta(4, 2) / G3, t1)
+            stt(b23[:, 1], h[:, 0], beta(3, 3) / (2 * beta(4, 2)), h[:, 1])
             stt(p1, e[:, 0], beta(2, 3) / G1, p1)
             stt(bz[:, 1], e[:, 1], beta(1, 3) / G1, e[:, 0])
+            stt(bz[:, 3], t1[:], 2 * beta(4, 3) / G3, h[:, 0])
             stt(bz[:, 2], e[:, 1], beta(2, 2) / G1, p1)
 
         def signs(c):
@@ -271,7 +275,7 @@ def tile_bsplinekanlayer_t_kernel(tc, x, coeff, base_weight, knots, out):
 
         def adds(c):
             for b in range(START[c], START[c] + SIZES[c]):
-                o_sb = wk.tile([P, 4, NO], F32, name="o_sb", bufs=2)
+                o_sb = wk.tile([P, 4, NO], F32, name="o_sb", bufs=3)
                 for h in range(2):
                     nc.vector.tensor_tensor(out=o_sb[:, 2 * h:2 * h + 2, :].rearrange("p a o -> p (a o)"),
                                             in0=st["sp", b, h][:].rearrange("p a o -> p (a o)"),
@@ -292,12 +296,13 @@ def tile_bsplinekanlayer_t_kernel(tc, x, coeff, base_weight, knots, out):
         relus(0)
         small(1)
         transposes(2)
+        copies(2)
         coeff_prep()
         squares(1)
         coeff_quant()
-        copies(2)
         base(0, 0)
         base(0, 1)
+        first_sum(0, nc.vector)
         for p in range(NCH):
             last = p == NCH - 1
             if ok(p + 4):
@@ -310,8 +315,6 @@ def tile_bsplinekanlayer_t_kernel(tc, x, coeff, base_weight, knots, out):
             if ok(p + 1):
                 cubes_a(p + 1)
                 cubes_b(p + 1)
-            if ok(p - 1) and not last:
-                adds(p - 1)
             if last:
                 quant(p, "b")
             maxima(p)
@@ -320,7 +323,9 @@ def tile_bsplinekanlayer_t_kernel(tc, x, coeff, base_weight, knots, out):
             if not last:
                 quant(p, "b")
             quant(p, "a")
-            if last:
+            if ok(p + 1):
+                first_sum(p + 1, nc.gpsimd)
+            if ok(p - 1):
                 adds(p - 1)
             if ok(p + 3):
                 transposes(p + 3)

@@ -49,8 +49,8 @@ def tile_bsplinekanlayer_t_kernel(tc, x, coeff, base_weight, knots, out):
     with ExitStack() as ctx:
         const = ctx.enter_context(tc.tile_pool(name="const", bufs=1))
         wk = ctx.enter_context(tc.tile_pool(name="wk", bufs=1))
-        ps_tq = ctx.enter_context(tc.psum_pool(name="ps_tq", bufs=1))
-        ps_xt = ctx.enter_context(tc.psum_pool(name="ps_xt", bufs=1))
+        ps_z = ctx.enter_context(tc.psum_pool(name="ps_z", bufs=1))
+        ps_tr = ctx.enter_context(tc.psum_pool(name="ps_tr", bufs=1))
         ps_sp = ctx.enter_context(tc.psum_pool(name="ps_sp", bufs=4))
         ps_pb = ctx.enter_context(tc.psum_pool(name="ps_pb", bufs=2))
         ctx.enter_context(tc.manual_schedule())
@@ -112,44 +112,41 @@ def tile_bsplinekanlayer_t_kernel(tc, x, coeff, base_weight, knots, out):
         def stt(o, a, s, b, op0=ALU.mult, op1=ALU.add):
             nc.vector.scalar_tensor_tensor(out=o, in0=a, scalar=s, in1=b, op0=op0, op1=op1)
 
-        def transposes(c):
-            xc = st["xc", c]
-            xw = xc[:].rearrange("p n i -> p (n i)").bitcast(F32)
-            nb = SIZES[c]
-            tq = ps_tq.tile([P, nb, 2, P], F32, name="tq")
-            for b in range(nb):
-                for u in range(2):
-                    nc.tensor.transpose(tq[:, b, u, :], xw[:, b * 256 + u:(b + 1) * 256:2], ident_f[:])
-            xt_ps = ps_xt.tile([P, 4 * nb, P], BF16, name="xt_ps")
-            for m in range(4 * nb):
-                nc.tensor.transpose(xt_ps[:, m, :], xc[:, m, :], ident_b[:])
-            st["tq", c] = tq
-            st["xt_ps", c] = xt_ps
-
-        def copies(c):
-            nb = SIZES[c]
-            xq = wk.tile([P, F * nb], BF16, name="xq", bufs=2)
-            nc.scalar.copy(
-                out=xq[:].bitcast(F32).rearrange("p (n b u) -> p n b u", u=2, n=nb),
-                in_=st["tq", c][:].rearrange("p n u b -> p n b u"),
-            )
-            st["xq", c] = xq
-            xT = wk.tile([P, F * nb], BF16, name="xT", bufs=5)
-            nc.scalar.copy(out=xT[:], in_=st["xt_ps", c][:].rearrange("p m b -> p (m b)"))
-            st["xT", c] = xT
-
         def small(c):
             f = F * SIZES[c]
-            xq = st["xq", c]
+            xf = st["xc", c][:].rearrange("p n i -> p (n i)")
             za = wk.tile([P, f], BF16, name="za", bufs=1)
-            z = wk.tile([P, f], BF16, name="z", bufs=3)
-            s = wk.tile([P, f], BF16, name="s", bufs=4)
-            nc.vector.tensor_single_scalar(out=za[:].bitcast(I32), in_=xq[:].bitcast(I32),
+            zt = wk.tile([P, f], BF16, name="zt", bufs=2)
+            sg = wk.tile([P, f], BF16, name="sg", bufs=3)
+            nc.vector.tensor_single_scalar(out=za[:].bitcast(I32), in_=xf.bitcast(I32),
                                            scalar=0x7FFF7FFF, op=ALU.bitwise_and)
-            nc.vector.tensor_scalar(out=s[:], in0=xq[:], scalar1=0.0, scalar2=0.5, op0=ALU.is_ge, op1=ALU.subtract)
-            nc.vector.tensor_scalar(out=z[:], in0=za[:], scalar1=T[8], scalar2=None, op0=ALU.min)
-            st["z", c] = z
-            st["s", c] = s
+            nc.vector.tensor_scalar(out=sg[:], in0=xf, scalar1=0.0, scalar2=0.5, op0=ALU.is_ge, op1=ALU.subtract)
+            nc.vector.tensor_scalar(out=zt[:], in0=za[:], scalar1=T[8], scalar2=None, op0=ALU.min)
+            st["zt", c] = zt
+            st["sg", c] = sg
+
+        def turn(c, src, pool, tag):
+            w = src[:].bitcast(F32)
+            tq = pool.tile([P, SIZES[c], P, 2], F32, name=tag)
+            for b in range(SIZES[c]):
+                for u in range(2):
+                    nc.tensor.transpose(tq[:, b, :, u], w[:, b * 256 + u:(b + 1) * 256:2], ident_f[:])
+            return tq[:].rearrange("p n b u -> p (n b u)").bitcast(BF16)
+
+        def turn_z(c):
+            st["z", c] = turn(c, st["zt", c], ps_z, "z")
+
+        def turn_s(c):
+            st["s", c] = turn(c, st["sg", c], ps_tr, "tr")
+
+        def turn_x(c):
+            nb = SIZES[c]
+            xt_ps = ps_tr.tile([P, 4 * nb, P], BF16, name="tr")
+            for m in range(4 * nb):
+                nc.tensor.transpose(xt_ps[:, m, :], st["xc", c][:, m, :], ident_b[:])
+            xT = wk.tile([P, F * nb], BF16, name="xT", bufs=4)
+            nc.scalar.copy(out=xT[:], in_=xt_ps[:].rearrange("p m b -> p (m b)"))
+            st["xT", c] = xT
 
         def squares(c):
             f = F * SIZES[c]
@@ -157,19 +154,19 @@ def tile_bsplinekanlayer_t_kernel(tc, x, coeff, base_weight, knots, out):
             v67 = wk.tile([P, 2, f], F32, name="v67", bufs=2)
             v8f = wk.tile([P, 2, f], F32, name="v8f", bufs=2)
             for o, sc, t in ((v67[:, 0], 1.0, -T[6]), (v67[:, 1], 1.0, -T[7]), (v8f[:, 0], S8, -T[8]), (v8f[:, 1], SF, T[6])):
-                nc.scalar.activation(out=o, in_=z[:], func=ACTF.Square, bias=sc * t, scale=sc)
+                nc.scalar.activation(out=o, in_=z, func=ACTF.Square, bias=sc * t, scale=sc)
             st["v67", c] = v67
             st["v8f", c] = v8f
 
         def cubes_a(c):
             for i in range(2):
                 v = st["v67", c][:, i]
-                stt(v, st["z", c][:], T[6 + i], v, ALU.subtract, ALU.mult)
+                stt(v, st["z", c], T[6 + i], v, ALU.subtract, ALU.mult)
 
         def cubes_b(c):
             for i, t in ((0, T[8]), (1, T[5])):
                 v = st["v8f", c][:, i]
-                stt(v, st["z", c][:], t, v, ALU.subtract, ALU.mult)
+                stt(v, st["z", c], t, v, ALU.subtract, ALU.mult)
 
         def relus(c):
             f = F * SIZES[c]
@@ -206,21 +203,22 @@ def tile_bsplinekanlayer_t_kernel(tc, x, coeff, base_weight, knots, out):
             f = F * SIZES[c]
             bo = wk.tile([P, 6, f], BF16, name="bo", bufs=1)
             nc.vector.tensor_tensor(out=bo[:, 0:4], in0=st["bz", c][:],
-                                    in1=st["s", c][:].unsqueeze(1).to_broadcast([P, 4, f]), op=ALU.mult)
+                                    in1=st["s", c].unsqueeze(1).to_broadcast([P, 4, f]), op=ALU.mult)
             st["bo", c] = bo
 
-        def mirror(c):
+        def mirror(c, part):
             f = F * SIZES[c]
             bo = st["bo", c]
-            nc.scalar.activation(out=bo[:, 4:6], in_=bo[:, 2:4], func=ACTF.Copy, scale=-1.0)
+            if part == 0:
+                nc.scalar.activation(out=bo[:, 4:6], in_=bo[:, 2:4], func=ACTF.Copy, scale=-1.0)
+                return
             bas_b = wk.tile([P, 4, f], BF16, name="bas_b", bufs=1, align_bytes=64)
             if c < NCH - 1:
                 nc.scalar.activation(out=bas_b[:, 0:2], in_=bo[:, 0:2], func=ACTF.Relu)
-                nc.scalar.activation(out=bas_b[:, 2:4], in_=bo[:, 0:2], func=ACTF.Relu, scale=-1.0)
             else:
                 nc.vector.tensor_scalar(out=bas_b[:, 0:2], in0=bo[:, 0:2], scalar1=0.0, scalar2=None, op0=ALU.max)
-                nc.vector.tensor_scalar(out=bas_b[:, 2:4], in0=bo[:, 0:2], scalar1=-1.0, scalar2=0.0,
-                                        op0=ALU.mult, op1=ALU.max)
+            nc.vector.tensor_scalar(out=bas_b[:, 2:4], in0=bo[:, 0:2], scalar1=-1.0, scalar2=0.0,
+                                    op0=ALU.mult, op1=ALU.max)
             st["bas_b", c] = bas_b
 
         def maxima(c):
@@ -285,23 +283,19 @@ def tile_bsplinekanlayer_t_kernel(tc, x, coeff, base_weight, knots, out):
         def ok(c):
             return 0 <= c < NCH
 
-        transposes(0)
-        copies(0)
         small(0)
-        transposes(1)
+        turn_z(0)
+        turn_x(0)
         squares(0)
-        copies(1)
         cubes_a(0)
         cubes_b(0)
-        relus(0)
         small(1)
-        transposes(2)
-        copies(2)
+        turn_z(1)
+        turn_s(0)
+        relus(0)
         coeff_prep()
         squares(1)
         coeff_quant()
-        base(0, 0)
-        base(0, 1)
         first_sum(0, nc.vector)
         for p in range(NCH):
             last = p == NCH - 1
@@ -311,10 +305,14 @@ def tile_bsplinekanlayer_t_kernel(tc, x, coeff, base_weight, knots, out):
             if ok(p + 2):
                 small(p + 2)
             signs(p)
-            mirror(p)
+            mirror(p, 0)
+            if ok(p + 1):
+                turn_x(p + 1)
+                turn_s(p + 1)
             if ok(p + 1):
                 cubes_a(p + 1)
                 cubes_b(p + 1)
+            mirror(p, 1)
             if last:
                 quant(p, "b")
             maxima(p)
@@ -327,9 +325,11 @@ def tile_bsplinekanlayer_t_kernel(tc, x, coeff, base_weight, knots, out):
                 first_sum(p + 1, nc.gpsimd)
             if ok(p - 1):
                 adds(p - 1)
-            if ok(p + 3):
-                transposes(p + 3)
-                copies(p + 3)
+            if ok(p + 2):
+                turn_z(p + 2)
+            if p == 0:
+                base(p, 0)
+                base(p, 1)
             if not last:
                 base(p + 1, 0)
             spline(p, 0)

@@ -32,16 +32,18 @@ assert all(T[k] == -T[11 - k] for k in range(12))
 assert all(abs(beta(r, j) - beta(7 - r, 4 - j)) < 1e-12 for r in range(8) for j in range(5))
 G0, G1, G2, G3 = beta(0, 4), beta(1, 4), beta(2, 4), beta(3, 4)
 S8 = (beta(4, 4) * G3 / -beta(4, 3)) ** 0.5
-SF = (2 * G2) ** 0.5
+SF = (2 * G2 * G1 / -beta(2, 3)) ** 0.5
 
 OG = NO // 4
 F = 512
 SIZES = (1,) + (2,) * 7 + (1,)
 NCH = len(SIZES)
+OUTS_ACT = 0
+FILL = 2
 START = [sum(SIZES[:c]) for c in range(NCH)]
-SLOT_A = {5: 0, 4: 1, 2: 2, 3: 3}
+SLOT_A = {4: 0, 5: 1, 3: 2, 2: 3}
 SLOT_B = {7: 0, 6: 1, 0: 2, 1: 3}
-RS = (5, 4, 2, 3, 7, 6, 0, 1)
+RS = (4, 5, 3, 2, 7, 6, 0, 1)
 
 
 def tile_bsplinekanlayer_t_kernel(tc, x, coeff, base_weight, knots, out):
@@ -117,7 +119,7 @@ def tile_bsplinekanlayer_t_kernel(tc, x, coeff, base_weight, knots, out):
             xf = st["xc", c][:].rearrange("p n i -> p (n i)")
             za = wk.tile([P, f], BF16, name="za", bufs=1)
             zt = wk.tile([P, f], BF16, name="zt", bufs=2)
-            sg = wk.tile([P, f], BF16, name="sg", bufs=3)
+            sg = wk.tile([P, f], BF16, name="sg", bufs=4)
             nc.vector.tensor_single_scalar(out=za[:].bitcast(I32), in_=xf.bitcast(I32),
                                            scalar=0x7FFF7FFF, op=ALU.bitwise_and)
             nc.vector.tensor_scalar(out=sg[:], in0=xf, scalar1=0.0, scalar2=0.5, op0=ALU.is_ge, op1=ALU.subtract)
@@ -144,7 +146,7 @@ def tile_bsplinekanlayer_t_kernel(tc, x, coeff, base_weight, knots, out):
             xt_ps = ps_tr.tile([P, 4 * nb, P], BF16, name="tr")
             for m in range(4 * nb):
                 nc.tensor.transpose(xt_ps[:, m, :], st["xc", c][:, m, :], ident_b[:])
-            xT = wk.tile([P, F * nb], BF16, name="xT", bufs=4)
+            xT = wk.tile([P, F * nb], BF16, name="xT", bufs=2)
             nc.scalar.copy(out=xT[:], in_=xt_ps[:].rearrange("p m b -> p (m b)"))
             st["xT", c] = xT
 
@@ -158,65 +160,78 @@ def tile_bsplinekanlayer_t_kernel(tc, x, coeff, base_weight, knots, out):
             st["v67", c] = v67
             st["v8f", c] = v8f
 
-        def cubes_a(c):
-            for i in range(2):
-                v = st["v67", c][:, i]
-                stt(v, st["z", c], T[6 + i], v, ALU.subtract, ALU.mult)
-
-        def cubes_b(c):
-            for i, t in ((0, T[8]), (1, T[5])):
-                v = st["v8f", c][:, i]
+        def cubes(c):
+            for v, t in ((st["v67", c][:, 0], T[6]), (st["v67", c][:, 1], T[7]),
+                         (st["v8f", c][:, 0], T[8]), (st["v8f", c][:, 1], T[5])):
                 stt(v, st["z", c], t, v, ALU.subtract, ALU.mult)
 
-        def relus(c):
+        def relu(c, key, i, scale):
+            t = wk.tile([P, F * SIZES[c]], F32, name=key, bufs=1)
+            nc.scalar.activation(out=t[:], in_=st["v67", c][:, i], func=ACTF.Relu, scale=scale)
+            st[key, c] = t
+
+        def relus_early(c):
+            relu(c, "e6", 0, 2 * G1)
+            relu(c, "e7b", 1, -2 * beta(1, 3))
+            relu(c, "h6b", 0, beta(3, 3))
+            relu(c, "h7", 1, -G3)
+
+        def relus_late(c):
             f = F * SIZES[c]
-            v67 = st["v67", c]
-            h = wk.tile([P, 2, f], F32, name="h", bufs=1)
-            e = wk.tile([P, 2, f], F32, name="e", bufs=1)
+            bz = st["bz", c]
+            b32 = st["b32", c]
+            nc.scalar.activation(out=bz[:, 0], in_=st["v67", c][:, 1], func=ACTF.Relu, scale=2 * G0)
+            relu(c, "h6", 0, -2 * beta(4, 2))
+            nc.scalar.activation(out=b32[:, 1], in_=st["v67", c][:, 0], func=ACTF.Relu, scale=-G2)
+            relu(c, "e7", 1, 2 * beta(2, 2))
+
+        def sums(c, eng):
+            f = F * SIZES[c]
+            p1 = wk.tile([P, f], F32, name="p1", bufs=1)
+            eng.tensor_tensor(out=p1[:], in0=st["e6", c][:], in1=st["v8f", c][:, 1], op=ALU.subtract)
             bz = wk.tile([P, 4, f], BF16, name="bz", bufs=1)
-            b23 = wk.tile([P, 2, f], BF16, name="b23", bufs=2)
-            nc.scalar.activation(out=h[:, 1], in_=v67[:, 1], func=ACTF.Relu, scale=-G3)
-            nc.scalar.activation(out=h[:, 0], in_=v67[:, 0], func=ACTF.Relu, scale=-2 * beta(4, 2))
-            nc.scalar.activation(out=e[:], in_=v67[:], func=ACTF.Relu, scale=2 * G1)
-            nc.scalar.activation(out=bz[:, 0], in_=v67[:, 1], func=ACTF.Relu, scale=2 * G0)
-            nc.scalar.activation(out=b23[:, 0], in_=v67[:, 0], func=ACTF.Relu, scale=-G2)
-            st["h", c] = h
-            st["e", c] = e
+            eng.tensor_tensor(out=bz[:, 1], in0=st["e6", c][:], in1=st["e7b", c][:], op=ALU.subtract)
+            b32 = wk.tile([P, 2, f], BF16, name="b32", bufs=2)
+            eng.tensor_tensor(out=b32[:, 0], in0=st["h7", c][:], in1=st["h6b", c][:], op=ALU.subtract)
+            st["p1", c] = p1
             st["bz", c] = bz
-            st["b23", c] = b23
+            st["b32", c] = b32
 
         def first_sum(c, eng):
             t1 = wk.tile([P, F * SIZES[c]], F32, name="bas_a", bufs=1, align_bytes=64)
-            eng.tensor_tensor(out=t1[:], in0=st["h", c][:, 1], in1=st["v8f", c][:, 0], op=ALU.add)
+            eng.tensor_tensor(out=t1[:], in0=st["h7", c][:], in1=st["v8f", c][:, 0], op=ALU.add)
             st["t1", c] = t1
 
-        def combos(c):
-            e, h, v8f, bz, b23, t1 = (st[k, c] for k in ("e", "h", "v8f", "bz", "b23", "t1"))
-            p1 = v8f[:, 1]
-            stt(b23[:, 1], h[:, 0], beta(3, 3) / (2 * beta(4, 2)), h[:, 1])
-            stt(p1, e[:, 0], beta(2, 3) / G1, p1)
-            stt(bz[:, 1], e[:, 1], beta(1, 3) / G1, e[:, 0])
-            stt(bz[:, 3], t1[:], 2 * beta(4, 3) / G3, h[:, 0])
-            stt(bz[:, 2], e[:, 1], beta(2, 2) / G1, p1)
+        def combos(c, part):
+            if part == 0:
+                stt(st["bz", c][:, 2], st["t1", c][:], 2 * beta(4, 3) / G3, st["h6", c][:])
+            else:
+                stt(st["bz", c][:, 3], st["p1", c][:], beta(2, 3) / G1, st["e7", c][:])
 
         def signs(c):
             f = F * SIZES[c]
             bo = wk.tile([P, 6, f], BF16, name="bo", bufs=1)
-            nc.vector.tensor_tensor(out=bo[:, 0:4], in0=st["bz", c][:],
-                                    in1=st["s", c].unsqueeze(1).to_broadcast([P, 4, f]), op=ALU.mult)
+            for lo, hi in ((0, 3), (3, 4)):
+                nc.vector.tensor_tensor(out=bo[:, lo:hi], in0=st["bz", c][:, lo:hi],
+                                        in1=st["s", c].unsqueeze(1).to_broadcast([P, hi - lo, f]), op=ALU.mult)
             st["bo", c] = bo
 
-        def mirror(c, part):
+        def negs(c):
+            bo = st["bo", c]
+            if c < FILL or c == NCH - 1:
+                nc.vector.tensor_scalar(out=bo[:, 4:6], in0=bo[:, 2:4], scalar1=-1.0, scalar2=None, op0=ALU.mult)
+            else:
+                nc.scalar.activation(out=bo[:, 4:6], in_=bo[:, 2:4], func=ACTF.Copy, scale=-1.0)
+
+        def outer(c):
             f = F * SIZES[c]
             bo = st["bo", c]
-            if part == 0:
-                nc.scalar.activation(out=bo[:, 4:6], in_=bo[:, 2:4], func=ACTF.Copy, scale=-1.0)
-                return
             bas_b = wk.tile([P, 4, f], BF16, name="bas_b", bufs=1, align_bytes=64)
-            if c < NCH - 1:
-                nc.scalar.activation(out=bas_b[:, 0:2], in_=bo[:, 0:2], func=ACTF.Relu)
-            else:
-                nc.vector.tensor_scalar(out=bas_b[:, 0:2], in0=bo[:, 0:2], scalar1=0.0, scalar2=None, op0=ALU.max)
+            na = OUTS_ACT if c < NCH - 1 else 0
+            if na:
+                nc.scalar.activation(out=bas_b[:, 0:na], in_=bo[:, 0:na], func=ACTF.Relu)
+            if na < 2:
+                nc.vector.tensor_scalar(out=bas_b[:, na:2], in0=bo[:, na:2], scalar1=0.0, scalar2=None, op0=ALU.max)
             nc.vector.tensor_scalar(out=bas_b[:, 2:4], in0=bo[:, 0:2], scalar1=-1.0, scalar2=0.0,
                                     op0=ALU.mult, op1=ALU.max)
             st["bas_b", c] = bas_b
@@ -226,7 +241,7 @@ def tile_bsplinekanlayer_t_kernel(tc, x, coeff, base_weight, knots, out):
             bas_a = wk.tile([P, 4, f], BF16, name="bas_a", bufs=1, align_bytes=64)
             nc.vector.tensor_tensor(
                 out=bas_a[:].rearrange("p (h m) f -> p h (m f)", h=2),
-                in0=st["b23", c][:].rearrange("p m f -> p (m f)").unsqueeze(1).to_broadcast([P, 2, 2 * f]),
+                in0=st["b32", c][:].rearrange("p m f -> p (m f)").unsqueeze(1).to_broadcast([P, 2, 2 * f]),
                 in1=st["bo", c][:, 2:6].rearrange("p (h m) f -> p h (m f)", h=2), op=ALU.max)
             st["bas_a", c] = bas_a
 
@@ -287,54 +302,63 @@ def tile_bsplinekanlayer_t_kernel(tc, x, coeff, base_weight, knots, out):
         turn_z(0)
         turn_x(0)
         squares(0)
-        cubes_a(0)
-        cubes_b(0)
+        cubes(0)
         small(1)
         turn_z(1)
         turn_s(0)
-        relus(0)
+        relus_early(0)
         coeff_prep()
         squares(1)
+        sums(0, nc.vector)
+        relus_late(0)
         coeff_quant()
         first_sum(0, nc.vector)
+        cubes(1)
+        small(2)
+        turn_z(2)
+        relus_early(1)
+        squares(2)
+        base(0, 0)
+        base(0, 1)
         for p in range(NCH):
             last = p == NCH - 1
             if ok(p + 4):
                 load(p + 4)
-            combos(p)
-            if ok(p + 2):
-                small(p + 2)
+            combos(p, 0)
+            if ok(p + 3):
+                small(p + 3)
+            combos(p, 1)
             signs(p)
-            mirror(p, 0)
+            if ok(p + 1):
+                sums(p + 1, nc.gpsimd)
+            negs(p)
             if ok(p + 1):
                 turn_x(p + 1)
                 turn_s(p + 1)
+            if ok(p + 2):
+                cubes(p + 2)
+            outer(p)
             if ok(p + 1):
-                cubes_a(p + 1)
-                cubes_b(p + 1)
-            mirror(p, 1)
+                relus_late(p + 1)
             if last:
                 quant(p, "b")
             maxima(p)
-            if ok(p + 1):
-                relus(p + 1)
             if not last:
                 quant(p, "b")
             quant(p, "a")
             if ok(p + 1):
-                first_sum(p + 1, nc.gpsimd)
+                first_sum(p + 1, nc.gpsimd if p > 0 else nc.vector)
             if ok(p - 1):
                 adds(p - 1)
+            if ok(p + 3):
+                turn_z(p + 3)
             if ok(p + 2):
-                turn_z(p + 2)
-            if p == 0:
-                base(p, 0)
-                base(p, 1)
+                relus_early(p + 2)
             if not last:
                 base(p + 1, 0)
             spline(p, 0)
-            if ok(p + 2):
-                squares(p + 2)
+            if ok(p + 3):
+                squares(p + 3)
             if not last:
                 base(p + 1, 1)
             spline(p, 1)

@@ -32,14 +32,16 @@ assert all(T[k] == -T[11 - k] for k in range(12))
 assert all(abs(beta(r, j) - beta(7 - r, 4 - j)) < 1e-12 for r in range(8) for j in range(5))
 G0, G1, G2, G3 = beta(0, 4), beta(1, 4), beta(2, 4), beta(3, 4)
 S8 = (beta(4, 4) * G3 / -beta(4, 3)) ** 0.5
-SF = (2 * G2 * G1 / -beta(2, 3)) ** 0.5
+SF = (G2 * G1 / -beta(2, 3)) ** 0.5
 
 OG = NO // 4
 F = 512
 SIZES = (1,) + (2,) * 7 + (1,)
 NCH = len(SIZES)
 OUTS_ACT = 0
-FILL = 2
+FILL = 9
+FIRST_SC = 6
+SQUARES = {"v67": ((1.0, T[6]), (1.0, T[7])), "v8f": ((S8, T[8]), (SF, T[5]))}
 START = [sum(SIZES[:c]) for c in range(NCH)]
 SLOT_A = {4: 0, 5: 1, 3: 2, 2: 3}
 SLOT_B = {7: 0, 6: 1, 0: 2, 1: 3}
@@ -74,6 +76,7 @@ def tile_bsplinekanlayer_t_kernel(tc, x, coeff, base_weight, knots, out):
         load(1)
         load(2)
         load(3)
+        load(4)
         c_ld = const.tile([P, 4, OG * NB], BF16)
         c_v = coeff.rearrange("(j t) o r -> j t (o r)", t=4)
         for g in range(4):
@@ -116,15 +119,26 @@ def tile_bsplinekanlayer_t_kernel(tc, x, coeff, base_weight, knots, out):
 
         def small(c):
             f = F * SIZES[c]
-            xf = st["xc", c][:].rearrange("p n i -> p (n i)")
-            za = wk.tile([P, f], BF16, name="za", bufs=1)
+            if c < FIRST_SC:
+                size_and_sign(c)
             zt = wk.tile([P, f], BF16, name="zt", bufs=2)
-            sg = wk.tile([P, f], BF16, name="sg", bufs=4)
-            nc.vector.tensor_single_scalar(out=za[:].bitcast(I32), in_=xf.bitcast(I32),
-                                           scalar=0x7FFF7FFF, op=ALU.bitwise_and)
-            nc.vector.tensor_scalar(out=sg[:], in0=xf, scalar1=0.0, scalar2=0.5, op0=ALU.is_ge, op1=ALU.subtract)
-            nc.vector.tensor_scalar(out=zt[:], in0=za[:], scalar1=T[8], scalar2=None, op0=ALU.min)
+            nc.vector.tensor_scalar(out=zt[:], in0=st["ab", c][:], scalar1=T[8], scalar2=None, op0=ALU.min)
             st["zt", c] = zt
+
+        def size_and_sign(c):
+            f = F * SIZES[c]
+            xf = st["xc", c][:].rearrange("p n i -> p (n i)")
+            ab = wk.tile([P, f], BF16, name="ab", bufs=1)
+            sg = wk.tile([P, f], BF16, name="sg", bufs=4)
+            if c < FIRST_SC:
+                nc.vector.tensor_single_scalar(out=ab[:].bitcast(I32), in_=xf.bitcast(I32),
+                                               scalar=0x7FFF7FFF, op=ALU.bitwise_and)
+                nc.vector.tensor_scalar(out=sg[:].bitcast(I32), in0=xf.bitcast(I32), scalar1=-0x7FFF8000,
+                                        scalar2=0x3F803F80, op0=ALU.bitwise_and, op1=ALU.bitwise_or)
+            else:
+                nc.scalar.activation(out=ab[:], in_=xf, func=ACTF.Abs)
+                nc.scalar.activation(out=sg[:], in_=xf, func=ACTF.Sign)
+            st["ab", c] = ab
             st["sg", c] = sg
 
         def turn(c, src, pool, tag):
@@ -136,7 +150,10 @@ def tile_bsplinekanlayer_t_kernel(tc, x, coeff, base_weight, knots, out):
             return tq[:].rearrange("p n b u -> p (n b u)").bitcast(BF16)
 
         def turn_z(c):
+            st["za", c] = turn(c, st["zt", c], ps_sp, "sp") if c < 3 else None
             st["z", c] = turn(c, st["zt", c], ps_z, "z")
+            if c >= 3:
+                st["za", c] = st["z", c]
 
         def turn_s(c):
             st["s", c] = turn(c, st["sg", c], ps_tr, "tr")
@@ -150,15 +167,11 @@ def tile_bsplinekanlayer_t_kernel(tc, x, coeff, base_weight, knots, out):
             nc.scalar.copy(out=xT[:], in_=xt_ps[:].rearrange("p m b -> p (m b)"))
             st["xT", c] = xT
 
-        def squares(c):
-            f = F * SIZES[c]
-            z = st["z", c]
-            v67 = wk.tile([P, 2, f], F32, name="v67", bufs=2)
-            v8f = wk.tile([P, 2, f], F32, name="v8f", bufs=2)
-            for o, sc, t in ((v67[:, 0], 1.0, -T[6]), (v67[:, 1], 1.0, -T[7]), (v8f[:, 0], S8, -T[8]), (v8f[:, 1], SF, T[6])):
-                nc.scalar.activation(out=o, in_=z, func=ACTF.Square, bias=sc * t, scale=sc)
-            st["v67", c] = v67
-            st["v8f", c] = v8f
+        def squares(c, key):
+            v = wk.tile([P, 2, F * SIZES[c]], F32, name=key, bufs=2)
+            for i, (sc, t) in enumerate(SQUARES[key]):
+                nc.scalar.activation(out=v[:, i], in_=st["za", c], func=ACTF.Square, bias=-sc * t, scale=sc)
+            st[key, c] = v
 
         def cubes(c):
             for v, t in ((st["v67", c][:, 0], T[6]), (st["v67", c][:, 1], T[7]),
@@ -171,8 +184,8 @@ def tile_bsplinekanlayer_t_kernel(tc, x, coeff, base_weight, knots, out):
             st[key, c] = t
 
         def relus_early(c):
-            relu(c, "e6", 0, 2 * G1)
-            relu(c, "e7b", 1, -2 * beta(1, 3))
+            relu(c, "e6", 0, G1)
+            relu(c, "e7b", 1, -beta(1, 3))
             relu(c, "h6b", 0, beta(3, 3))
             relu(c, "h7", 1, -G3)
 
@@ -180,31 +193,32 @@ def tile_bsplinekanlayer_t_kernel(tc, x, coeff, base_weight, knots, out):
             f = F * SIZES[c]
             bz = st["bz", c]
             b32 = st["b32", c]
-            nc.scalar.activation(out=bz[:, 0], in_=st["v67", c][:, 1], func=ACTF.Relu, scale=2 * G0)
-            relu(c, "h6", 0, -2 * beta(4, 2))
+            nc.scalar.activation(out=bz[:, 0], in_=st["v67", c][:, 1], func=ACTF.Relu, scale=G0)
+            relu(c, "h6", 0, -beta(4, 2))
             nc.scalar.activation(out=b32[:, 1], in_=st["v67", c][:, 0], func=ACTF.Relu, scale=-G2)
-            relu(c, "e7", 1, 2 * beta(2, 2))
+            relu(c, "e7", 1, beta(2, 2))
 
         def sums(c, eng):
             f = F * SIZES[c]
+            eng2 = eng if c < NCH - 1 else nc.vector
             p1 = wk.tile([P, f], F32, name="p1", bufs=1)
             eng.tensor_tensor(out=p1[:], in0=st["e6", c][:], in1=st["v8f", c][:, 1], op=ALU.subtract)
             bz = wk.tile([P, 4, f], BF16, name="bz", bufs=1)
-            eng.tensor_tensor(out=bz[:, 1], in0=st["e6", c][:], in1=st["e7b", c][:], op=ALU.subtract)
+            eng2.tensor_tensor(out=bz[:, 1], in0=st["e6", c][:], in1=st["e7b", c][:], op=ALU.subtract)
             b32 = wk.tile([P, 2, f], BF16, name="b32", bufs=2)
-            eng.tensor_tensor(out=b32[:, 0], in0=st["h7", c][:], in1=st["h6b", c][:], op=ALU.subtract)
+            eng2.tensor_tensor(out=b32[:, 0], in0=st["h7", c][:], in1=st["h6b", c][:], op=ALU.subtract)
             st["p1", c] = p1
             st["bz", c] = bz
             st["b32", c] = b32
 
         def first_sum(c, eng):
-            t1 = wk.tile([P, F * SIZES[c]], F32, name="bas_a", bufs=1, align_bytes=64)
+            t1 = wk.tile([P, F * SIZES[c]], F32, name="t1", bufs=1)
             eng.tensor_tensor(out=t1[:], in0=st["h7", c][:], in1=st["v8f", c][:, 0], op=ALU.add)
             st["t1", c] = t1
 
         def combos(c, part):
             if part == 0:
-                stt(st["bz", c][:, 2], st["t1", c][:], 2 * beta(4, 3) / G3, st["h6", c][:])
+                stt(st["bz", c][:, 2], st["t1", c][:], beta(4, 3) / G3, st["h6", c][:])
             else:
                 stt(st["bz", c][:, 3], st["p1", c][:], beta(2, 3) / G1, st["e7", c][:])
 
@@ -300,15 +314,17 @@ def tile_bsplinekanlayer_t_kernel(tc, x, coeff, base_weight, knots, out):
 
         small(0)
         turn_z(0)
+        squares(0, "v67")
+        squares(0, "v8f")
         turn_x(0)
-        squares(0)
         cubes(0)
         small(1)
         turn_z(1)
         turn_s(0)
         relus_early(0)
         coeff_prep()
-        squares(1)
+        squares(1, "v67")
+        squares(1, "v8f")
         sums(0, nc.vector)
         relus_late(0)
         coeff_quant()
@@ -317,49 +333,61 @@ def tile_bsplinekanlayer_t_kernel(tc, x, coeff, base_weight, knots, out):
         small(2)
         turn_z(2)
         relus_early(1)
-        squares(2)
-        base(0, 0)
-        base(0, 1)
+        squares(2, "v67")
+        squares(2, "v8f")
         for p in range(NCH):
             last = p == NCH - 1
-            if ok(p + 4):
-                load(p + 4)
-            combos(p, 0)
+            if ok(p + 5):
+                load(p + 5)
             if ok(p + 3):
                 small(p + 3)
             combos(p, 1)
+            combos(p, 0)
             signs(p)
             if ok(p + 1):
                 sums(p + 1, nc.gpsimd)
-            negs(p)
-            if ok(p + 1):
-                turn_x(p + 1)
-                turn_s(p + 1)
+                if p > 0:
+                    first_sum(p + 1, nc.gpsimd)
+            if FILL <= p < NCH - 1:
+                negs(p)
             if ok(p + 2):
                 cubes(p + 2)
+            if ok(p - 1) and ok(p + 2):
+                adds(p - 1)
+            if p == 0:
+                first_sum(1, nc.vector)
+            if not FILL <= p < NCH - 1:
+                negs(p)
             outer(p)
+            if ok(p + 3):
+                turn_z(p + 3)
             if ok(p + 1):
                 relus_late(p + 1)
+                turn_x(p + 1)
+                turn_s(p + 1)
+            if ok(p + 4):
+                size_and_sign(p + 4)
             if last:
                 quant(p, "b")
             maxima(p)
             if not last:
                 quant(p, "b")
             quant(p, "a")
-            if ok(p + 1):
-                first_sum(p + 1, nc.gpsimd if p > 0 else nc.vector)
-            if ok(p - 1):
+            if ok(p - 1) and not ok(p + 2):
                 adds(p - 1)
             if ok(p + 3):
-                turn_z(p + 3)
-            if ok(p + 2):
-                relus_early(p + 2)
-            if not last:
+                squares(p + 3, "v67")
+            if p < 2:
+                base(p, 0)
+                base(p, 1)
+            if 0 < p and not last:
                 base(p + 1, 0)
             spline(p, 0)
+            if ok(p + 2):
+                relus_early(p + 2)
             if ok(p + 3):
-                squares(p + 3)
-            if not last:
+                squares(p + 3, "v8f")
+            if 0 < p and not last:
                 base(p + 1, 1)
             spline(p, 1)
         adds(NCH - 1)

@@ -38,8 +38,10 @@ OG = NO // 4
 F = 512
 SIZES = (1,) + (2,) * 7 + (1,)
 NCH = len(SIZES)
-OUTS_ACT = 0
-FILL = 9
+OUT_SC = 5
+NEG_SC = 9
+CODB = 2
+OB = 3
 FIRST_SC = 6
 SQUARES = {"v67": ((1.0, T[6]), (1.0, T[7])), "v8f": ((S8, T[8]), (SF, T[5]))}
 START = [sum(SIZES[:c]) for c in range(NCH)]
@@ -95,8 +97,8 @@ def tile_bsplinekanlayer_t_kernel(tc, x, coeff, base_weight, knots, out):
         c_p = c_ld[:].rearrange("p t (o r) -> p r o t", r=NB)
         c_q = const.tile([P, NB * OG], U32, align_bytes=64)
         c_qs = const.tile([P, NB * OG], U8, align_bytes=64)
-        c_scl = const.tile([P, NB * NO], U8, align_bytes=64)
-        nc.gpsimd.memset(c_scl[:].bitcast(I32), 0)
+        c_scl = const.tile([P, NB, 2 * NO], U8, align_bytes=64)
+        nc.gpsimd.memset(c_scl[:].rearrange("p r o -> p (r o)").bitcast(I32), 0)
 
         def coeff_prep():
             nc.vector.tensor_copy(out=c_g[:], in_=c_p)
@@ -106,12 +108,12 @@ def tile_bsplinekanlayer_t_kernel(tc, x, coeff, base_weight, knots, out):
                                   in_=c_g[:].rearrange("p r o t -> p (r o t)"))
             codes = c_q[:].bitcast(I32).rearrange("p (r o) -> p r o", r=NB)
             scales = c_qs[:].bitcast(I32).rearrange("p (r o) -> p r o", r=NB)
-            c_scl_w = c_scl[:].bitcast(I32).rearrange("p (r o) -> p r o", r=NB)
+            c_scl_w = c_scl[:].rearrange("p r o -> p (r o)").bitcast(I32).rearrange("p (r q o) -> p r q o", r=NB, q=2)
             for q in range(4):
                 for g in range(4):
                     nc.sync.dma_start(out=c_z[32 * q:32 * q + 32, :, q, OG * g:OG * g + OG].bitcast(I32),
                                       in_=codes[32 * g:32 * g + 32])
-                    nc.sync.dma_start(out=c_scl_w[32 * q:32 * q + 4, :, 16 * g:16 * g + 16],
+                    nc.sync.dma_start(out=c_scl_w[32 * q:32 * q + 4, :, q % 2, 16 * g:16 * g + 16],
                                       in_=scales[32 * g:32 * g + 4])
 
         def stt(o, a, s, b, op0=ALU.mult, op1=ALU.add):
@@ -232,7 +234,7 @@ def tile_bsplinekanlayer_t_kernel(tc, x, coeff, base_weight, knots, out):
 
         def negs(c):
             bo = st["bo", c]
-            if c < FILL or c == NCH - 1:
+            if c < NEG_SC:
                 nc.vector.tensor_scalar(out=bo[:, 4:6], in0=bo[:, 2:4], scalar1=-1.0, scalar2=None, op0=ALU.mult)
             else:
                 nc.scalar.activation(out=bo[:, 4:6], in_=bo[:, 2:4], func=ACTF.Copy, scale=-1.0)
@@ -241,11 +243,10 @@ def tile_bsplinekanlayer_t_kernel(tc, x, coeff, base_weight, knots, out):
             f = F * SIZES[c]
             bo = st["bo", c]
             bas_b = wk.tile([P, 4, f], BF16, name="bas_b", bufs=1, align_bytes=64)
-            na = OUTS_ACT if c < NCH - 1 else 0
-            if na:
-                nc.scalar.activation(out=bas_b[:, 0:na], in_=bo[:, 0:na], func=ACTF.Relu)
-            if na < 2:
-                nc.vector.tensor_scalar(out=bas_b[:, na:2], in0=bo[:, na:2], scalar1=0.0, scalar2=None, op0=ALU.max)
+            if OUT_SC <= c < NCH - 1:
+                nc.scalar.activation(out=bas_b[:, 0:2], in_=bo[:, 0:2], func=ACTF.Relu)
+            else:
+                nc.vector.tensor_scalar(out=bas_b[:, 0:2], in0=bo[:, 0:2], scalar1=0.0, scalar2=None, op0=ALU.max)
             nc.vector.tensor_scalar(out=bas_b[:, 2:4], in0=bo[:, 0:2], scalar1=-1.0, scalar2=0.0,
                                     op0=ALU.mult, op1=ALU.max)
             st["bas_b", c] = bas_b
@@ -261,8 +262,8 @@ def tile_bsplinekanlayer_t_kernel(tc, x, coeff, base_weight, knots, out):
 
         def quant(c, ab):
             f = F * SIZES[c]
-            cod = wk.tile([P, f], U32, name="cod_" + ab, bufs=2, align_bytes=64)
-            scl = wk.tile([P, f], U8, name="scl_" + ab, bufs=2, align_bytes=64)
+            cod = wk.tile([P, f], U32, name="cod_" + ab, bufs=CODB, align_bytes=64)
+            scl = wk.tile([P, f], U8, name="scl_" + ab, bufs=CODB, align_bytes=64)
             nc.vector.quantize_mx(out=cod[:].bitcast(FP8X4), scales=scl[:],
                                   in_=st["bas_" + ab, c][:].rearrange("p m f -> p (m f)"))
             st["cod_" + ab, c] = cod
@@ -285,29 +286,31 @@ def tile_bsplinekanlayer_t_kernel(tc, x, coeff, base_weight, knots, out):
             if b < SIZES[c]:
                 for h in range(2):
                     sp = ps_sp.tile([P, 2, NO], F32, name="sp")
-                    for qq in range(2):
-                        for r in RS:
-                            ab, slot = ("a", SLOT_A[r]) if r in SLOT_A else ("b", SLOT_B[r])
-                            lo = slot * (F * SIZES[c] // 4) + b * P
-                            nc.tensor.matmul_mx(
-                                out=sp[:, qq, :],
-                                lhsT=st["cod_" + ab, c][:, lo:lo + P].bitcast(FP8X4),
-                                lhsT_scale=st["scl_" + ab, c][:, lo:lo + P],
-                                rhs=c_z[:, r, 2 * h + qq, :].bitcast(FP8X4),
-                                rhs_scale=c_scl[:, r * NO:(r + 1) * NO],
-                                start=r == RS[0],
-                                stop=r == RS[-1],
-                            )
+                    for r in RS:
+                        ab, slot = ("a", SLOT_A[r]) if r in SLOT_A else ("b", SLOT_B[r])
+                        lo = slot * (F * SIZES[c] // 4) + b * P
+                        nc.tensor.matmul_mx(
+                            out=sp[:].rearrange("p q o -> p (q o)"),
+                            lhsT=st["cod_" + ab, c][:, lo:lo + P].bitcast(FP8X4),
+                            lhsT_scale=st["scl_" + ab, c][:, lo:lo + P],
+                            rhs=c_z[:, r, 2 * h:2 * h + 2, :].rearrange("p q o -> p (q o)").bitcast(FP8X4),
+                            rhs_scale=c_scl[:, r, :],
+                            start=r == RS[0],
+                            stop=r == RS[-1],
+                        )
                     st["sp", START[c] + b, h] = sp
 
         def adds(c):
             for b in range(START[c], START[c] + SIZES[c]):
-                o_sb = wk.tile([P, 4, NO], F32, name="o_sb", bufs=3)
+                o_sb = wk.tile([P, 4, NO], F32, name="o_sb", bufs=OB)
                 for h in range(2):
                     nc.vector.tensor_tensor(out=o_sb[:, 2 * h:2 * h + 2, :].rearrange("p a o -> p (a o)"),
                                             in0=st["sp", b, h][:].rearrange("p a o -> p (a o)"),
                                             in1=st["sil", b, h][:], op=ALU.add)
-                nc.sync.dma_start(out=out_v[:, 4 * b:4 * b + 4, :], in_=o_sb[:])
+                    if c == NCH - 1:
+                        nc.sync.dma_start(out=out_v[:, 4 * b + 2 * h:4 * b + 2 * h + 2, :], in_=o_sb[:, 2 * h:2 * h + 2, :])
+                if c < NCH - 1:
+                    nc.sync.dma_start(out=out_v[:, 4 * b:4 * b + 4, :], in_=o_sb[:])
 
         def ok(c):
             return 0 <= c < NCH
@@ -348,7 +351,7 @@ def tile_bsplinekanlayer_t_kernel(tc, x, coeff, base_weight, knots, out):
                 sums(p + 1, nc.gpsimd)
                 if p > 0:
                     first_sum(p + 1, nc.gpsimd)
-            if FILL <= p < NCH - 1:
+            if p >= NEG_SC:
                 negs(p)
             if ok(p + 2):
                 cubes(p + 2)
@@ -356,17 +359,31 @@ def tile_bsplinekanlayer_t_kernel(tc, x, coeff, base_weight, knots, out):
                 adds(p - 1)
             if p == 0:
                 first_sum(1, nc.vector)
-            if not FILL <= p < NCH - 1:
+            if p < NEG_SC:
                 negs(p)
             outer(p)
-            if ok(p + 3):
-                turn_z(p + 3)
             if ok(p + 1):
                 relus_late(p + 1)
                 turn_x(p + 1)
+            if ok(p + 3):
+                turn_z(p + 3)
+            if ok(p + 1):
                 turn_s(p + 1)
+            if ok(p + 3):
+                squares(p + 3, "v67")
+            if ok(p + 3):
+                squares(p + 3, "v8f")
+            if p < 2:
+                base(p, 0)
+                base(p, 1)
+            if 0 < p and not last:
+                base(p + 1, 0)
             if ok(p + 4):
                 size_and_sign(p + 4)
+            if ok(p + 2):
+                relus_early(p + 2)
+            if 0 < p and not last:
+                base(p + 1, 1)
             if last:
                 quant(p, "b")
             maxima(p)
@@ -375,19 +392,6 @@ def tile_bsplinekanlayer_t_kernel(tc, x, coeff, base_weight, knots, out):
             quant(p, "a")
             if ok(p - 1) and not ok(p + 2):
                 adds(p - 1)
-            if ok(p + 3):
-                squares(p + 3, "v67")
-            if p < 2:
-                base(p, 0)
-                base(p, 1)
-            if 0 < p and not last:
-                base(p + 1, 0)
             spline(p, 0)
-            if ok(p + 2):
-                relus_early(p + 2)
-            if ok(p + 3):
-                squares(p + 3, "v8f")
-            if 0 < p and not last:
-                base(p + 1, 1)
             spline(p, 1)
         adds(NCH - 1)

@@ -39,7 +39,10 @@ F = 512
 SIZES = (1,) + (2,) * 7 + (1,)
 NCH = len(SIZES)
 OUT_SC = 5
-NEG_SC = 9
+OUT_END = 8
+T1_SC = 2
+T1_END = 6
+ADD_LATE = 7
 CODB = 2
 OB = 3
 FIRST_SC = 6
@@ -91,14 +94,17 @@ def tile_bsplinekanlayer_t_kernel(tc, x, coeff, base_weight, knots, out):
         ident_b = const.tile([P, P], BF16)
         make_identity(nc, ident_b[:])
         c_z = const.tile([P, NB, 4, NO], U32, align_bytes=64)
-        nc.gpsimd.memset(c_z[:].bitcast(F32), 0.0)
+        zeros = wk.tile([P, 4 * NO], U32, name="o_sb", bufs=OB)
+        nc.gpsimd.memset(zeros[:].bitcast(I32), 0)
 
         c_g = const.tile([P, NB, OG, 4], BF16, align_bytes=64)
         c_p = c_ld[:].rearrange("p t (o r) -> p r o t", r=NB)
         c_q = const.tile([P, NB * OG], U32, align_bytes=64)
         c_qs = const.tile([P, NB * OG], U8, align_bytes=64)
         c_scl = const.tile([P, NB, 2 * NO], U8, align_bytes=64)
-        nc.gpsimd.memset(c_scl[:].rearrange("p r o -> p (r o)").bitcast(I32), 0)
+        for r in range(NB):
+            nc.sync.dma_start(out=c_z[:, r].rearrange("p q o -> p (q o)").bitcast(I32), in_=zeros[:].bitcast(I32))
+        nc.sync.dma_start(out=c_scl[:].rearrange("p r o -> p (r o)").bitcast(I32), in_=zeros[:].bitcast(I32))
 
         def coeff_prep():
             nc.vector.tensor_copy(out=c_g[:], in_=c_p)
@@ -226,30 +232,21 @@ def tile_bsplinekanlayer_t_kernel(tc, x, coeff, base_weight, knots, out):
 
         def signs(c):
             f = F * SIZES[c]
-            bo = wk.tile([P, 6, f], BF16, name="bo", bufs=1)
+            bo = wk.tile([P, 10, f], BF16, name="bo", bufs=1, align_bytes=64)
             for lo, hi in ((0, 3), (3, 4)):
                 nc.vector.tensor_tensor(out=bo[:, lo:hi], in0=st["bz", c][:, lo:hi],
                                         in1=st["s", c].unsqueeze(1).to_broadcast([P, hi - lo, f]), op=ALU.mult)
             st["bo", c] = bo
 
-        def negs(c):
+        def spread(c):
             bo = st["bo", c]
-            if c < NEG_SC:
-                nc.vector.tensor_scalar(out=bo[:, 4:6], in0=bo[:, 2:4], scalar1=-1.0, scalar2=None, op0=ALU.mult)
+            if OUT_SC <= c < OUT_END:
+                nc.scalar.activation(out=bo[:, 4:6], in_=bo[:, 0:2], func=ACTF.Relu)
             else:
-                nc.scalar.activation(out=bo[:, 4:6], in_=bo[:, 2:4], func=ACTF.Copy, scale=-1.0)
-
-        def outer(c):
-            f = F * SIZES[c]
-            bo = st["bo", c]
-            bas_b = wk.tile([P, 4, f], BF16, name="bas_b", bufs=1, align_bytes=64)
-            if OUT_SC <= c < NCH - 1:
-                nc.scalar.activation(out=bas_b[:, 0:2], in_=bo[:, 0:2], func=ACTF.Relu)
-            else:
-                nc.vector.tensor_scalar(out=bas_b[:, 0:2], in0=bo[:, 0:2], scalar1=0.0, scalar2=None, op0=ALU.max)
-            nc.vector.tensor_scalar(out=bas_b[:, 2:4], in0=bo[:, 0:2], scalar1=-1.0, scalar2=0.0,
+                nc.vector.tensor_scalar(out=bo[:, 4:6], in0=bo[:, 0:2], scalar1=0.0, scalar2=None, op0=ALU.max)
+            nc.vector.tensor_scalar(out=bo[:, 6:10], in0=bo[:, 0:4], scalar1=-1.0, scalar2=0.0,
                                     op0=ALU.mult, op1=ALU.max)
-            st["bas_b", c] = bas_b
+            st["bas_b", c] = bo[:, 4:8]
 
         def maxima(c):
             f = F * SIZES[c]
@@ -257,15 +254,15 @@ def tile_bsplinekanlayer_t_kernel(tc, x, coeff, base_weight, knots, out):
             nc.vector.tensor_tensor(
                 out=bas_a[:].rearrange("p (h m) f -> p h (m f)", h=2),
                 in0=st["b32", c][:].rearrange("p m f -> p (m f)").unsqueeze(1).to_broadcast([P, 2, 2 * f]),
-                in1=st["bo", c][:, 2:6].rearrange("p (h m) f -> p h (m f)", h=2), op=ALU.max)
-            st["bas_a", c] = bas_a
+                in1=st["bo", c][:].rearrange("p m f -> p (m f)")[:, 2 * f:].rearrange("p (h m) -> p h m", m=2 * f)[:, 0:4:3], op=ALU.max)
+            st["bas_a", c] = bas_a[:]
 
         def quant(c, ab):
             f = F * SIZES[c]
             cod = wk.tile([P, f], U32, name="cod_" + ab, bufs=CODB, align_bytes=64)
             scl = wk.tile([P, f], U8, name="scl_" + ab, bufs=CODB, align_bytes=64)
             nc.vector.quantize_mx(out=cod[:].bitcast(FP8X4), scales=scl[:],
-                                  in_=st["bas_" + ab, c][:].rearrange("p m f -> p (m f)"))
+                                  in_=st["bas_" + ab, c].rearrange("p m f -> p (m f)"))
             st["cod_" + ab, c] = cod
             st["scl_" + ab, c] = scl
 
@@ -320,9 +317,9 @@ def tile_bsplinekanlayer_t_kernel(tc, x, coeff, base_weight, knots, out):
         squares(0, "v67")
         squares(0, "v8f")
         turn_x(0)
-        cubes(0)
         small(1)
         turn_z(1)
+        cubes(0)
         turn_s(0)
         relus_early(0)
         coeff_prep()
@@ -349,19 +346,15 @@ def tile_bsplinekanlayer_t_kernel(tc, x, coeff, base_weight, knots, out):
             signs(p)
             if ok(p + 1):
                 sums(p + 1, nc.gpsimd)
-                if p > 0:
+                if T1_SC <= p < T1_END:
                     first_sum(p + 1, nc.gpsimd)
-            if p >= NEG_SC:
-                negs(p)
             if ok(p + 2):
                 cubes(p + 2)
-            if ok(p - 1) and ok(p + 2):
+            if ok(p - 1) and p < ADD_LATE:
                 adds(p - 1)
-            if p == 0:
-                first_sum(1, nc.vector)
-            if p < NEG_SC:
-                negs(p)
-            outer(p)
+            if ok(p + 1) and not T1_SC <= p < T1_END:
+                first_sum(p + 1, nc.vector)
+            spread(p)
             if ok(p + 1):
                 relus_late(p + 1)
                 turn_x(p + 1)
@@ -390,7 +383,7 @@ def tile_bsplinekanlayer_t_kernel(tc, x, coeff, base_weight, knots, out):
             if not last:
                 quant(p, "b")
             quant(p, "a")
-            if ok(p - 1) and not ok(p + 2):
+            if ok(p - 1) and p >= ADD_LATE:
                 adds(p - 1)
             spline(p, 0)
             spline(p, 1)

@@ -38,19 +38,21 @@ OG = NO // 4
 F = 512
 SIZES = (1,) + (2,) * 7 + (1,)
 NCH = len(SIZES)
-OUT_SC = 5
+OUT_SC = 4
 OUT_END = 8
 T1_SC = 2
 T1_END = 6
-ADD_LATE = 7
+TAIL = 7
+E7_V = 2
 CODB = 2
 OB = 3
-FIRST_SC = 6
+FIRST_SC = 7
 SQUARES = {"v67": ((1.0, T[6]), (1.0, T[7])), "v8f": ((S8, T[8]), (SF, T[5]))}
 START = [sum(SIZES[:c]) for c in range(NCH)]
 SLOT_A = {4: 0, 5: 1, 3: 2, 2: 3}
 SLOT_B = {7: 0, 6: 1, 0: 2, 1: 3}
-RS = (4, 5, 3, 2, 7, 6, 0, 1)
+RS_A = (4, 5, 3, 2)
+RS_B = (7, 6, 0, 1)
 
 
 def tile_bsplinekanlayer_t_kernel(tc, x, coeff, base_weight, knots, out):
@@ -97,6 +99,7 @@ def tile_bsplinekanlayer_t_kernel(tc, x, coeff, base_weight, knots, out):
         zeros = wk.tile([P, 4 * NO], U32, name="o_sb", bufs=OB)
         nc.gpsimd.memset(zeros[:].bitcast(I32), 0)
 
+        one = const.tile([P, 1], F32)
         c_g = const.tile([P, NB, OG, 4], BF16, align_bytes=64)
         c_p = c_ld[:].rearrange("p t (o r) -> p r o t", r=NB)
         c_q = const.tile([P, NB * OG], U32, align_bytes=64)
@@ -107,7 +110,8 @@ def tile_bsplinekanlayer_t_kernel(tc, x, coeff, base_weight, knots, out):
         nc.sync.dma_start(out=c_scl[:].rearrange("p r o -> p (r o)").bitcast(I32), in_=zeros[:].bitcast(I32))
 
         def coeff_prep():
-            nc.vector.tensor_copy(out=c_g[:], in_=c_p)
+            nc.vector.memset(one[:], 1.0)
+            nc.gpsimd.tensor_scalar(out=c_g[:], in0=c_p, scalar1=one[:], scalar2=0.0, op0=ALU.mult, op1=ALU.add)
 
         def coeff_quant():
             nc.vector.quantize_mx(out=c_q[:].bitcast(FP8X4), scales=c_qs[:],
@@ -129,6 +133,10 @@ def tile_bsplinekanlayer_t_kernel(tc, x, coeff, base_weight, knots, out):
             f = F * SIZES[c]
             if c < FIRST_SC:
                 size_and_sign(c)
+            smaller(c)
+
+        def smaller(c):
+            f = F * SIZES[c]
             zt = wk.tile([P, f], BF16, name="zt", bufs=2)
             nc.vector.tensor_scalar(out=zt[:], in0=st["ab", c][:], scalar1=T[8], scalar2=None, op0=ALU.min)
             st["zt", c] = zt
@@ -191,6 +199,12 @@ def tile_bsplinekanlayer_t_kernel(tc, x, coeff, base_weight, knots, out):
             nc.scalar.activation(out=t[:], in_=st["v67", c][:, i], func=ACTF.Relu, scale=scale)
             st[key, c] = t
 
+        def relu_v(c, key, i, scale):
+            t = wk.tile([P, F * SIZES[c]], F32, name=key, bufs=1)
+            nc.vector.tensor_scalar(out=t[:], in0=st["v67", c][:, i], scalar1=scale, scalar2=0.0,
+                                    op0=ALU.mult, op1=ALU.max)
+            st[key, c] = t
+
         def relus_early(c):
             relu(c, "e6", 0, G1)
             relu(c, "e7b", 1, -beta(1, 3))
@@ -204,7 +218,7 @@ def tile_bsplinekanlayer_t_kernel(tc, x, coeff, base_weight, knots, out):
             nc.scalar.activation(out=bz[:, 0], in_=st["v67", c][:, 1], func=ACTF.Relu, scale=G0)
             relu(c, "h6", 0, -beta(4, 2))
             nc.scalar.activation(out=b32[:, 1], in_=st["v67", c][:, 0], func=ACTF.Relu, scale=-G2)
-            relu(c, "e7", 1, beta(2, 2))
+            (relu_v if c < E7_V else relu)(c, "e7", 1, beta(2, 2))
 
         def sums(c, eng):
             f = F * SIZES[c]
@@ -233,19 +247,22 @@ def tile_bsplinekanlayer_t_kernel(tc, x, coeff, base_weight, knots, out):
         def signs(c):
             f = F * SIZES[c]
             bo = wk.tile([P, 10, f], BF16, name="bo", bufs=1, align_bytes=64)
-            for lo, hi in ((0, 3), (3, 4)):
-                nc.vector.tensor_tensor(out=bo[:, lo:hi], in0=st["bz", c][:, lo:hi],
-                                        in1=st["s", c].unsqueeze(1).to_broadcast([P, hi - lo, f]), op=ALU.mult)
+            nc.vector.tensor_tensor(out=bo[:, 0:4], in0=st["bz", c][:],
+                                    in1=st["s", c].unsqueeze(1).to_broadcast([P, 4, f]), op=ALU.mult)
             st["bo", c] = bo
 
         def spread(c):
             bo = st["bo", c]
+            def mirror(lo, hi):
+                nc.vector.tensor_scalar(out=bo[:, 6 + lo:6 + hi], in0=bo[:, lo:hi], scalar1=-1.0, scalar2=0.0,
+                                        op0=ALU.mult, op1=ALU.max)
+
             if OUT_SC <= c < OUT_END:
                 nc.scalar.activation(out=bo[:, 4:6], in_=bo[:, 0:2], func=ACTF.Relu)
+                mirror(0, 4)
             else:
+                mirror(0, 4)
                 nc.vector.tensor_scalar(out=bo[:, 4:6], in0=bo[:, 0:2], scalar1=0.0, scalar2=None, op0=ALU.max)
-            nc.vector.tensor_scalar(out=bo[:, 6:10], in0=bo[:, 0:4], scalar1=-1.0, scalar2=0.0,
-                                    op0=ALU.mult, op1=ALU.max)
             st["bas_b", c] = bo[:, 4:8]
 
         def maxima(c):
@@ -279,23 +296,25 @@ def tile_bsplinekanlayer_t_kernel(tc, x, coeff, base_weight, knots, out):
                     nc.scalar.activation(out=sil[:], in_=pb[:].rearrange("p a o -> p (a o)"), func=ACTF.Silu)
                     st["sil", START[c] + b, h] = sil
 
-        def spline(c, b):
-            if b < SIZES[c]:
+        def spline(c, ab, rs, first):
+            slots = SLOT_A if ab == "a" else SLOT_B
+            for b in range(SIZES[c]):
                 for h in range(2):
-                    sp = ps_sp.tile([P, 2, NO], F32, name="sp")
-                    for r in RS:
-                        ab, slot = ("a", SLOT_A[r]) if r in SLOT_A else ("b", SLOT_B[r])
-                        lo = slot * (F * SIZES[c] // 4) + b * P
+                    if first:
+                        pool, tag = (ps_pb, "pb") if c == NCH - 1 else (ps_sp, "sp")
+                        st["sp", START[c] + b, h] = pool.tile([P, 2, NO], F32, name=tag)
+                    sp = st["sp", START[c] + b, h]
+                    for r in rs:
+                        lo = slots[r] * (F * SIZES[c] // 4) + b * P
                         nc.tensor.matmul_mx(
                             out=sp[:].rearrange("p q o -> p (q o)"),
                             lhsT=st["cod_" + ab, c][:, lo:lo + P].bitcast(FP8X4),
                             lhsT_scale=st["scl_" + ab, c][:, lo:lo + P],
                             rhs=c_z[:, r, 2 * h:2 * h + 2, :].rearrange("p q o -> p (q o)").bitcast(FP8X4),
                             rhs_scale=c_scl[:, r, :],
-                            start=r == RS[0],
-                            stop=r == RS[-1],
+                            start=first and r == rs[0],
+                            stop=not first and r == rs[-1],
                         )
-                    st["sp", START[c] + b, h] = sp
 
         def adds(c):
             for b in range(START[c], START[c] + SIZES[c]):
@@ -318,18 +337,18 @@ def tile_bsplinekanlayer_t_kernel(tc, x, coeff, base_weight, knots, out):
         squares(0, "v8f")
         turn_x(0)
         small(1)
-        turn_z(1)
         cubes(0)
+        turn_z(1)
         turn_s(0)
         relus_early(0)
-        coeff_prep()
         squares(1, "v67")
         squares(1, "v8f")
         sums(0, nc.vector)
         relus_late(0)
-        coeff_quant()
         first_sum(0, nc.vector)
+        coeff_prep()
         cubes(1)
+        coeff_quant()
         small(2)
         turn_z(2)
         relus_early(1)
@@ -339,10 +358,12 @@ def tile_bsplinekanlayer_t_kernel(tc, x, coeff, base_weight, knots, out):
             last = p == NCH - 1
             if ok(p + 5):
                 load(p + 5)
-            if ok(p + 3):
-                small(p + 3)
+            if ok(p + 3) and p + 3 < FIRST_SC:
+                size_and_sign(p + 3)
             combos(p, 1)
             combos(p, 0)
+            if ok(p + 3):
+                smaller(p + 3)
             signs(p)
             if ok(p + 1):
                 sums(p + 1, nc.gpsimd)
@@ -350,11 +371,15 @@ def tile_bsplinekanlayer_t_kernel(tc, x, coeff, base_weight, knots, out):
                     first_sum(p + 1, nc.gpsimd)
             if ok(p + 2):
                 cubes(p + 2)
-            if ok(p - 1) and p < ADD_LATE:
+            if p == TAIL:
+                spread(p)
+                quant(p, "b")
+            if ok(p - 1) and not last:
                 adds(p - 1)
             if ok(p + 1) and not T1_SC <= p < T1_END:
                 first_sum(p + 1, nc.vector)
-            spread(p)
+            if p != TAIL:
+                spread(p)
             if ok(p + 1):
                 relus_late(p + 1)
                 turn_x(p + 1)
@@ -371,7 +396,7 @@ def tile_bsplinekanlayer_t_kernel(tc, x, coeff, base_weight, knots, out):
                 base(p, 1)
             if 0 < p and not last:
                 base(p + 1, 0)
-            if ok(p + 4):
+            if ok(p + 4) and p + 4 >= FIRST_SC:
                 size_and_sign(p + 4)
             if ok(p + 2):
                 relus_early(p + 2)
@@ -380,11 +405,11 @@ def tile_bsplinekanlayer_t_kernel(tc, x, coeff, base_weight, knots, out):
             if last:
                 quant(p, "b")
             maxima(p)
-            if not last:
+            if p < TAIL:
                 quant(p, "b")
             quant(p, "a")
-            if ok(p - 1) and p >= ADD_LATE:
+            if last:
                 adds(p - 1)
-            spline(p, 0)
-            spline(p, 1)
+            spline(p, "b", RS_B, True)
+            spline(p, "a", RS_A, False)
         adds(NCH - 1)

@@ -38,21 +38,20 @@ OG = NO // 4
 F = 512
 SIZES = (1,) + (2,) * 7 + (1,)
 NCH = len(SIZES)
-OUT_SC = 4
+OUT_SC = 5
 OUT_END = 8
 T1_SC = 2
 T1_END = 6
 TAIL = 7
+CUT = 0.5
 E7_V = 2
 CODB = 2
 OB = 3
 FIRST_SC = 7
-SQUARES = {"v67": ((1.0, T[6]), (1.0, T[7])), "v8f": ((S8, T[8]), (SF, T[5]))}
+SQUARES = {"v67": ((1.0, T[6]), (1.0, T[7])), "v8f": ((SF, T[5]), (S8, T[8]))}
 START = [sum(SIZES[:c]) for c in range(NCH)]
 SLOT_A = {4: 0, 5: 1, 3: 2, 2: 3}
 SLOT_B = {7: 0, 6: 1, 0: 2, 1: 3}
-RS_A = (4, 5, 3, 2)
-RS_B = (7, 6, 0, 1)
 
 
 def tile_bsplinekanlayer_t_kernel(tc, x, coeff, base_weight, knots, out):
@@ -84,7 +83,7 @@ def tile_bsplinekanlayer_t_kernel(tc, x, coeff, base_weight, knots, out):
         load(2)
         load(3)
         load(4)
-        c_ld = const.tile([P, 4, OG * NB], BF16)
+        c_ld = wk.tile([P, 4, OG * NB], BF16, name="bo", bufs=1, align_bytes=64)
         c_v = coeff.rearrange("(j t) o r -> j t (o r)", t=4)
         for g in range(4):
             nc.scalar.dma_start(out=c_ld[32 * g:32 * g + 32, :, :], in_=c_v[:, :, OG * NB * g:OG * NB * (g + 1)])
@@ -100,7 +99,7 @@ def tile_bsplinekanlayer_t_kernel(tc, x, coeff, base_weight, knots, out):
         nc.gpsimd.memset(zeros[:].bitcast(I32), 0)
 
         one = const.tile([P, 1], F32)
-        c_g = const.tile([P, NB, OG, 4], BF16, align_bytes=64)
+        c_g = wk.tile([P, NB, OG, 4], BF16, name="bas_a", bufs=1, align_bytes=64)
         c_p = c_ld[:].rearrange("p t (o r) -> p r o t", r=NB)
         c_q = const.tile([P, NB * OG], U32, align_bytes=64)
         c_qs = const.tile([P, NB * OG], U8, align_bytes=64)
@@ -191,13 +190,22 @@ def tile_bsplinekanlayer_t_kernel(tc, x, coeff, base_weight, knots, out):
 
         def cubes(c):
             for v, t in ((st["v67", c][:, 0], T[6]), (st["v67", c][:, 1], T[7]),
-                         (st["v8f", c][:, 0], T[8]), (st["v8f", c][:, 1], T[5])):
+                         (st["v8f", c][:, 0], T[5]), (st["v8f", c][:, 1], T[8])):
                 stt(v, st["z", c], t, v, ALU.subtract, ALU.mult)
 
         def relu(c, key, i, scale):
             t = wk.tile([P, F * SIZES[c]], F32, name=key, bufs=1)
             nc.scalar.activation(out=t[:], in_=st["v67", c][:, i], func=ACTF.Relu, scale=scale)
             st[key, c] = t
+
+        def relu_pair(c, key, slot, i, scale):
+            if slot == 0:
+                st[key, c] = wk.tile([P, 2, F * SIZES[c]], F32, name=key, bufs=1)
+            if c == 0 and slot == 0:
+                nc.vector.tensor_scalar(out=st[key, c][:, slot], in0=st["v67", c][:, i], scalar1=scale, scalar2=0.0,
+                                        op0=ALU.mult, op1=ALU.max)
+            else:
+                nc.scalar.activation(out=st[key, c][:, slot], in_=st["v67", c][:, i], func=ACTF.Relu, scale=scale)
 
         def relu_v(c, key, i, scale):
             t = wk.tile([P, F * SIZES[c]], F32, name=key, bufs=1)
@@ -206,48 +214,45 @@ def tile_bsplinekanlayer_t_kernel(tc, x, coeff, base_weight, knots, out):
             st[key, c] = t
 
         def relus_early(c):
-            relu(c, "e6", 0, G1)
-            relu(c, "e7b", 1, -beta(1, 3))
-            relu(c, "h6b", 0, beta(3, 3))
-            relu(c, "h7", 1, -G3)
+            relu_pair(c, "e6h7", 0, 0, G1)
+            relu_pair(c, "e7h6", 0, 1, -beta(1, 3))
+            relu_pair(c, "e7h6", 1, 0, beta(3, 3))
+            relu_pair(c, "e6h7", 1, 1, -G3)
 
         def relus_late(c):
-            f = F * SIZES[c]
-            bz = st["bz", c]
-            b32 = st["b32", c]
-            nc.scalar.activation(out=bz[:, 0], in_=st["v67", c][:, 1], func=ACTF.Relu, scale=G0)
+            b6 = st["b6", c]
+            nc.scalar.activation(out=b6[:, 0], in_=st["v67", c][:, 1], func=ACTF.Relu, scale=G0)
             relu(c, "h6", 0, -beta(4, 2))
-            nc.scalar.activation(out=b32[:, 1], in_=st["v67", c][:, 0], func=ACTF.Relu, scale=-G2)
+            nc.scalar.activation(out=b6[:, 5], in_=st["v67", c][:, 0], func=ACTF.Relu, scale=-G2)
             (relu_v if c < E7_V else relu)(c, "e7", 1, beta(2, 2))
 
         def sums(c, eng):
             f = F * SIZES[c]
-            eng2 = eng if c < NCH - 1 else nc.vector
+            e6h7, e7h6 = st["e6h7", c], st["e7h6", c]
             p1 = wk.tile([P, f], F32, name="p1", bufs=1)
-            eng.tensor_tensor(out=p1[:], in0=st["e6", c][:], in1=st["v8f", c][:, 1], op=ALU.subtract)
-            bz = wk.tile([P, 4, f], BF16, name="bz", bufs=1)
-            eng2.tensor_tensor(out=bz[:, 1], in0=st["e6", c][:], in1=st["e7b", c][:], op=ALU.subtract)
-            b32 = wk.tile([P, 2, f], BF16, name="b32", bufs=2)
-            eng2.tensor_tensor(out=b32[:, 0], in0=st["h7", c][:], in1=st["h6b", c][:], op=ALU.subtract)
+            eng.tensor_tensor(out=p1[:], in0=e6h7[:, 0], in1=st["v8f", c][:, 0], op=ALU.subtract)
+            b6 = wk.tile([P, 6, f], BF16, name="b6", bufs=2)
+            (eng if c < NCH - 1 else nc.vector).tensor_tensor(out=b6[:, 1:5:3], in0=e6h7[:], in1=e7h6[:], op=ALU.subtract)
             st["p1", c] = p1
-            st["bz", c] = bz
-            st["b32", c] = b32
+            st["b6", c] = b6
 
-        def first_sum(c, eng):
-            t1 = wk.tile([P, F * SIZES[c]], F32, name="t1", bufs=1)
-            eng.tensor_tensor(out=t1[:], in0=st["h7", c][:], in1=st["v8f", c][:, 0], op=ALU.add)
-            st["t1", c] = t1
+        def first_sum(c, eng, lo, hi):
+            f = F * SIZES[c]
+            if lo == 0:
+                st["t1", c] = wk.tile([P, f], F32, name="t1", bufs=1)
+            a, b = int(lo * f), int(hi * f)
+            eng.tensor_tensor(out=st["t1", c][:, a:b], in0=st["e6h7", c][:, 1, a:b], in1=st["v8f", c][:, 1, a:b], op=ALU.add)
 
         def combos(c, part):
             if part == 0:
-                stt(st["bz", c][:, 2], st["t1", c][:], beta(4, 3) / G3, st["h6", c][:])
+                stt(st["b6", c][:, 2], st["t1", c][:], beta(4, 3) / G3, st["h6", c][:])
             else:
-                stt(st["bz", c][:, 3], st["p1", c][:], beta(2, 3) / G1, st["e7", c][:])
+                stt(st["b6", c][:, 3], st["p1", c][:], beta(2, 3) / G1, st["e7", c][:])
 
         def signs(c):
             f = F * SIZES[c]
             bo = wk.tile([P, 10, f], BF16, name="bo", bufs=1, align_bytes=64)
-            nc.vector.tensor_tensor(out=bo[:, 0:4], in0=st["bz", c][:],
+            nc.vector.tensor_tensor(out=bo[:, 0:4], in0=st["b6", c][:, 0:4],
                                     in1=st["s", c].unsqueeze(1).to_broadcast([P, 4, f]), op=ALU.mult)
             st["bo", c] = bo
 
@@ -270,7 +275,7 @@ def tile_bsplinekanlayer_t_kernel(tc, x, coeff, base_weight, knots, out):
             bas_a = wk.tile([P, 4, f], BF16, name="bas_a", bufs=1, align_bytes=64)
             nc.vector.tensor_tensor(
                 out=bas_a[:].rearrange("p (h m) f -> p h (m f)", h=2),
-                in0=st["b32", c][:].rearrange("p m f -> p (m f)").unsqueeze(1).to_broadcast([P, 2, 2 * f]),
+                in0=st["b6", c][:, 4:6].rearrange("p m f -> p (m f)").unsqueeze(1).to_broadcast([P, 2, 2 * f]),
                 in1=st["bo", c][:].rearrange("p m f -> p (m f)")[:, 2 * f:].rearrange("p (h m) -> p h m", m=2 * f)[:, 0:4:3], op=ALU.max)
             st["bas_a", c] = bas_a[:]
 
@@ -296,37 +301,44 @@ def tile_bsplinekanlayer_t_kernel(tc, x, coeff, base_weight, knots, out):
                     nc.scalar.activation(out=sil[:], in_=pb[:].rearrange("p a o -> p (a o)"), func=ACTF.Silu)
                     st["sil", START[c] + b, h] = sil
 
-        def spline(c, ab, rs, first):
-            slots = SLOT_A if ab == "a" else SLOT_B
-            for b in range(SIZES[c]):
-                for h in range(2):
-                    if first:
-                        pool, tag = (ps_pb, "pb") if c == NCH - 1 else (ps_sp, "sp")
-                        st["sp", START[c] + b, h] = pool.tile([P, 2, NO], F32, name=tag)
-                    sp = st["sp", START[c] + b, h]
-                    for r in rs:
-                        lo = slots[r] * (F * SIZES[c] // 4) + b * P
-                        nc.tensor.matmul_mx(
-                            out=sp[:].rearrange("p q o -> p (q o)"),
-                            lhsT=st["cod_" + ab, c][:, lo:lo + P].bitcast(FP8X4),
-                            lhsT_scale=st["scl_" + ab, c][:, lo:lo + P],
-                            rhs=c_z[:, r, 2 * h:2 * h + 2, :].rearrange("p q o -> p (q o)").bitcast(FP8X4),
-                            rhs_scale=c_scl[:, r, :],
-                            start=first and r == rs[0],
-                            stop=not first and r == rs[-1],
-                        )
+        def spline(c):
+            pool, tag = (ps_pb, "pb") if c == NCH - 1 else (ps_sp, "sp")
+            banks = [(b, h) for b in range(SIZES[c]) for h in range(2)]
+            steps = [(bank, half) for bank in banks for half in "ba"]
+            if c >= TAIL:
+                steps = [(bank, half) for half in "ba" for bank in banks]
+            for (b, h), half in steps:
+                if half == "b":
+                    st["sp", START[c] + b, h] = pool.tile([P, 2, NO], F32, name=tag)
+                slots = SLOT_A if half == "a" else SLOT_B
+                for r in slots:
+                    lo = slots[r] * (F * SIZES[c] // 4) + b * P
+                    nc.tensor.matmul_mx(
+                        out=st["sp", START[c] + b, h][:].rearrange("p q o -> p (q o)"),
+                        lhsT=st["cod_" + half, c][:, lo:lo + P].bitcast(FP8X4),
+                        lhsT_scale=st["scl_" + half, c][:, lo:lo + P],
+                        rhs=c_z[:, r, 2 * h:2 * h + 2, :].rearrange("p q o -> p (q o)").bitcast(FP8X4),
+                        rhs_scale=c_scl[:, r, :],
+                        start=half == "b" and slots[r] == 0,
+                        stop=half == "a" and slots[r] == 3,
+                    )
 
-        def adds(c):
-            for b in range(START[c], START[c] + SIZES[c]):
-                o_sb = wk.tile([P, 4, NO], F32, name="o_sb", bufs=OB)
-                for h in range(2):
-                    nc.vector.tensor_tensor(out=o_sb[:, 2 * h:2 * h + 2, :].rearrange("p a o -> p (a o)"),
-                                            in0=st["sp", b, h][:].rearrange("p a o -> p (a o)"),
-                                            in1=st["sil", b, h][:], op=ALU.add)
-                    if c == NCH - 1:
-                        nc.sync.dma_start(out=out_v[:, 4 * b + 2 * h:4 * b + 2 * h + 2, :], in_=o_sb[:, 2 * h:2 * h + 2, :])
-                if c < NCH - 1:
-                    nc.sync.dma_start(out=out_v[:, 4 * b:4 * b + 4, :], in_=o_sb[:])
+        def add(c, k):
+            b, h = START[c] + k // 2, k % 2
+            if h == 0:
+                st["o", b] = wk.tile([P, 4, NO], F32, name="o_sb", bufs=OB)
+            o_sb = st["o", b]
+            nc.vector.tensor_tensor(out=o_sb[:, 2 * h:2 * h + 2, :].rearrange("p a o -> p (a o)"),
+                                    in0=st["sp", b, h][:].rearrange("p a o -> p (a o)"),
+                                    in1=st["sil", b, h][:], op=ALU.add)
+            if c == NCH - 1:
+                nc.sync.dma_start(out=out_v[:, 4 * b + 2 * h:4 * b + 2 * h + 2, :], in_=o_sb[:, 2 * h:2 * h + 2, :])
+            elif h == 1:
+                nc.sync.dma_start(out=out_v[:, 4 * b:4 * b + 4, :], in_=o_sb[:])
+
+        def adds(c, lo=0, hi=4):
+            for k in range(lo, min(hi, 2 * SIZES[c])):
+                add(c, k)
 
         def ok(c):
             return 0 <= c < NCH
@@ -343,13 +355,13 @@ def tile_bsplinekanlayer_t_kernel(tc, x, coeff, base_weight, knots, out):
         relus_early(0)
         squares(1, "v67")
         squares(1, "v8f")
+        small(2)
         sums(0, nc.vector)
         relus_late(0)
-        first_sum(0, nc.vector)
+        first_sum(0, nc.vector, 0, 1)
         coeff_prep()
         cubes(1)
         coeff_quant()
-        small(2)
         turn_z(2)
         relus_early(1)
         squares(2, "v67")
@@ -368,18 +380,25 @@ def tile_bsplinekanlayer_t_kernel(tc, x, coeff, base_weight, knots, out):
             if ok(p + 1):
                 sums(p + 1, nc.gpsimd)
                 if T1_SC <= p < T1_END:
-                    first_sum(p + 1, nc.gpsimd)
+                    first_sum(p + 1, nc.gpsimd, 0, CUT)
             if ok(p + 2):
                 cubes(p + 2)
-            if p == TAIL:
+            if p < TAIL:
+                if ok(p - 1):
+                    adds(p - 1)
                 spread(p)
+                if not T1_SC <= p < T1_END:
+                    first_sum(p + 1, nc.vector, 0, 1)
+                else:
+                    first_sum(p + 1, nc.vector, CUT, 1)
+            else:
+                adds(p - 1, 0, 1)
+                spread(p)
+                if not last:
+                    adds(p - 1, 1, 2)
                 quant(p, "b")
-            if ok(p - 1) and not last:
-                adds(p - 1)
-            if ok(p + 1) and not T1_SC <= p < T1_END:
-                first_sum(p + 1, nc.vector)
-            if p != TAIL:
-                spread(p)
+                if not last:
+                    adds(p - 1, 2, 4)
             if ok(p + 1):
                 relus_late(p + 1)
                 turn_x(p + 1)
@@ -402,14 +421,13 @@ def tile_bsplinekanlayer_t_kernel(tc, x, coeff, base_weight, knots, out):
                 relus_early(p + 2)
             if 0 < p and not last:
                 base(p + 1, 1)
-            if last:
-                quant(p, "b")
             maxima(p)
             if p < TAIL:
                 quant(p, "b")
+            if p == TAIL:
+                first_sum(p + 1, nc.vector, 0, 1)
             quant(p, "a")
             if last:
-                adds(p - 1)
-            spline(p, "b", RS_B, True)
-            spline(p, "a", RS_A, False)
+                adds(p - 1, 1, 4)
+            spline(p)
         adds(NCH - 1)

@@ -43,7 +43,6 @@ OUT_END = 8
 T1_SC = 2
 T1_END = 6
 TAIL = 7
-CUT = 0.5
 E7_V = 2
 CODB = 2
 OB = 3
@@ -380,7 +379,7 @@ def tile_bsplinekanlayer_t_kernel(tc, x, coeff, base_weight, knots, out):
             if ok(p + 1):
                 sums(p + 1, nc.gpsimd)
                 if T1_SC <= p < T1_END:
-                    first_sum(p + 1, nc.gpsimd, 0, CUT)
+                    first_sum(p + 1, nc.gpsimd, 0, 1)
             if ok(p + 2):
                 cubes(p + 2)
             if p < TAIL:
@@ -389,8 +388,6 @@ def tile_bsplinekanlayer_t_kernel(tc, x, coeff, base_weight, knots, out):
                 spread(p)
                 if not T1_SC <= p < T1_END:
                     first_sum(p + 1, nc.vector, 0, 1)
-                else:
-                    first_sum(p + 1, nc.vector, CUT, 1)
             else:
                 adds(p - 1, 0, 1)
                 spread(p)

@@ -187,9 +187,9 @@ def tile_bsplinekanlayer_t_kernel(tc, x, coeff, base_weight, knots, out):
                 nc.scalar.activation(out=v[:, i], in_=st["za", c], func=ACTF.Square, bias=-sc * t, scale=sc)
             st[key, c] = v
 
-        def cubes(c):
+        def cubes(c, lo=0, hi=4):
             for v, t in ((st["v67", c][:, 0], T[6]), (st["v67", c][:, 1], T[7]),
-                         (st["v8f", c][:, 0], T[5]), (st["v8f", c][:, 1], T[8])):
+                         (st["v8f", c][:, 0], T[5]), (st["v8f", c][:, 1], T[8]))[lo:hi]:
                 stt(v, st["z", c], t, v, ALU.subtract, ALU.mult)
 
         def relu(c, key, i, scale):
@@ -371,17 +371,21 @@ def tile_bsplinekanlayer_t_kernel(tc, x, coeff, base_weight, knots, out):
                 load(p + 5)
             if ok(p + 3) and p + 3 < FIRST_SC:
                 size_and_sign(p + 3)
-            combos(p, 1)
-            combos(p, 0)
             if ok(p + 3):
                 smaller(p + 3)
+            combos(p, 1)
+            combos(p, 0)
+            if ok(p + 2):
+                cubes(p + 2, 0, 1)
             signs(p)
             if ok(p + 1):
                 sums(p + 1, nc.gpsimd)
                 if T1_SC <= p < T1_END:
                     first_sum(p + 1, nc.gpsimd, 0, 1)
             if ok(p + 2):
-                cubes(p + 2)
+                cubes(p + 2, 1)
+            if ok(p + 1):
+                relus_late(p + 1)
             if p < TAIL:
                 if ok(p - 1):
                     adds(p - 1)
@@ -397,7 +401,6 @@ def tile_bsplinekanlayer_t_kernel(tc, x, coeff, base_weight, knots, out):
                 if not last:
                     adds(p - 1, 2, 4)
             if ok(p + 1):
-                relus_late(p + 1)
                 turn_x(p + 1)
             if ok(p + 3):
                 turn_z(p + 3)

@@ -38,10 +38,11 @@ OG = NO // 4
 F = 512
 SIZES = (1,) + (2,) * 7 + (1,)
 NCH = len(SIZES)
-OUT_SC = 5
+OUT_SC = 6
 OUT_END = 8
-T1_SC = 2
-T1_END = 6
+PE_SC = 3
+PE_END = 8
+T1_END = 7
 TAIL = 7
 E7_V = 2
 CODB = 2
@@ -100,8 +101,8 @@ def tile_bsplinekanlayer_t_kernel(tc, x, coeff, base_weight, knots, out):
         one = const.tile([P, 1], F32)
         c_g = wk.tile([P, NB, OG, 4], BF16, name="bas_a", bufs=1, align_bytes=64)
         c_p = c_ld[:].rearrange("p t (o r) -> p r o t", r=NB)
-        c_q = const.tile([P, NB * OG], U32, align_bytes=64)
-        c_qs = const.tile([P, NB * OG], U8, align_bytes=64)
+        c_q = wk.tile([P, NB * OG], U32, name="cod_a", bufs=CODB, align_bytes=64)
+        c_qs = wk.tile([P, NB * OG], U8, name="scl_a", bufs=CODB, align_bytes=64)
         c_scl = const.tile([P, NB, 2 * NO], U8, align_bytes=64)
         for r in range(NB):
             nc.sync.dma_start(out=c_z[:, r].rearrange("p q o -> p (q o)").bitcast(I32), in_=zeros[:].bitcast(I32))
@@ -182,7 +183,7 @@ def tile_bsplinekanlayer_t_kernel(tc, x, coeff, base_weight, knots, out):
             st["xT", c] = xT
 
         def squares(c, key):
-            v = wk.tile([P, 2, F * SIZES[c]], F32, name=key, bufs=2)
+            v = wk.tile([P, 2, F * SIZES[c]], F32, name=key, bufs=2 if key == "v67" else 3)
             for i, (sc, t) in enumerate(SQUARES[key]):
                 nc.scalar.activation(out=v[:, i], in_=st["za", c], func=ACTF.Square, bias=-sc * t, scale=sc)
             st[key, c] = v
@@ -200,7 +201,7 @@ def tile_bsplinekanlayer_t_kernel(tc, x, coeff, base_weight, knots, out):
         def relu_pair(c, key, slot, i, scale):
             if slot == 0:
                 st[key, c] = wk.tile([P, 2, F * SIZES[c]], F32, name=key, bufs=1)
-            if c == 0 and slot == 0:
+            if c == 0:
                 nc.vector.tensor_scalar(out=st[key, c][:, slot], in0=st["v67", c][:, i], scalar1=scale, scalar2=0.0,
                                         op0=ALU.mult, op1=ALU.max)
             else:
@@ -235,16 +236,27 @@ def tile_bsplinekanlayer_t_kernel(tc, x, coeff, base_weight, knots, out):
             st["p1", c] = p1
             st["b6", c] = b6
 
-        def first_sum(c, eng, lo, hi):
-            f = F * SIZES[c]
-            if lo == 0:
-                st["t1", c] = wk.tile([P, f], F32, name="t1", bufs=1)
-            a, b = int(lo * f), int(hi * f)
-            eng.tensor_tensor(out=st["t1", c][:, a:b], in0=st["e6h7", c][:, 1, a:b], in1=st["v8f", c][:, 1, a:b], op=ALU.add)
+        def by_pe(c):
+            return F if PE_SC <= c < PE_END else 0
+
+        def pe_sum(c):
+            ps = ps_sp.tile([P, F], F32, name="sp")
+            for k, t in enumerate((st["v8f", c], st["e6h7", c])):
+                nc.tensor.matmul(out=ps[:], lhsT=ident_f[:], rhs=t[:, 1, :F], start=k == 0, stop=k == 1)
+            st["t1_pe", c] = ps
+
+        def first_sum(c, eng):
+            n = by_pe(c)
+            t1 = wk.tile([P, F * SIZES[c]], F32, name="t1", bufs=1)
+            eng.tensor_tensor(out=t1[:, n:], in0=st["e6h7", c][:, 1, n:], in1=st["v8f", c][:, 1, n:], op=ALU.add)
+            st["t1", c] = t1
 
         def combos(c, part):
             if part == 0:
-                stt(st["b6", c][:, 2], st["t1", c][:], beta(4, 3) / G3, st["h6", c][:])
+                n = by_pe(c)
+                stt(st["b6", c][:, 2, n:], st["t1", c][:, n:], beta(4, 3) / G3, st["h6", c][:, n:])
+                if n:
+                    stt(st["b6", c][:, 2, :n], st["t1_pe", c][:], beta(4, 3) / G3, st["h6", c][:, :n])
             else:
                 stt(st["b6", c][:, 3], st["p1", c][:], beta(2, 3) / G1, st["e7", c][:])
 
@@ -255,17 +267,18 @@ def tile_bsplinekanlayer_t_kernel(tc, x, coeff, base_weight, knots, out):
                                     in1=st["s", c].unsqueeze(1).to_broadcast([P, 4, f]), op=ALU.mult)
             st["bo", c] = bo
 
+        def outer(c):
+            bo = st["bo", c]
+            nc.scalar.activation(out=bo[:, 4:6], in_=bo[:, 0:2], func=ACTF.Relu)
+
         def spread(c):
             bo = st["bo", c]
             def mirror(lo, hi):
                 nc.vector.tensor_scalar(out=bo[:, 6 + lo:6 + hi], in0=bo[:, lo:hi], scalar1=-1.0, scalar2=0.0,
                                         op0=ALU.mult, op1=ALU.max)
 
-            if OUT_SC <= c < OUT_END:
-                nc.scalar.activation(out=bo[:, 4:6], in_=bo[:, 0:2], func=ACTF.Relu)
-                mirror(0, 4)
-            else:
-                mirror(0, 4)
+            mirror(0, 4)
+            if not OUT_SC <= c < OUT_END:
                 nc.vector.tensor_scalar(out=bo[:, 4:6], in0=bo[:, 0:2], scalar1=0.0, scalar2=None, op0=ALU.max)
             st["bas_b", c] = bo[:, 4:8]
 
@@ -342,6 +355,14 @@ def tile_bsplinekanlayer_t_kernel(tc, x, coeff, base_weight, knots, out):
         def ok(c):
             return 0 <= c < NCH
 
+        def before_signs(c):
+            if ok(c + 3):
+                if c + 3 < FIRST_SC:
+                    size_and_sign(c + 3)
+                smaller(c + 3)
+            combos(c, 1)
+            combos(c, 0)
+
         small(0)
         turn_z(0)
         squares(0, "v67")
@@ -357,7 +378,7 @@ def tile_bsplinekanlayer_t_kernel(tc, x, coeff, base_weight, knots, out):
         small(2)
         sums(0, nc.vector)
         relus_late(0)
-        first_sum(0, nc.vector, 0, 1)
+        first_sum(0, nc.vector)
         coeff_prep()
         cubes(1)
         coeff_quant()
@@ -365,23 +386,18 @@ def tile_bsplinekanlayer_t_kernel(tc, x, coeff, base_weight, knots, out):
         relus_early(1)
         squares(2, "v67")
         squares(2, "v8f")
+        before_signs(0)
         for p in range(NCH):
             last = p == NCH - 1
             if ok(p + 5):
                 load(p + 5)
-            if ok(p + 3) and p + 3 < FIRST_SC:
-                size_and_sign(p + 3)
-            if ok(p + 3):
-                smaller(p + 3)
-            combos(p, 1)
-            combos(p, 0)
             if ok(p + 2):
                 cubes(p + 2, 0, 1)
             signs(p)
             if ok(p + 1):
                 sums(p + 1, nc.gpsimd)
-                if T1_SC <= p < T1_END:
-                    first_sum(p + 1, nc.gpsimd, 0, 1)
+                if PE_SC <= p + 1 < T1_END:
+                    first_sum(p + 1, nc.gpsimd)
             if ok(p + 2):
                 cubes(p + 2, 1)
             if ok(p + 1):
@@ -390,10 +406,12 @@ def tile_bsplinekanlayer_t_kernel(tc, x, coeff, base_weight, knots, out):
                 if ok(p - 1):
                     adds(p - 1)
                 spread(p)
-                if not T1_SC <= p < T1_END:
-                    first_sum(p + 1, nc.vector, 0, 1)
+                if not PE_SC <= p + 1 < T1_END:
+                    first_sum(p + 1, nc.vector)
             else:
                 adds(p - 1, 0, 1)
+                if not last:
+                    outer(p)
                 spread(p)
                 if not last:
                     adds(p - 1, 1, 2)
@@ -404,6 +422,10 @@ def tile_bsplinekanlayer_t_kernel(tc, x, coeff, base_weight, knots, out):
                 turn_x(p + 1)
             if ok(p + 3):
                 turn_z(p + 3)
+            if OUT_SC <= p < TAIL:
+                outer(p)
+            if by_pe(p + 1):
+                pe_sum(p + 1)
             if ok(p + 1):
                 turn_s(p + 1)
             if ok(p + 3):
@@ -425,8 +447,10 @@ def tile_bsplinekanlayer_t_kernel(tc, x, coeff, base_weight, knots, out):
             if p < TAIL:
                 quant(p, "b")
             if p == TAIL:
-                first_sum(p + 1, nc.vector, 0, 1)
+                first_sum(p + 1, nc.vector)
             quant(p, "a")
+            if not last:
+                before_signs(p + 1)
             if last:
                 adds(p - 1, 1, 4)
             spline(p)

@@ -40,9 +40,10 @@ SIZES = (1,) + (2,) * 7 + (1,)
 NCH = len(SIZES)
 OUT_SC = 6
 OUT_END = 8
-PE_SC = 3
+PE_SC = 2
 PE_END = 8
-T1_END = 7
+G_SC = 3
+G_END = 7
 TAIL = 7
 E7_V = 2
 CODB = 2
@@ -130,8 +131,8 @@ def tile_bsplinekanlayer_t_kernel(tc, x, coeff, base_weight, knots, out):
 
         def small(c):
             f = F * SIZES[c]
-            if c < FIRST_SC:
-                size_and_sign(c)
+            sizes(c)
+            x_signs(c)
             smaller(c)
 
         def smaller(c):
@@ -140,20 +141,24 @@ def tile_bsplinekanlayer_t_kernel(tc, x, coeff, base_weight, knots, out):
             nc.vector.tensor_scalar(out=zt[:], in0=st["ab", c][:], scalar1=T[8], scalar2=None, op0=ALU.min)
             st["zt", c] = zt
 
-        def size_and_sign(c):
-            f = F * SIZES[c]
+        def sizes(c):
             xf = st["xc", c][:].rearrange("p n i -> p (n i)")
-            ab = wk.tile([P, f], BF16, name="ab", bufs=1)
-            sg = wk.tile([P, f], BF16, name="sg", bufs=4)
+            ab = wk.tile([P, F * SIZES[c]], BF16, name="ab", bufs=1)
             if c < FIRST_SC:
                 nc.vector.tensor_single_scalar(out=ab[:].bitcast(I32), in_=xf.bitcast(I32),
                                                scalar=0x7FFF7FFF, op=ALU.bitwise_and)
+            else:
+                nc.scalar.activation(out=ab[:], in_=xf, func=ACTF.Abs)
+            st["ab", c] = ab
+
+        def x_signs(c):
+            xf = st["xc", c][:].rearrange("p n i -> p (n i)")
+            sg = wk.tile([P, F * SIZES[c]], BF16, name="sg", bufs=4)
+            if c < FIRST_SC:
                 nc.vector.tensor_scalar(out=sg[:].bitcast(I32), in0=xf.bitcast(I32), scalar1=-0x7FFF8000,
                                         scalar2=0x3F803F80, op0=ALU.bitwise_and, op1=ALU.bitwise_or)
             else:
-                nc.scalar.activation(out=ab[:], in_=xf, func=ACTF.Abs)
                 nc.scalar.activation(out=sg[:], in_=xf, func=ACTF.Sign)
-            st["ab", c] = ab
             st["sg", c] = sg
 
         def turn(c, src, pool, tag):
@@ -358,7 +363,8 @@ def tile_bsplinekanlayer_t_kernel(tc, x, coeff, base_weight, knots, out):
         def before_signs(c):
             if ok(c + 3):
                 if c + 3 < FIRST_SC:
-                    size_and_sign(c + 3)
+                    sizes(c + 3)
+                    x_signs(c + 3)
                 smaller(c + 3)
             combos(c, 1)
             combos(c, 0)
@@ -396,7 +402,7 @@ def tile_bsplinekanlayer_t_kernel(tc, x, coeff, base_weight, knots, out):
             signs(p)
             if ok(p + 1):
                 sums(p + 1, nc.gpsimd)
-                if PE_SC <= p + 1 < T1_END:
+                if G_SC <= p + 1 < G_END:
                     first_sum(p + 1, nc.gpsimd)
             if ok(p + 2):
                 cubes(p + 2, 1)
@@ -406,7 +412,7 @@ def tile_bsplinekanlayer_t_kernel(tc, x, coeff, base_weight, knots, out):
                 if ok(p - 1):
                     adds(p - 1)
                 spread(p)
-                if not PE_SC <= p + 1 < T1_END:
+                if not G_SC <= p + 1 < G_END:
                     first_sum(p + 1, nc.vector)
             else:
                 adds(p - 1, 0, 1)
@@ -438,11 +444,13 @@ def tile_bsplinekanlayer_t_kernel(tc, x, coeff, base_weight, knots, out):
             if 0 < p and not last:
                 base(p + 1, 0)
             if ok(p + 4) and p + 4 >= FIRST_SC:
-                size_and_sign(p + 4)
+                sizes(p + 4)
             if ok(p + 2):
                 relus_early(p + 2)
             if 0 < p and not last:
                 base(p + 1, 1)
+            if ok(p + 3) and p + 3 >= FIRST_SC:
+                x_signs(p + 3)
             maxima(p)
             if p < TAIL:
                 quant(p, "b")

@@ -40,8 +40,10 @@ SIZES = (1,) + (2,) * 7 + (1,)
 NCH = len(SIZES)
 OUT_SC = 6
 OUT_END = 8
-PE_SC = 2
+PE_SC = 3
 PE_END = 8
+B4_SC = 4
+B4_END = 7
 G_SC = 3
 G_END = 7
 TAIL = 7
@@ -93,6 +95,8 @@ def tile_bsplinekanlayer_t_kernel(tc, x, coeff, base_weight, knots, out):
 
         ident_f = const.tile([P, P], F32)
         make_identity(nc, ident_f[:])
+        id_7 = const.tile([P, P], F32)
+        id_6 = const.tile([P, P], F32)
         ident_b = const.tile([P, P], BF16)
         make_identity(nc, ident_b[:])
         c_z = const.tile([P, NB, 4, NO], U32, align_bytes=64)
@@ -108,6 +112,9 @@ def tile_bsplinekanlayer_t_kernel(tc, x, coeff, base_weight, knots, out):
         for r in range(NB):
             nc.sync.dma_start(out=c_z[:, r].rearrange("p q o -> p (q o)").bitcast(I32), in_=zeros[:].bitcast(I32))
         nc.sync.dma_start(out=c_scl[:].rearrange("p r o -> p (r o)").bitcast(I32), in_=zeros[:].bitcast(I32))
+
+        for m, scale in ((id_7, beta(4, 3) / G3), (id_6, beta(4, 2) / -beta(3, 3))):
+            nc.gpsimd.tensor_scalar(out=m[:], in0=ident_f[:], scalar1=scale, scalar2=0.0, op0=ALU.mult, op1=ALU.add)
 
         def coeff_prep():
             nc.vector.memset(one[:], 1.0)
@@ -227,7 +234,10 @@ def tile_bsplinekanlayer_t_kernel(tc, x, coeff, base_weight, knots, out):
         def relus_late(c):
             b6 = st["b6", c]
             nc.scalar.activation(out=b6[:, 0], in_=st["v67", c][:, 1], func=ACTF.Relu, scale=G0)
-            relu(c, "h6", 0, -beta(4, 2))
+            n = F if whole_b4(c) else 0
+            h6 = wk.tile([P, F * SIZES[c]], F32, name="h6", bufs=1)
+            nc.scalar.activation(out=h6[:, n:], in_=st["v67", c][:, 0, n:], func=ACTF.Relu, scale=-beta(4, 2))
+            st["h6", c] = h6
             nc.scalar.activation(out=b6[:, 5], in_=st["v67", c][:, 0], func=ACTF.Relu, scale=-G2)
             (relu_v if c < E7_V else relu)(c, "e7", 1, beta(2, 2))
 
@@ -244,11 +254,21 @@ def tile_bsplinekanlayer_t_kernel(tc, x, coeff, base_weight, knots, out):
         def by_pe(c):
             return F if PE_SC <= c < PE_END else 0
 
+        def whole_b4(c):
+            return B4_SC <= c < B4_END
+
         def pe_sum(c):
+            v8f, e6h7, e7h6 = st["v8f", c], st["e6h7", c], st["e7h6", c]
+            terms = ((ident_f, v8f), (ident_f, e6h7))
+            if whole_b4(c):
+                terms = ((id_7, v8f), (id_7, e6h7), (id_6, e7h6))
             ps = ps_sp.tile([P, F], F32, name="sp")
-            for k, t in enumerate((st["v8f", c], st["e6h7", c])):
-                nc.tensor.matmul(out=ps[:], lhsT=ident_f[:], rhs=t[:, 1, :F], start=k == 0, stop=k == 1)
-            st["t1_pe", c] = ps
+            for k, (m, t) in enumerate(terms):
+                nc.tensor.matmul(out=ps[:], lhsT=m[:], rhs=t[:, 1, :F], start=k == 0, stop=k == len(terms) - 1)
+            st["pe", c] = ps
+
+        def pe_out(c):
+            nc.scalar.activation(out=st["b6", c][:, 2, :F], in_=st["pe", c][:], func=ACTF.Relu)
 
         def first_sum(c, eng):
             n = by_pe(c)
@@ -260,8 +280,8 @@ def tile_bsplinekanlayer_t_kernel(tc, x, coeff, base_weight, knots, out):
             if part == 0:
                 n = by_pe(c)
                 stt(st["b6", c][:, 2, n:], st["t1", c][:, n:], beta(4, 3) / G3, st["h6", c][:, n:])
-                if n:
-                    stt(st["b6", c][:, 2, :n], st["t1_pe", c][:], beta(4, 3) / G3, st["h6", c][:, :n])
+                if n and not whole_b4(c):
+                    stt(st["b6", c][:, 2, :n], st["pe", c][:], beta(4, 3) / G3, st["h6", c][:, :n])
             else:
                 stt(st["b6", c][:, 3], st["p1", c][:], beta(2, 3) / G1, st["e7", c][:])
 
@@ -445,6 +465,8 @@ def tile_bsplinekanlayer_t_kernel(tc, x, coeff, base_weight, knots, out):
                 base(p + 1, 0)
             if ok(p + 4) and p + 4 >= FIRST_SC:
                 sizes(p + 4)
+            if whole_b4(p + 1):
+                pe_out(p + 1)
             if ok(p + 2):
                 relus_early(p + 2)
             if 0 < p and not last:

@@ -46,6 +46,7 @@ B4_SC = 4
 B4_END = 7
 G_SC = 3
 G_END = 7
+P1_PE = 1
 TAIL = 7
 E7_V = 2
 CODB = 2
@@ -97,6 +98,7 @@ def tile_bsplinekanlayer_t_kernel(tc, x, coeff, base_weight, knots, out):
         make_identity(nc, ident_f[:])
         id_7 = const.tile([P, P], F32)
         id_6 = const.tile([P, P], F32)
+        id_n = const.tile([P, P], F32)
         ident_b = const.tile([P, P], BF16)
         make_identity(nc, ident_b[:])
         c_z = const.tile([P, NB, 4, NO], U32, align_bytes=64)
@@ -113,7 +115,7 @@ def tile_bsplinekanlayer_t_kernel(tc, x, coeff, base_weight, knots, out):
             nc.sync.dma_start(out=c_z[:, r].rearrange("p q o -> p (q o)").bitcast(I32), in_=zeros[:].bitcast(I32))
         nc.sync.dma_start(out=c_scl[:].rearrange("p r o -> p (r o)").bitcast(I32), in_=zeros[:].bitcast(I32))
 
-        for m, scale in ((id_7, beta(4, 3) / G3), (id_6, beta(4, 2) / -beta(3, 3))):
+        for m, scale in ((id_n, -1.0), (id_7, beta(4, 3) / G3), (id_6, beta(4, 2) / -beta(3, 3))):
             nc.gpsimd.tensor_scalar(out=m[:], in0=ident_f[:], scalar1=scale, scalar2=0.0, op0=ALU.mult, op1=ALU.add)
 
         def coeff_prep():
@@ -244,8 +246,9 @@ def tile_bsplinekanlayer_t_kernel(tc, x, coeff, base_weight, knots, out):
         def sums(c, eng):
             f = F * SIZES[c]
             e6h7, e7h6 = st["e6h7", c], st["e7h6", c]
+            n = F if c == P1_PE else 0
             p1 = wk.tile([P, f], F32, name="p1", bufs=1)
-            eng.tensor_tensor(out=p1[:], in0=e6h7[:, 0], in1=st["v8f", c][:, 0], op=ALU.subtract)
+            eng.tensor_tensor(out=p1[:, n:], in0=e6h7[:, 0, n:], in1=st["v8f", c][:, 0, n:], op=ALU.subtract)
             b6 = wk.tile([P, 6, f], BF16, name="b6", bufs=2)
             (eng if c < NCH - 1 else nc.vector).tensor_tensor(out=b6[:, 1:5:3], in0=e6h7[:], in1=e7h6[:], op=ALU.subtract)
             st["p1", c] = p1
@@ -267,6 +270,12 @@ def tile_bsplinekanlayer_t_kernel(tc, x, coeff, base_weight, knots, out):
                 nc.tensor.matmul(out=ps[:], lhsT=m[:], rhs=t[:, 1, :F], start=k == 0, stop=k == len(terms) - 1)
             st["pe", c] = ps
 
+        def pe_p1(c):
+            ps = ps_sp.tile([P, F], F32, name="sp")
+            nc.tensor.matmul(out=ps[:], lhsT=ident_f[:], rhs=st["e6h7", c][:, 0, :F], start=True, stop=False)
+            nc.tensor.matmul(out=ps[:], lhsT=id_n[:], rhs=st["v8f", c][:, 0, :F], start=False, stop=True)
+            st["p1_pe"] = ps
+
         def pe_out(c):
             nc.scalar.activation(out=st["b6", c][:, 2, :F], in_=st["pe", c][:], func=ACTF.Relu)
 
@@ -283,7 +292,10 @@ def tile_bsplinekanlayer_t_kernel(tc, x, coeff, base_weight, knots, out):
                 if n and not whole_b4(c):
                     stt(st["b6", c][:, 2, :n], st["pe", c][:], beta(4, 3) / G3, st["h6", c][:, :n])
             else:
-                stt(st["b6", c][:, 3], st["p1", c][:], beta(2, 3) / G1, st["e7", c][:])
+                n = F if c == P1_PE else 0
+                stt(st["b6", c][:, 3, n:], st["p1", c][:, n:], beta(2, 3) / G1, st["e7", c][:, n:])
+                if n:
+                    stt(st["b6", c][:, 3, :n], st["p1_pe"][:], beta(2, 3) / G1, st["e7", c][:, :n])
 
         def signs(c):
             f = F * SIZES[c]
@@ -413,6 +425,7 @@ def tile_bsplinekanlayer_t_kernel(tc, x, coeff, base_weight, knots, out):
         squares(2, "v67")
         squares(2, "v8f")
         before_signs(0)
+        pe_p1(P1_PE)
         for p in range(NCH):
             last = p == NCH - 1
             if ok(p + 5):

from contextlib import ExitStack

import concourse.mybir as mybir
from concourse.masks import make_identity

F32 = mybir.dt.float32
BF16 = mybir.dt.bfloat16
U32 = mybir.dt.uint32
I32 = mybir.dt.int32
U8 = mybir.dt.uint8
FP8X4 = mybir.dt.float8_e4m3fn_x4
ALU = mybir.AluOpType
ACTF = mybir.ActivationFunctionType

P = 128
M, NI, NO, NB = 8192, 128, 256, 8
FLOPS = 2 * M * NB * NI * NO + 2 * M * NI * NO

T = [-141 / 64, -115 / 64, -179 / 128, -1.0, -77 / 128, -205 / 1024,
     205 / 1024, 77 / 128, 1.0, 179 / 128, 115 / 64, 141 / 64]


def beta(r, j):
    prod = 1.0
    for m in range(5):
        if m != j:
            prod = prod * (T[r + j] - T[r + m])
    return (T[r + 4] - T[r]) / prod


assert all(T[k] == -T[11 - k] for k in range(12))
assert all(abs(beta(r, j) - beta(7 - r, 4 - j)) < 1e-12 for r in range(8) for j in range(5))
G0, G1, G2, G3 = beta(0, 4), beta(1, 4), beta(2, 4), beta(3, 4)
S8 = (beta(4, 4) * G3 / -beta(4, 3)) ** 0.5
SF = (G2 * G1 / -beta(2, 3)) ** 0.5

OG = NO // 4
F = 512
SIZES = (1,) + (2,) * 7 + (1,)
NCH = len(SIZES)
OUT_SC = 6
OUT_END = 8
PE_SC = 3
PE_END = 8
B4_SC = 4
B4_END = 7
G_SC = 3
G_END = 7
P1_PE = 1
TAIL = 7
E7_V = 2
CODB = 2
OB = 3
FIRST_SC = 7
SQUARES = {"v67": ((1.0, T[6]), (1.0, T[7])), "v8f": ((SF, T[5]), (S8, T[8]))}
START = [sum(SIZES[:c]) for c in range(NCH)]
SLOT_A = {4: 0, 5: 1, 3: 2, 2: 3}
SLOT_B = {7: 0, 6: 1, 0: 2, 1: 3}


def tile_bsplinekanlayer_t_kernel(tc, x, coeff, base_weight, knots, out):
    nc = tc.nc
    with ExitStack() as ctx:
        const = ctx.enter_context(tc.tile_pool(name="const", bufs=1))
        wk = ctx.enter_context(tc.tile_pool(name="wk", bufs=1))
        ps_z = ctx.enter_context(tc.psum_pool(name="ps_z", bufs=1))
        ps_tr = ctx.enter_context(tc.psum_pool(name="ps_tr", bufs=1))
        ps_sp = ctx.enter_context(tc.psum_pool(name="ps_sp", bufs=4))
        ps_pb = ctx.enter_context(tc.psum_pool(name="ps_pb", bufs=2))
        ctx.enter_context(tc.manual_schedule())

        warm = const.tile([P, 2], F32)
        nc.vector.memset(warm[:, 0:1], 0.0)
        nc.scalar.activation(out=warm[:, 1:2], in_=warm[:, 0:1], func=ACTF.Silu)

        x_v = x.rearrange("(p n) i -> p n i", n=64)
        out_v = out.rearrange("(p n) o -> p n o", n=64)
        st = {}

        def load(c):
            xc = wk.tile([P, 4 * SIZES[c], NI], BF16, name="xc", bufs=5)
            nc.sync.dma_start(out=xc[:], in_=x_v[:, 4 * START[c]:4 * (START[c] + SIZES[c]), :])
            st["xc", c] = xc

        load(0)
        load(1)
        load(2)
        load(3)
        load(4)
        c_ld = wk.tile([P, 4, OG * NB], BF16, name="bo", bufs=1, align_bytes=64)
        c_v = coeff.rearrange("(j t) o r -> j t (o r)", t=4)
        for g in range(4):
            nc.scalar.dma_start(out=c_ld[32 * g:32 * g + 32, :, :], in_=c_v[:, :, OG * NB * g:OG * NB * (g + 1)])
        bw_sb = const.tile([P, NO], BF16)
        nc.scalar.dma_start(out=bw_sb[:], in_=base_weight)

        ident_f = const.tile([P, P], F32)
        make_identity(nc, ident_f[:])
        id_7 = const.tile([P, P], F32)
        id_6 = const.tile([P, P], F32)
        id_n = const.tile([P, P], F32)
        ident_b = const.tile([P, P], BF16)
        make_identity(nc, ident_b[:])
        c_z = const.tile([P, NB, 4, NO], U32, align_bytes=64)
        zeros = wk.tile([P, 4 * NO], U32, name="o_sb", bufs=OB)
        nc.gpsimd.memset(zeros[:].bitcast(I32), 0)

        one = const.tile([P, 1], F32)
        c_g = wk.tile([P, NB, OG, 4], BF16, name="bas_a", bufs=1, align_bytes=64)
        c_p = c_ld[:].rearrange("p t (o r) -> p r o t", r=NB)
        c_q = wk.tile([P, NB * OG], U32, name="cod_a", bufs=CODB, align_bytes=64)
        c_qs = wk.tile([P, NB * OG], U8, name="scl_a", bufs=CODB, align_bytes=64)
        c_scl = const.tile([P, NB, 2 * NO], U8, align_bytes=64)
        for r in range(NB):
            nc.sync.dma_start(out=c_z[:, r].rearrange("p q o -> p (q o)").bitcast(I32), in_=zeros[:].bitcast(I32))
        nc.sync.dma_start(out=c_scl[:].rearrange("p r o -> p (r o)").bitcast(I32), in_=zeros[:].bitcast(I32))

        for m, scale in ((id_n, -1.0), (id_7, beta(4, 3) / G3), (id_6, beta(4, 2) / -beta(3, 3))):
            nc.gpsimd.tensor_scalar(out=m[:], in0=ident_f[:], scalar1=scale, scalar2=0.0, op0=ALU.mult, op1=ALU.add)

        def coeff_prep():
            nc.vector.memset(one[:], 1.0)
            nc.gpsimd.tensor_scalar(out=c_g[:], in0=c_p, scalar1=one[:], scalar2=0.0, op0=ALU.mult, op1=ALU.add)

        def coeff_quant():
            nc.vector.quantize_mx(out=c_q[:].bitcast(FP8X4), scales=c_qs[:],
                                  in_=c_g[:].rearrange("p r o t -> p (r o t)"))
            codes = c_q[:].bitcast(I32).rearrange("p (r o) -> p r o", r=NB)
            scales = c_qs[:].bitcast(I32).rearrange("p (r o) -> p r o", r=NB)
            c_scl_w = c_scl[:].rearrange("p r o -> p (r o)").bitcast(I32).rearrange("p (r q o) -> p r q o", r=NB, q=2)
            for q in range(4):
                for g in range(4):
                    nc.sync.dma_start(out=c_z[32 * q:32 * q + 32, :, q, OG * g:OG * g + OG].bitcast(I32),
                                      in_=codes[32 * g:32 * g + 32])
                    nc.sync.dma_start(out=c_scl_w[32 * q:32 * q + 4, :, q % 2, 16 * g:16 * g + 16],
                                      in_=scales[32 * g:32 * g + 4])

        def stt(o, a, s, b, op0=ALU.mult, op1=ALU.add):
            nc.vector.scalar_tensor_tensor(out=o, in0=a, scalar=s, in1=b, op0=op0, op1=op1)

        def small(c):
            f = F * SIZES[c]
            sizes(c)
            x_signs(c)
            smaller(c)

        def smaller(c):
            f = F * SIZES[c]
            zt = wk.tile([P, f], BF16, name="zt", bufs=2)
            nc.vector.tensor_scalar(out=zt[:], in0=st["ab", c][:], scalar1=T[8], scalar2=None, op0=ALU.min)
            st["zt", c] = zt

        def sizes(c):
            xf = st["xc", c][:].rearrange("p n i -> p (n i)")
            ab = wk.tile([P, F * SIZES[c]], BF16, name="ab", bufs=1)
            if c < FIRST_SC:
                nc.vector.tensor_single_scalar(out=ab[:].bitcast(I32), in_=xf.bitcast(I32),
                                               scalar=0x7FFF7FFF, op=ALU.bitwise_and)
            else:
                nc.scalar.activation(out=ab[:], in_=xf, func=ACTF.Abs)
            st["ab", c] = ab

        def x_signs(c):
            xf = st["xc", c][:].rearrange("p n i -> p (n i)")
            sg = wk.tile([P, F * SIZES[c]], BF16, name="sg", bufs=4)
            if c < FIRST_SC:
                nc.vector.tensor_scalar(out=sg[:].bitcast(I32), in0=xf.bitcast(I32), scalar1=-0x7FFF8000,
                                        scalar2=0x3F803F80, op0=ALU.bitwise_and, op1=ALU.bitwise_or)
            else:
                nc.scalar.activation(out=sg[:], in_=xf, func=ACTF.Sign)
            st["sg", c] = sg

        def turn(c, src, pool, tag):
            w = src[:].bitcast(F32)
            tq = pool.tile([P, SIZES[c], P, 2], F32, name=tag)
            for b in range(SIZES[c]):
                for u in range(2):
                    nc.tensor.transpose(tq[:, b, :, u], w[:, b * 256 + u:(b + 1) * 256:2], ident_f[:])
            return tq[:].rearrange("p n b u -> p (n b u)").bitcast(BF16)

        def turn_z(c):
            st["za", c] = turn(c, st["zt", c], ps_sp, "sp") if c < 3 else None
            st["z", c] = turn(c, st["zt", c], ps_z, "z")
            if c >= 3:
                st["za", c] = st["z", c]

        def turn_s(c):
            st["s", c] = turn(c, st["sg", c], ps_tr, "tr")

        def turn_x(c):
            nb = SIZES[c]
            xt_ps = ps_tr.tile([P, 4 * nb, P], BF16, name="tr")
            for m in range(4 * nb):
                nc.tensor.transpose(xt_ps[:, m, :], st["xc", c][:, m, :], ident_b[:])
            xT = wk.tile([P, F * nb], BF16, name="xT", bufs=2)
            nc.scalar.copy(out=xT[:], in_=xt_ps[:].rearrange("p m b -> p (m b)"))
            st["xT", c] = xT

        def squares(c, key):
            v = wk.tile([P, 2, F * SIZES[c]], F32, name=key, bufs=2 if key == "v67" else 3)
            for i, (sc, t) in enumerate(SQUARES[key]):
                nc.scalar.activation(out=v[:, i], in_=st["za", c], func=ACTF.Square, bias=-sc * t, scale=sc)
            st[key, c] = v

        def cubes(c, lo=0, hi=4):
            for v, t in ((st["v67", c][:, 0], T[6]), (st["v67", c][:, 1], T[7]),
                         (st["v8f", c][:, 0], T[5]), (st["v8f", c][:, 1], T[8]))[lo:hi]:
                stt(v, st["z", c], t, v, ALU.subtract, ALU.mult)

        def relu(c, key, i, scale):
            t = wk.tile([P, F * SIZES[c]], F32, name=key, bufs=1)
            nc.scalar.activation(out=t[:], in_=st["v67", c][:, i], func=ACTF.Relu, scale=scale)
            st[key, c] = t

        def relu_pair(c, key, slot, i, scale):
            if slot == 0:
                st[key, c] = wk.tile([P, 2, F * SIZES[c]], F32, name=key, bufs=1)
            if c == 0:
                nc.vector.tensor_scalar(out=st[key, c][:, slot], in0=st["v67", c][:, i], scalar1=scale, scalar2=0.0,
                                        op0=ALU.mult, op1=ALU.max)
            else:
                nc.scalar.activation(out=st[key, c][:, slot], in_=st["v67", c][:, i], func=ACTF.Relu, scale=scale)

        def relu_v(c, key, i, scale):
            t = wk.tile([P, F * SIZES[c]], F32, name=key, bufs=1)
            nc.vector.tensor_scalar(out=t[:], in0=st["v67", c][:, i], scalar1=scale, scalar2=0.0,
                                    op0=ALU.mult, op1=ALU.max)
            st[key, c] = t

        def relus_early(c):
            relu_pair(c, "e6h7", 0, 0, G1)
            relu_pair(c, "e7h6", 0, 1, -beta(1, 3))
            relu_pair(c, "e7h6", 1, 0, beta(3, 3))
            relu_pair(c, "e6h7", 1, 1, -G3)

        def relus_late(c):
            b6 = st["b6", c]
            nc.scalar.activation(out=b6[:, 0], in_=st["v67", c][:, 1], func=ACTF.Relu, scale=G0)
            n = F if whole_b4(c) else 0
            h6 = wk.tile([P, F * SIZES[c]], F32, name="h6", bufs=1)
            nc.scalar.activation(out=h6[:, n:], in_=st["v67", c][:, 0, n:], func=ACTF.Relu, scale=-beta(4, 2))
            st["h6", c] = h6
            nc.scalar.activation(out=b6[:, 5], in_=st["v67", c][:, 0], func=ACTF.Relu, scale=-G2)
            (relu_v if c < E7_V else relu)(c, "e7", 1, beta(2, 2))

        def sums(c, eng):
            f = F * SIZES[c]
            e6h7, e7h6 = st["e6h7", c], st["e7h6", c]
            n = F if c == P1_PE else 0
            p1 = wk.tile([P, f], F32, name="p1", bufs=1)
            eng.tensor_tensor(out=p1[:, n:], in0=e6h7[:, 0, n:], in1=st["v8f", c][:, 0, n:], op=ALU.subtract)
            b6 = wk.tile([P, 6, f], BF16, name="b6", bufs=2)
            (eng if c < NCH - 1 else nc.vector).tensor_tensor(out=b6[:, 1:5:3], in0=e6h7[:], in1=e7h6[:], op=ALU.subtract)
            st["p1", c] = p1
            st["b6", c] = b6

        def by_pe(c):
            return F if PE_SC <= c < PE_END else 0

        def whole_b4(c):
            return B4_SC <= c < B4_END

        def pe_sum(c):
            v8f, e6h7, e7h6 = st["v8f", c], st["e6h7", c], st["e7h6", c]
            terms = ((ident_f, v8f), (ident_f, e6h7))
            if whole_b4(c):
                terms = ((id_7, v8f), (id_7, e6h7), (id_6, e7h6))
            ps = ps_sp.tile([P, F], F32, name="sp")
            for k, (m, t) in enumerate(terms):
                nc.tensor.matmul(out=ps[:], lhsT=m[:], rhs=t[:, 1, :F], start=k == 0, stop=k == len(terms) - 1)
            st["pe", c] = ps

        def pe_p1(c):
            ps = ps_sp.tile([P, F], F32, name="sp")
            nc.tensor.matmul(out=ps[:], lhsT=ident_f[:], rhs=st["e6h7", c][:, 0, :F], start=True, stop=False)
            nc.tensor.matmul(out=ps[:], lhsT=id_n[:], rhs=st["v8f", c][:, 0, :F], start=False, stop=True)
            st["p1_pe"] = ps

        def pe_out(c):
            nc.scalar.activation(out=st["b6", c][:, 2, :F], in_=st["pe", c][:], func=ACTF.Relu)

        def first_sum(c, eng):
            n = by_pe(c)
            t1 = wk.tile([P, F * SIZES[c]], F32, name="t1", bufs=1)
            eng.tensor_tensor(out=t1[:, n:], in0=st["e6h7", c][:, 1, n:], in1=st["v8f", c][:, 1, n:], op=ALU.add)
            st["t1", c] = t1

        def combos(c, part):
            if part == 0:
                n = by_pe(c)
                stt(st["b6", c][:, 2, n:], st["t1", c][:, n:], beta(4, 3) / G3, st["h6", c][:, n:])
                if n and not whole_b4(c):
                    stt(st["b6", c][:, 2, :n], st["pe", c][:], beta(4, 3) / G3, st["h6", c][:, :n])
            else:
                n = F if c == P1_PE else 0
                stt(st["b6", c][:, 3, n:], st["p1", c][:, n:], beta(2, 3) / G1, st["e7", c][:, n:])
                if n:
                    stt(st["b6", c][:, 3, :n], st["p1_pe"][:], beta(2, 3) / G1, st["e7", c][:, :n])

        def signs(c):
            f = F * SIZES[c]
            bo = wk.tile([P, 10, f], BF16, name="bo", bufs=1, align_bytes=64)
            nc.vector.tensor_tensor(out=bo[:, 0:4], in0=st["b6", c][:, 0:4],
                                    in1=st["s", c].unsqueeze(1).to_broadcast([P, 4, f]), op=ALU.mult)
            st["bo", c] = bo

        def outer(c):
            bo = st["bo", c]
            nc.scalar.activation(out=bo[:, 4:6], in_=bo[:, 0:2], func=ACTF.Relu)

        def spread(c):
            bo = st["bo", c]
            def mirror(lo, hi):
                nc.vector.tensor_scalar(out=bo[:, 6 + lo:6 + hi], in0=bo[:, lo:hi], scalar1=-1.0, scalar2=0.0,
                                        op0=ALU.mult, op1=ALU.max)

            mirror(0, 4)
            if not OUT_SC <= c < OUT_END:
                nc.vector.tensor_scalar(out=bo[:, 4:6], in0=bo[:, 0:2], scalar1=0.0, scalar2=None, op0=ALU.max)
            st["bas_b", c] = bo[:, 4:8]

        def maxima(c):
            f = F * SIZES[c]
            bas_a = wk.tile([P, 4, f], BF16, name="bas_a", bufs=1, align_bytes=64)
            nc.vector.tensor_tensor(
                out=bas_a[:].rearrange("p (h m) f -> p h (m f)", h=2),
                in0=st["b6", c][:, 4:6].rearrange("p m f -> p (m f)").unsqueeze(1).to_broadcast([P, 2, 2 * f]),
                in1=st["bo", c][:].rearrange("p m f -> p (m f)")[:, 2 * f:].rearrange("p (h m) -> p h m", m=2 * f)[:, 0:4:3], op=ALU.max)
            st["bas_a", c] = bas_a[:]

        def quant(c, ab):
            f = F * SIZES[c]
            cod = wk.tile([P, f], U32, name="cod_" + ab, bufs=CODB, align_bytes=64)
            scl = wk.tile([P, f], U8, name="scl_" + ab, bufs=CODB, align_bytes=64)
            nc.vector.quantize_mx(out=cod[:].bitcast(FP8X4), scales=scl[:],
                                  in_=st["bas_" + ab, c].rearrange("p m f -> p (m f)"))
            st["cod_" + ab, c] = cod
            st["scl_" + ab, c] = scl

        def base(c, b):
            xT = st["xT", c]
            if b < SIZES[c]:
                for h in range(2):
                    pb = ps_pb.tile([P, 2, NO], F32, name="pb")
                    for qq in range(2):
                        q = 4 * b + 2 * h + qq
                        nc.tensor.matmul(out=pb[:, qq, :], lhsT=xT[:, q * P:(q + 1) * P],
                                         rhs=bw_sb[:], start=True, stop=True)
                    sil = wk.tile([P, 2 * NO], F32, name="sil", bufs=8)
                    nc.scalar.activation(out=sil[:], in_=pb[:].rearrange("p a o -> p (a o)"), func=ACTF.Silu)
                    st["sil", START[c] + b, h] = sil

        def spline(c):
            pool, tag = (ps_pb, "pb") if c == NCH - 1 else (ps_sp, "sp")
            banks = [(b, h) for b in range(SIZES[c]) for h in range(2)]
            steps = [(bank, half) for bank in banks for half in "ba"]
            if c >= TAIL:
                steps = [(bank, half) for half in "ba" for bank in banks]
            for (b, h), half in steps:
                if half == "b":
                    st["sp", START[c] + b, h] = pool.tile([P, 2, NO], F32, name=tag)
                slots = SLOT_A if half == "a" else SLOT_B
                for r in slots:
                    lo = slots[r] * (F * SIZES[c] // 4) + b * P
                    nc.tensor.matmul_mx(
                        out=st["sp", START[c] + b, h][:].rearrange("p q o -> p (q o)"),
                        lhsT=st["cod_" + half, c][:, lo:lo + P].bitcast(FP8X4),
                        lhsT_scale=st["scl_" + half, c][:, lo:lo + P],
                        rhs=c_z[:, r, 2 * h:2 * h + 2, :].rearrange("p q o -> p (q o)").bitcast(FP8X4),
                        rhs_scale=c_scl[:, r, :],
                        start=half == "b" and slots[r] == 0,
                        stop=half == "a" and slots[r] == 3,
                    )

        def add(c, k):
            b, h = START[c] + k // 2, k % 2
            if h == 0:
                st["o", b] = wk.tile([P, 4, NO], F32, name="o_sb", bufs=OB)
            o_sb = st["o", b]
            nc.vector.tensor_tensor(out=o_sb[:, 2 * h:2 * h + 2, :].rearrange("p a o -> p (a o)"),
                                    in0=st["sp", b, h][:].rearrange("p a o -> p (a o)"),
                                    in1=st["sil", b, h][:], op=ALU.add)
            if c == NCH - 1:
                nc.sync.dma_start(out=out_v[:, 4 * b + 2 * h:4 * b + 2 * h + 2, :], in_=o_sb[:, 2 * h:2 * h + 2, :])
            elif h == 1:
                nc.sync.dma_start(out=out_v[:, 4 * b:4 * b + 4, :], in_=o_sb[:])

        def adds(c, lo=0, hi=4):
            for k in range(lo, min(hi, 2 * SIZES[c])):
                add(c, k)

        def ok(c):
            return 0 <= c < NCH

        def before_signs(c):
            if ok(c + 3):
                if c + 3 < FIRST_SC:
                    sizes(c + 3)
                    x_signs(c + 3)
                smaller(c + 3)
            combos(c, 1)
            combos(c, 0)

        small(0)
        turn_z(0)
        squares(0, "v67")
        squares(0, "v8f")
        turn_x(0)
        small(1)
        cubes(0)
        turn_z(1)
        turn_s(0)
        relus_early(0)
        squares(1, "v67")
        squares(1, "v8f")
        small(2)
        sums(0, nc.vector)
        relus_late(0)
        first_sum(0, nc.vector)
        coeff_prep()
        cubes(1)
        coeff_quant()
        turn_z(2)
        relus_early(1)
        squares(2, "v67")
        squares(2, "v8f")
        before_signs(0)
        pe_p1(P1_PE)
        for p in range(NCH):
            last = p == NCH - 1
            if ok(p + 5):
                load(p + 5)
            if ok(p + 2):
                cubes(p + 2, 0, 1)
            signs(p)
            if ok(p + 1):
                sums(p + 1, nc.gpsimd)
                if G_SC <= p + 1 < G_END:
                    first_sum(p + 1, nc.gpsimd)
            if ok(p + 2):
                cubes(p + 2, 1)
            if ok(p + 1):
                relus_late(p + 1)
            if p < TAIL:
                if ok(p - 1):
                    adds(p - 1)
                spread(p)
                if not G_SC <= p + 1 < G_END:
                    first_sum(p + 1, nc.vector)
            else:
                adds(p - 1, 0, 1)
                if not last:
                    outer(p)
                spread(p)
                if not last:
                    adds(p - 1, 1, 2)
                quant(p, "b")
                if not last:
                    adds(p - 1, 2, 4)
            if ok(p + 1):
                turn_x(p + 1)
            if ok(p + 3):
                turn_z(p + 3)
            if OUT_SC <= p < TAIL:
                outer(p)
            if by_pe(p + 1):
                pe_sum(p + 1)
            if ok(p + 1):
                turn_s(p + 1)
            if ok(p + 3):
                squares(p + 3, "v67")
            if ok(p + 3):
                squares(p + 3, "v8f")
            if p < 2:
                base(p, 0)
                base(p, 1)
            if 0 < p and not last:
                base(p + 1, 0)
            if ok(p + 4) and p + 4 >= FIRST_SC:
                sizes(p + 4)
            if whole_b4(p + 1):
                pe_out(p + 1)
            if ok(p + 2):
                relus_early(p + 2)
            if 0 < p and not last:
                base(p + 1, 1)
            if ok(p + 3) and p + 3 >= FIRST_SC:
                x_signs(p + 3)
            maxima(p)
            if p < TAIL:
                quant(p, "b")
            if p == TAIL:
                first_sum(p + 1, nc.vector)
            quant(p, "a")
            if not last:
                before_signs(p + 1)
            if last:
                adds(p - 1, 1, 4)
            spline(p)
        adds(NCH - 1)
